import numpy as np
import ml_dtypes


def mxq(x, axis, fmt="e4m3"):
    dtype, down = {"e4m3": (ml_dtypes.float8_e4m3fn, 7), "e5m2": (ml_dtypes.float8_e5m2, 14)}[fmt]
    v = np.moveaxis(np.asarray(x, np.float32).astype(ml_dtypes.bfloat16).astype(np.float64), axis, -1)
    blocks = v.reshape(v.shape[:-1] + (-1, 32))
    amax = np.abs(blocks).max(-1, keepdims=True)
    byte = np.maximum(np.where(amax > 0, np.frexp(amax)[1] - 1 + 127, 0) - down, 1)
    scale = np.exp2(byte - 127.0)
    codes = (blocks / scale).astype(np.float32).astype(dtype).astype(np.float64)
    return np.moveaxis((codes * scale).reshape(v.shape), -1, axis)


WIDE = False


def mx_kscale(k):
    if not WIDE:
        return np.ones(k)
    levels = np.array([10, -10, 5, -5, 0])
    a = np.random.permutation(np.resize(levels, k // 512 * 4)).reshape(k // 512, 4)
    idx = np.arange(k)
    return np.exp2(a[idx // 512, idx % 128 // 32])


BF16 = ml_dtypes.bfloat16


def bf(x):
    return np.asarray(x, np.float32).astype(BF16)


def f64(x):
    return np.asarray(x).astype(np.float64)


B, N, D, H = 64, 16, 128, 1024


def setup_inputs():
    t = mx_kscale(H)
    return {
        "xi_p": bf(np.random.standard_normal((B, N, H)) * 0.7 * t),
        "xj_p": bf(np.random.standard_normal((B, N, H)) * 0.7 * t),
        "node_mask": bf(np.random.uniform(size=(B, N)) < 0.9),
        "mb1": bf(np.random.standard_normal(H) * 0.2 * t),
        "mw2": bf(np.random.standard_normal((H, D)) * 0.5 / np.sqrt(H) / t[:, None]),
        "mb2": bf(np.random.standard_normal(D) * 0.1),
    }


def reference(xi_p, xj_p, node_mask, mb1, mw2, mb2):
    mask = f64(node_mask)[..., None]
    h = np.maximum(f64(xi_p)[:, :, None, :] + f64(xj_p)[:, None, :, :] + f64(mb1), 0.0)
    msgs = np.maximum((mxq(h, 3, "e4m3") @ mxq(f64(mw2), 0, "e4m3")) + f64(mb2), 0.0)
    msgs = msgs * mask[:, None]
    return msgs.sum(axis=2)

@@ -1,0 +1,200 @@
+from contextlib import ExitStack
+
+import concourse.mybir as mybir
+from concourse.masks import make_identity
+
+F32 = mybir.dt.float32
+BF16 = mybir.dt.bfloat16
+U32 = mybir.dt.uint32
+U8 = mybir.dt.uint8
+FP8X4 = mybir.dt.float8_e4m3fn_x4
+ADD = mybir.AluOpType.add
+MULT = mybir.AluOpType.mult
+RELU = mybir.ActivationFunctionType.Relu
+
+GRAPHS, NODES, D, H = 64, 16, 128, 1024
+P = 128
+PACK = 4
+K_PASS = P * PACK
+PASSES = H // K_PASS
+WORDS = K_PASS // 2
+
+ROW_TILES = GRAPHS * NODES // P
+TILE_GRAPHS = P // NODES
+GROUP_GRAPHS = 4
+GROUP_NODES = GROUP_GRAPHS * NODES
+GROUP_COLS = GROUP_GRAPHS * NODES * NODES
+N_TILE = 512
+RECEIVERS = P // NODES
+
+FLOPS = 2 * GRAPHS * NODES * NODES * H * D
+
+
+def tile_graphdynamics_pa_t_kernel(tc, xi_p, xj_p, node_mask, mb1, mw2, mb2, out):
+    nc = tc.nc
+    xi_rows = xi_p.rearrange("b i k -> (b i) k")
+    xj_rows = xj_p.rearrange("b j k -> (b j) k")
+    out_rows = out.rearrange("b i d -> (b i) d")
+
+    with ExitStack() as ctx:
+        const = ctx.enter_context(tc.tile_pool(name="const", bufs=1))
+        rows = ctx.enter_context(tc.tile_pool(name="rows", bufs=ROW_TILES))
+        turned = ctx.enter_context(tc.tile_pool(name="turned", bufs=2))
+        hidden = ctx.enter_context(tc.tile_pool(name="hidden", bufs=4))
+        packed = ctx.enter_context(tc.tile_pool(name="packed", bufs=4))
+        tail = ctx.enter_context(tc.tile_pool(name="tail", bufs=3))
+        ps_turn = ctx.enter_context(tc.psum_pool(name="ps_turn", bufs=2))
+        ps_acc = ctx.enter_context(tc.psum_pool(name="ps_acc", bufs=2))
+        ps_msg = ctx.enter_context(tc.psum_pool(name="ps_msg", bufs=2))
+        ps_sum = ctx.enter_context(tc.psum_pool(name="ps_sum", bufs=1))
+        ps_out = ctx.enter_context(tc.psum_pool(name="ps_out", bufs=1))
+
+        w_raw = const.tile([P, PASSES, PACK, D], BF16)
+        nc.sync.dma_start(out=w_raw[:], in_=mw2.rearrange("(c p t) d -> p c t d", c=PASSES, p=P, t=PACK))
+        mb1_words = const.tile([P, PASSES, PACK], BF16)
+        with nc.allow_non_contiguous_dma(reason="mb1 in the order of the packed words: runs of 4 values"):
+            nc.sync.dma_start(out=mb1_words[:], in_=mb1.rearrange("(c p t) -> p c t", c=PASSES, p=P, t=PACK))
+        small = const.tile([P, RECEIVERS, NODES], BF16)
+        nc.vector.memset(small[:], 0.0)
+        nc.sync.dma_start(
+            out=small[0:GRAPHS, :, :],
+            in_=node_mask.unsqueeze(1).to_broadcast([GRAPHS, RECEIVERS, NODES]),
+        )
+        nc.sync.dma_start(
+            out=small[GRAPHS : GRAPHS + 1, :, :].rearrange("o r j -> o (r j)"),
+            in_=mb2.unsqueeze(0),
+        )
+        xi_sb = []
+        xj_sb = []
+        for rt in range(ROW_TILES):
+            xi_tile = rows.tile([P, H], BF16, name="xi_tile")
+            nc.sync.dma_start(out=xi_tile[:], in_=xi_rows[rt * P : (rt + 1) * P, :])
+            xj_tile = rows.tile([P, H], BF16, name="xj_tile")
+            nc.sync.dma_start(out=xj_tile[:], in_=xj_rows[rt * P : (rt + 1) * P, :])
+            xi_sb.append(xi_tile)
+            xj_sb.append(xj_tile)
+
+        ident = const.tile([P, P], F32)
+        make_identity(nc, ident[:])
+
+        w_grouped = const.tile([P, PASSES, D, PACK], BF16, align_bytes=64)
+        nc.vector.tensor_copy(out=w_grouped[:], in_=w_raw[:].rearrange("p c t d -> p c d t"))
+        w_codes = const.tile([P, PASSES * D], U32, align_bytes=64)
+        w_scales = const.tile([P, PASSES * D], U8, align_bytes=64)
+        nc.vector.quantize_mx(
+            out=w_codes[:].bitcast(FP8X4),
+            scales=w_scales[:],
+            in_=w_grouped[:].rearrange("p c d t -> p (c d t)"),
+        )
+
+        small_f32 = const.tile([P, P], F32)
+        nc.vector.tensor_copy(out=small_f32[:], in_=small[:].rearrange("p r j -> p (r j)"))
+        small_ps = ps_out.tile([P, P], F32, name="small_ps", tag="ps_out")
+        nc.tensor.transpose(small_ps[:], small_f32[:], ident[:])
+        small_t = const.tile([P, GRAPHS + 1], F32)
+        nc.vector.tensor_copy(out=small_t[:], in_=small_ps[:, 0 : GRAPHS + 1])
+        mb2_col = small_t[:, GRAPHS : GRAPHS + 1]
+
+        pick = const.tile([P, RECEIVERS], F32)
+        nc.vector.tensor_reduce(
+            out=pick[:],
+            in_=ident[:].rearrange("p (r j) -> p r j", j=NODES),
+            axis=mybir.AxisListType.X,
+            op=ADD,
+        )
+        masked_pick = const.tile([P, GRAPHS, RECEIVERS], F32)
+        nc.vector.tensor_tensor(
+            out=masked_pick[:],
+            in0=small_t[:, 0:GRAPHS].unsqueeze(2).to_broadcast([P, GRAPHS, RECEIVERS]),
+            in1=pick[:].unsqueeze(1).to_broadcast([P, GRAPHS, RECEIVERS]),
+            op=MULT,
+        )
+
+        def turn_rows(x_tile, name):
+            words = x_tile[:].bitcast(F32)
+            bank = ps_turn.tile([P, PASSES, 2, P], F32, name="bank")
+            for c in range(PASSES):
+                for u in range(2):
+                    nc.tensor.transpose(bank[:, c, u, :], words[:, c * WORDS + u : (c + 1) * WORDS : 2], ident[:])
+            x_t = turned.tile([P, PASSES, P, PACK], BF16, name=name)
+            nc.scalar.copy(out=x_t[:].bitcast(F32), in_=bank[:].rearrange("p c u r -> p c r u"))
+            return x_t
+
+        for rt in range(ROW_TILES):
+            xi_t = turn_rows(xi_sb[rt], "xi_t")
+            xj_t = turn_rows(xj_sb[rt], "xj_t")
+            recv = turned.tile([P, PASSES, P, PACK], F32, name="recv")
+            nc.vector.tensor_tensor(
+                out=recv[:],
+                in0=xi_t[:],
+                in1=mb1_words[:].unsqueeze(2).to_broadcast([P, PASSES, P, PACK]),
+                op=ADD,
+            )
+            sums_ps = ps_sum.tile([P, P], F32, name="sums_ps")
+
+            for g in range(TILE_GRAPHS // GROUP_GRAPHS):
+                nodes = slice(g * GROUP_NODES, (g + 1) * GROUP_NODES)
+                pair_shape = [P, GROUP_GRAPHS, NODES, NODES, PACK]
+                codes = []
+                scales = []
+                for c in range(PASSES):
+                    h = hidden.tile(pair_shape, BF16, name="h", align_bytes=64)
+                    nc.vector.tensor_tensor(
+                        out=h[:],
+                        in0=recv[:, c, nodes, :]
+                        .rearrange("p (b i) t -> p b i t", b=GROUP_GRAPHS)
+                        .unsqueeze(3)
+                        .to_broadcast(pair_shape),
+                        in1=xj_t[:, c, nodes, :]
+                        .rearrange("p (b j) t -> p b j t", b=GROUP_GRAPHS)
+                        .unsqueeze(2)
+                        .to_broadcast(pair_shape),
+                        op=ADD,
+                    )
+                    h_flat = h[:].rearrange("p b i j t -> p (b i j t)")
+                    nc.scalar.activation(out=h_flat, in_=h_flat, func=RELU)
+                    h_codes = packed.tile([P, GROUP_COLS], U32, name="h_codes", align_bytes=64)
+                    h_scales = packed.tile([P, GROUP_COLS], U8, name="h_scales", align_bytes=64)
+                    nc.vector.quantize_mx(out=h_codes[:].bitcast(FP8X4), scales=h_scales[:], in_=h_flat)
+                    codes.append(h_codes)
+                    scales.append(h_scales)
+
+                for nb in range(GROUP_COLS // N_TILE):
+                    cols = slice(nb * N_TILE, (nb + 1) * N_TILE)
+                    acc = ps_acc.tile([P, N_TILE], F32, name="acc")
+                    for c in range(PASSES):
+                        nc.tensor.matmul_mx(
+                            out=acc[:],
+                            lhsT=w_codes[:, c * D : (c + 1) * D].bitcast(FP8X4),
+                            lhsT_scale=w_scales[:, c * D : (c + 1) * D],
+                            rhs=codes[c][:, cols].bitcast(FP8X4),
+                            rhs_scale=scales[c][:, cols],
+                            start=(c == 0),
+                            stop=(c == PASSES - 1),
+                        )
+                    msg = tail.tile([P, N_TILE], F32, name="msg")
+                    nc.scalar.activation(out=msg[:], in_=acc[:], func=RELU, bias=mb2_col, scale=1.0)
+                    blocks = N_TILE // P
+                    msg_ps = ps_msg.tile([P, blocks, D], F32, name="msg_ps")
+                    for q in range(blocks):
+                        nc.tensor.transpose(msg_ps[:, q, :], msg[:, q * P : (q + 1) * P], ident[:])
+                    msg_t = tail.tile([P, blocks, D], F32, name="msg_t")
+                    nc.scalar.copy(out=msg_t[:], in_=msg_ps[:])
+                    for q in range(blocks):
+                        block = (g * GROUP_COLS + nb * N_TILE) // P + q
+                        graph = rt * TILE_GRAPHS + block * RECEIVERS // NODES
+                        nc.tensor.matmul(
+                            out=sums_ps[:, block * RECEIVERS : (block + 1) * RECEIVERS],
+                            lhsT=msg_t[:, q, :],
+                            rhs=masked_pick[:, graph, :],
+                            start=True,
+                            stop=True,
+                        )
+
+            sums = tail.tile([P, P], F32, name="sums")
+            nc.scalar.copy(out=sums[:], in_=sums_ps[:])
+            out_ps = ps_out.tile([P, D], F32, name="out_ps", tag="ps_out")
+            nc.tensor.transpose(out_ps[:], sums[:], ident[:])
+            out_sb = tail.tile([P, D], F32, name="out_sb")
+            nc.scalar.copy(out=out_sb[:], in_=out_ps[:])
+            nc.sync.dma_start(out=out_rows[rt * P : (rt + 1) * P, :], in_=out_sb[:])

@@ -17,15 +17,11 @@ P = 128
 PACK = 4
 K_PASS = P * PACK
 PASSES = H // K_PASS
-WORDS = K_PASS // 2
-
 ROW_TILES = GRAPHS * NODES // P
 TILE_GRAPHS = P // NODES
-GROUP_GRAPHS = 4
-GROUP_NODES = GROUP_GRAPHS * NODES
-GROUP_COLS = GROUP_GRAPHS * NODES * NODES
 N_TILE = 512
-RECEIVERS = P // NODES
+QUANT_COLS = 1024
+ROT_PE = 10
 
 FLOPS = 2 * GRAPHS * NODES * NODES * H * D
 
@@ -38,44 +34,37 @@ def tile_graphdynamics_pa_t_kernel(tc, xi_p, xj_p, node_mask, mb1, mw2, mb2, out
 
     with ExitStack() as ctx:
         const = ctx.enter_context(tc.tile_pool(name="const", bufs=1))
-        rows = ctx.enter_context(tc.tile_pool(name="rows", bufs=ROW_TILES))
-        turned = ctx.enter_context(tc.tile_pool(name="turned", bufs=2))
-        hidden = ctx.enter_context(tc.tile_pool(name="hidden", bufs=4))
+        rows = ctx.enter_context(tc.tile_pool(name="rows", bufs=3))
+        prep = ctx.enter_context(tc.tile_pool(name="prep", bufs=2))
+        hidden = ctx.enter_context(tc.tile_pool(name="hidden", bufs=3))
         packed = ctx.enter_context(tc.tile_pool(name="packed", bufs=4))
-        tail = ctx.enter_context(tc.tile_pool(name="tail", bufs=3))
-        ps_turn = ctx.enter_context(tc.psum_pool(name="ps_turn", bufs=2))
+        tail = ctx.enter_context(tc.tile_pool(name="tail", bufs=2))
+        ps_pair = ctx.enter_context(tc.psum_pool(name="ps_pair", bufs=4))
         ps_acc = ctx.enter_context(tc.psum_pool(name="ps_acc", bufs=2))
-        ps_msg = ctx.enter_context(tc.psum_pool(name="ps_msg", bufs=2))
-        ps_sum = ctx.enter_context(tc.psum_pool(name="ps_sum", bufs=1))
-        ps_out = ctx.enter_context(tc.psum_pool(name="ps_out", bufs=1))
+        ps_out = ctx.enter_context(tc.psum_pool(name="ps_out", bufs=2))
 
+        mb1_all = const.tile([P, H], BF16)
+        nc.sync.dma_start(out=mb1_all[:], in_=mb1.partition_broadcast(P))
         w_raw = const.tile([P, PASSES, PACK, D], BF16)
-        nc.sync.dma_start(out=w_raw[:], in_=mw2.rearrange("(c p t) d -> p c t d", c=PASSES, p=P, t=PACK))
-        mb1_words = const.tile([P, PASSES, PACK], BF16)
-        with nc.allow_non_contiguous_dma(reason="mb1 in the order of the packed words: runs of 4 values"):
-            nc.sync.dma_start(out=mb1_words[:], in_=mb1.rearrange("(c p t) -> p c t", c=PASSES, p=P, t=PACK))
-        small = const.tile([P, RECEIVERS, NODES], BF16)
-        nc.vector.memset(small[:], 0.0)
-        nc.sync.dma_start(
-            out=small[0:GRAPHS, :, :],
-            in_=node_mask.unsqueeze(1).to_broadcast([GRAPHS, RECEIVERS, NODES]),
+        nc.sync.dma_start(out=w_raw[:], in_=mw2.rearrange("(c t p) d -> p c t d", c=PASSES, t=PACK, p=P))
+        mb2_bf = const.tile([P, 1], BF16)
+        with nc.allow_non_contiguous_dma(reason="mb2: one value a partition, 128 values in all"):
+            nc.scalar.dma_start(out=mb2_bf[:], in_=mb2.unsqueeze(1))
+        mask_all = const.tile([P, GRAPHS, NODES], BF16)
+        nc.scalar.dma_start(
+            out=mask_all[:].rearrange("p b j -> p (b j)"),
+            in_=node_mask.rearrange("b j -> (b j)").partition_broadcast(P),
         )
-        nc.sync.dma_start(
-            out=small[GRAPHS : GRAPHS + 1, :, :].rearrange("o r j -> o (r j)"),
-            in_=mb2.unsqueeze(0),
-        )
-        xi_sb = []
-        xj_sb = []
-        for rt in range(ROW_TILES):
-            xi_tile = rows.tile([P, H], BF16, name="xi_tile")
-            nc.sync.dma_start(out=xi_tile[:], in_=xi_rows[rt * P : (rt + 1) * P, :])
-            xj_tile = rows.tile([P, H], BF16, name="xj_tile")
-            nc.sync.dma_start(out=xj_tile[:], in_=xj_rows[rt * P : (rt + 1) * P, :])
-            xi_sb.append(xi_tile)
-            xj_sb.append(xj_tile)
 
         ident = const.tile([P, P], F32)
         make_identity(nc, ident[:])
+        ident_twice = const.tile([P, TILE_GRAPHS, 2 * NODES], F32)
+        ident_blocks = ident[:].rearrange("p (b j) -> p b j", j=NODES)
+        nc.vector.tensor_copy(out=ident_twice[:, :, 0:NODES], in_=ident_blocks)
+        nc.vector.tensor_copy(out=ident_twice[:, :, NODES : 2 * NODES], in_=ident_blocks)
+
+        mb2_col = const.tile([P, 1], F32)
+        nc.vector.tensor_copy(out=mb2_col[:], in_=mb2_bf[:])
 
         w_grouped = const.tile([P, PASSES, D, PACK], BF16, align_bytes=64)
         nc.vector.tensor_copy(out=w_grouped[:], in_=w_raw[:].rearrange("p c t d -> p c d t"))
@@ -87,114 +76,110 @@ def tile_graphdynamics_pa_t_kernel(tc, xi_p, xj_p, node_mask, mb1, mw2, mb2, out
             in_=w_grouped[:].rearrange("p c d t -> p (c d t)"),
         )
 
-        small_f32 = const.tile([P, P], F32)
-        nc.vector.tensor_copy(out=small_f32[:], in_=small[:].rearrange("p r j -> p (r j)"))
-        small_ps = ps_out.tile([P, P], F32, name="small_ps", tag="ps_out")
-        nc.tensor.transpose(small_ps[:], small_f32[:], ident[:])
-        small_t = const.tile([P, GRAPHS + 1], F32)
-        nc.vector.tensor_copy(out=small_t[:], in_=small_ps[:, 0 : GRAPHS + 1])
-        mb2_col = small_t[:, GRAPHS : GRAPHS + 1]
-
-        pick = const.tile([P, RECEIVERS], F32)
-        nc.vector.tensor_reduce(
-            out=pick[:],
-            in_=ident[:].rearrange("p (r j) -> p r j", j=NODES),
-            axis=mybir.AxisListType.X,
-            op=ADD,
-        )
-        masked_pick = const.tile([P, GRAPHS, RECEIVERS], F32)
-        nc.vector.tensor_tensor(
-            out=masked_pick[:],
-            in0=small_t[:, 0:GRAPHS].unsqueeze(2).to_broadcast([P, GRAPHS, RECEIVERS]),
-            in1=pick[:].unsqueeze(1).to_broadcast([P, GRAPHS, RECEIVERS]),
-            op=MULT,
-        )
-
-        def turn_rows(x_tile, name):
-            words = x_tile[:].bitcast(F32)
-            bank = ps_turn.tile([P, PASSES, 2, P], F32, name="bank")
-            for c in range(PASSES):
-                for u in range(2):
-                    nc.tensor.transpose(bank[:, c, u, :], words[:, c * WORDS + u : (c + 1) * WORDS : 2], ident[:])
-            x_t = turned.tile([P, PASSES, P, PACK], BF16, name=name)
-            nc.scalar.copy(out=x_t[:].bitcast(F32), in_=bank[:].rearrange("p c u r -> p c r u"))
-            return x_t
+        mask_twice = const.tile([P, GRAPHS, 2 * NODES], BF16)
+        nc.vector.tensor_copy(out=mask_twice[:, :, 0:NODES], in_=mask_all[:])
+        nc.vector.tensor_copy(out=mask_twice[:, :, NODES : 2 * NODES], in_=mask_all[:])
+        mask_rot = const.tile([P, NODES, GRAPHS, NODES], BF16)
+        for q in range(NODES):
+            nc.vector.tensor_copy(out=mask_rot[:, q, :, :], in_=mask_twice[:, :, q : q + NODES])
 
         for rt in range(ROW_TILES):
-            xi_t = turn_rows(xi_sb[rt], "xi_t")
-            xj_t = turn_rows(xj_sb[rt], "xj_t")
-            recv = turned.tile([P, PASSES, P, PACK], F32, name="recv")
-            nc.vector.tensor_tensor(
-                out=recv[:],
-                in0=xi_t[:],
-                in1=mb1_words[:].unsqueeze(2).to_broadcast([P, PASSES, P, PACK]),
-                op=ADD,
-            )
-            sums_ps = ps_sum.tile([P, P], F32, name="sums_ps")
+            tile_rows = slice(rt * P, (rt + 1) * P)
+            xi_tile = rows.tile([P, H], BF16, name="xi_tile")
+            nc.sync.dma_start(out=xi_tile[:], in_=xi_rows[tile_rows, :])
+            xj_tile = rows.tile([P, H], BF16, name="xj_tile")
+            nc.sync.dma_start(out=xj_tile[:], in_=xj_rows[tile_rows, :])
 
-            for g in range(TILE_GRAPHS // GROUP_GRAPHS):
-                nodes = slice(g * GROUP_NODES, (g + 1) * GROUP_NODES)
-                pair_shape = [P, GROUP_GRAPHS, NODES, NODES, PACK]
-                codes = []
-                scales = []
-                for c in range(PASSES):
-                    h = hidden.tile(pair_shape, BF16, name="h", align_bytes=64)
+            recv_rows = prep.tile([P, H], F32, name="recv_rows")
+            nc.vector.tensor_tensor(out=recv_rows[:], in0=xi_tile[:], in1=mb1_all[:], op=ADD)
+            send_rows = prep.tile([P, H], F32, name="send_rows")
+            nc.scalar.copy(out=send_rows[:], in_=xj_tile[:])
+
+            recv_t = prep.tile([P, PASSES, P, PACK], F32, name="recv_t")
+            send_t = prep.tile([P, PASSES, TILE_GRAPHS, 2 * NODES, PACK], BF16, name="send_t")
+            for c in range(PASSES):
+                recv_ps = ps_pair.tile([P, PACK, P], F32, name="recv_ps", tag="pair")
+                send_ps = ps_pair.tile([P, PACK, P], F32, name="send_ps", tag="pair")
+                for t in range(PACK):
+                    ks = slice(c * K_PASS + t * P, c * K_PASS + (t + 1) * P)
+                    nc.tensor.transpose(recv_ps[:, t, :], recv_rows[:, ks], ident[:])
+                    nc.tensor.transpose(send_ps[:, t, :], send_rows[:, ks], ident[:])
+                nc.scalar.copy(out=recv_t[:, c, :, :], in_=recv_ps[:].rearrange("p t r -> p r t"))
+                nc.scalar.copy(
+                    out=send_t[:, c, :, 0:NODES, :],
+                    in_=send_ps[:].rearrange("p t (b j) -> p b j t", j=NODES),
+                )
+            nc.vector.tensor_copy(out=send_t[:, :, :, NODES : 2 * NODES, :], in_=send_t[:, :, :, 0:NODES, :])
+
+            codes = []
+            scales = []
+            for c in range(PASSES):
+                h = hidden.tile([P, NODES, P, PACK], BF16, name="h", align_bytes=64)
+                for q in range(ROT_PE):
+                    pair_ps = ps_pair.tile([P, PACK, P], F32, name="pair_ps", tag="pair")
+                    for t in range(PACK):
+                        ks = slice(c * K_PASS + t * P, c * K_PASS + (t + 1) * P)
+                        nc.tensor.matmul(
+                            out=pair_ps[:, t, :], lhsT=recv_rows[:, ks], rhs=ident[:],
+                            is_transpose=True, start=True, stop=False,
+                        )
+                        nc.tensor.matmul(
+                            out=pair_ps[:, t, :], lhsT=send_rows[:, ks], rhs=ident_twice[:, :, q : q + NODES],
+                            is_transpose=True, start=False, stop=True,
+                        )
+                    nc.scalar.activation(out=h[:, q, :, :], in_=pair_ps[:].rearrange("p t r -> p r t"), func=RELU)
+                for q in range(ROT_PE, NODES):
                     nc.vector.tensor_tensor(
-                        out=h[:],
-                        in0=recv[:, c, nodes, :]
-                        .rearrange("p (b i) t -> p b i t", b=GROUP_GRAPHS)
-                        .unsqueeze(3)
-                        .to_broadcast(pair_shape),
-                        in1=xj_t[:, c, nodes, :]
-                        .rearrange("p (b j) t -> p b j t", b=GROUP_GRAPHS)
-                        .unsqueeze(2)
-                        .to_broadcast(pair_shape),
+                        out=h[:, q, :, :].rearrange("p (b i) t -> p b i t", i=NODES),
+                        in0=recv_t[:, c, :, :].rearrange("p (b i) t -> p b i t", i=NODES),
+                        in1=send_t[:, c, :, q : q + NODES, :],
                         op=ADD,
                     )
-                    h_flat = h[:].rearrange("p b i j t -> p (b i j t)")
-                    nc.scalar.activation(out=h_flat, in_=h_flat, func=RELU)
-                    h_codes = packed.tile([P, GROUP_COLS], U32, name="h_codes", align_bytes=64)
-                    h_scales = packed.tile([P, GROUP_COLS], U8, name="h_scales", align_bytes=64)
-                    nc.vector.quantize_mx(out=h_codes[:].bitcast(FP8X4), scales=h_scales[:], in_=h_flat)
-                    codes.append(h_codes)
-                    scales.append(h_scales)
+                own = h[:, ROT_PE:NODES, :, :].rearrange("p q r t -> p (q r t)")
+                nc.vector.tensor_scalar_max(out=own, in0=own, scalar1=0.0)
 
-                for nb in range(GROUP_COLS // N_TILE):
-                    cols = slice(nb * N_TILE, (nb + 1) * N_TILE)
-                    acc = ps_acc.tile([P, N_TILE], F32, name="acc")
-                    for c in range(PASSES):
-                        nc.tensor.matmul_mx(
-                            out=acc[:],
-                            lhsT=w_codes[:, c * D : (c + 1) * D].bitcast(FP8X4),
-                            lhsT_scale=w_scales[:, c * D : (c + 1) * D],
-                            rhs=codes[c][:, cols].bitcast(FP8X4),
-                            rhs_scale=scales[c][:, cols],
-                            start=(c == 0),
-                            stop=(c == PASSES - 1),
-                        )
-                    msg = tail.tile([P, N_TILE], F32, name="msg")
-                    nc.scalar.activation(out=msg[:], in_=acc[:], func=RELU, bias=mb2_col, scale=1.0)
-                    blocks = N_TILE // P
-                    msg_ps = ps_msg.tile([P, blocks, D], F32, name="msg_ps")
-                    for q in range(blocks):
-                        nc.tensor.transpose(msg_ps[:, q, :], msg[:, q * P : (q + 1) * P], ident[:])
-                    msg_t = tail.tile([P, blocks, D], F32, name="msg_t")
-                    nc.scalar.copy(out=msg_t[:], in_=msg_ps[:])
-                    for q in range(blocks):
-                        block = (g * GROUP_COLS + nb * N_TILE) // P + q
-                        graph = rt * TILE_GRAPHS + block * RECEIVERS // NODES
-                        nc.tensor.matmul(
-                            out=sums_ps[:, block * RECEIVERS : (block + 1) * RECEIVERS],
-                            lhsT=msg_t[:, q, :],
-                            rhs=masked_pick[:, graph, :],
-                            start=True,
-                            stop=True,
-                        )
+                h_flat = h[:].rearrange("p q r t -> p (q r t)")
+                h_codes = packed.tile([P, NODES * P], U32, name="h_codes", align_bytes=64)
+                h_scales = packed.tile([P, NODES * P], U8, name="h_scales", align_bytes=64)
+                for part in range(NODES * P // QUANT_COLS):
+                    cols = slice(part * QUANT_COLS, (part + 1) * QUANT_COLS)
+                    nc.vector.quantize_mx(
+                        out=h_codes[:, cols].bitcast(FP8X4),
+                        scales=h_scales[:, cols],
+                        in_=h_flat[:, part * QUANT_COLS * PACK : (part + 1) * QUANT_COLS * PACK],
+                    )
+                codes.append(h_codes)
+                scales.append(h_scales)
 
-            sums = tail.tile([P, P], F32, name="sums")
-            nc.scalar.copy(out=sums[:], in_=sums_ps[:])
-            out_ps = ps_out.tile([P, D], F32, name="out_ps", tag="ps_out")
-            nc.tensor.transpose(out_ps[:], sums[:], ident[:])
+            msg = tail.tile([P, NODES, P], F32, name="msg")
+            out_ps = ps_out.tile([P, D], F32, name="out_ps")
+            rots = N_TILE // P
+            for nb in range(NODES // rots):
+                cols = slice(nb * N_TILE, (nb + 1) * N_TILE)
+                qs = slice(nb * rots, (nb + 1) * rots)
+                acc = ps_acc.tile([P, rots, P], F32, name="acc")
+                for c in range(PASSES):
+                    nc.tensor.matmul_mx(
+                        out=acc[:].rearrange("d q r -> d (q r)"),
+                        lhsT=w_codes[:, c * D : (c + 1) * D].bitcast(FP8X4),
+                        lhsT_scale=w_scales[:, c * D : (c + 1) * D],
+                        rhs=codes[c][:, cols].bitcast(FP8X4),
+                        rhs_scale=scales[c][:, cols],
+                        start=(c == 0),
+                        stop=(c == PASSES - 1),
+                    )
+                nc.scalar.activation(out=msg[:, qs, :], in_=acc[:], func=RELU, bias=mb2_col[:], scale=1.0)
+                nc.vector.tensor_tensor(
+                    out=msg[:, qs, :],
+                    in0=msg[:, qs, :],
+                    in1=mask_rot[:, qs, rt * TILE_GRAPHS : (rt + 1) * TILE_GRAPHS, :].rearrange("p q b i -> p q (b i)"),
+                    op=MULT,
+                )
+                for q in range(nb * rots, (nb + 1) * rots):
+                    nc.tensor.matmul(
+                        out=out_ps[:], lhsT=msg[:, q, :], rhs=ident[:],
+                        is_transpose=True, start=(q == 0), stop=(q == NODES - 1),
+                    )
             out_sb = tail.tile([P, D], F32, name="out_sb")
             nc.scalar.copy(out=out_sb[:], in_=out_ps[:])
-            nc.sync.dma_start(out=out_rows[rt * P : (rt + 1) * P, :], in_=out_sb[:])
+            nc.sync.dma_start(out=out_rows[tile_rows, :], in_=out_sb[:])

@@ -20,8 +20,8 @@ PASSES = H // K_PASS
 ROW_TILES = GRAPHS * NODES // P
 TILE_GRAPHS = P // NODES
 N_TILE = 512
-QUANT_COLS = 1024
-ROT_PE = 10
+BANK_ROTS = N_TILE // P
+HALF = NODES // 2
 
 FLOPS = 2 * GRAPHS * NODES * NODES * H * D
 
@@ -36,36 +36,66 @@ def tile_graphdynamics_pa_t_kernel(tc, xi_p, xj_p, node_mask, mb1, mw2, mb2, out
         const = ctx.enter_context(tc.tile_pool(name="const", bufs=1))
         rows = ctx.enter_context(tc.tile_pool(name="rows", bufs=3))
         prep = ctx.enter_context(tc.tile_pool(name="prep", bufs=2))
-        hidden = ctx.enter_context(tc.tile_pool(name="hidden", bufs=3))
-        packed = ctx.enter_context(tc.tile_pool(name="packed", bufs=4))
-        tail = ctx.enter_context(tc.tile_pool(name="tail", bufs=2))
+        hidden = ctx.enter_context(tc.tile_pool(name="hidden", bufs=2))
+        packed = ctx.enter_context(tc.tile_pool(name="packed", bufs=8))
+        tail = ctx.enter_context(tc.tile_pool(name="tail", bufs=3))
         ps_pair = ctx.enter_context(tc.psum_pool(name="ps_pair", bufs=4))
         ps_acc = ctx.enter_context(tc.psum_pool(name="ps_acc", bufs=2))
         ps_out = ctx.enter_context(tc.psum_pool(name="ps_out", bufs=2))
 
-        mb1_all = const.tile([P, H], BF16)
-        nc.sync.dma_start(out=mb1_all[:], in_=mb1.partition_broadcast(P))
-        w_raw = const.tile([P, PASSES, PACK, D], BF16)
-        nc.sync.dma_start(out=w_raw[:], in_=mw2.rearrange("(c t p) d -> p c t d", c=PASSES, t=PACK, p=P))
-        mb2_bf = const.tile([P, 1], BF16)
-        with nc.allow_non_contiguous_dma(reason="mb2: one value a partition, 128 values in all"):
-            nc.scalar.dma_start(out=mb2_bf[:], in_=mb2.unsqueeze(1))
-        mask_all = const.tile([P, GRAPHS, NODES], BF16)
-        nc.scalar.dma_start(
-            out=mask_all[:].rearrange("p b j -> p (b j)"),
-            in_=node_mask.rearrange("b j -> (b j)").partition_broadcast(P),
-        )
-
         ident = const.tile([P, P], F32)
         make_identity(nc, ident[:])
+        mb1_all = const.tile([P, H], BF16)
+        nc.scalar.dma_start(out=mb1_all[:], in_=mb1.partition_broadcast(P))
+
+        def pass_slice(c, t):
+            return slice(c * K_PASS + t * P, c * K_PASS + (t + 1) * P)
+
+        def prepare(rt):
+            xi_tile = rows.tile([P, H], BF16, name="xi_tile")
+            nc.sync.dma_start(out=xi_tile[:], in_=xi_rows[rt * P : (rt + 1) * P, :])
+            xj_tile = rows.tile([P, H], BF16, name="xj_tile")
+            nc.sync.dma_start(out=xj_tile[:], in_=xj_rows[rt * P : (rt + 1) * P, :])
+            recv_rows = prep.tile([P, H], F32, name="recv_rows")
+            nc.vector.tensor_tensor(out=recv_rows[:], in0=xi_tile[:], in1=mb1_all[:], op=ADD)
+            send_rows = prep.tile([P, H], F32, name="send_rows")
+            nc.scalar.copy(out=send_rows[:], in_=xj_tile[:])
+            recv_t = prep.tile([P, PASSES, P, PACK], F32, name="recv_t")
+            send_t = prep.tile([P, PASSES, TILE_GRAPHS, 2 * NODES, PACK], BF16, name="send_t")
+            for c in range(PASSES):
+                recv_ps = ps_pair.tile([P, PACK, P], F32, name="recv_ps", tag="pair")
+                send_ps = ps_pair.tile([P, PACK, P], F32, name="send_ps", tag="pair")
+                for t in range(PACK):
+                    nc.tensor.transpose(recv_ps[:, t, :], recv_rows[:, pass_slice(c, t)], ident[:])
+                for t in range(PACK):
+                    nc.tensor.transpose(send_ps[:, t, :], send_rows[:, pass_slice(c, t)], ident[:])
+                nc.scalar.copy(out=recv_t[:, c, :, :], in_=recv_ps[:].rearrange("p t r -> p r t"))
+                nc.scalar.copy(
+                    out=send_t[:, c, :, 0:NODES, :],
+                    in_=send_ps[:].rearrange("p t (b j) -> p b j t", j=NODES),
+                )
+            nc.vector.tensor_copy(out=send_t[:, :, :, NODES : 2 * NODES, :], in_=send_t[:, :, :, 0:NODES, :])
+            return recv_rows, send_rows, recv_t, send_t
+
+        def quantise(h_half):
+            h_codes = packed.tile([P, HALF * P], U32, name="h_codes", align_bytes=64)
+            h_scales = packed.tile([P, HALF * P], U8, name="h_scales", align_bytes=64)
+            nc.vector.quantize_mx(
+                out=h_codes[:].bitcast(FP8X4),
+                scales=h_scales[:],
+                in_=h_half.rearrange("p q r t -> p (q r t)"),
+            )
+            return h_codes, h_scales
+
+        ready = prepare(0)
+
         ident_twice = const.tile([P, TILE_GRAPHS, 2 * NODES], F32)
         ident_blocks = ident[:].rearrange("p (b j) -> p b j", j=NODES)
         nc.vector.tensor_copy(out=ident_twice[:, :, 0:NODES], in_=ident_blocks)
         nc.vector.tensor_copy(out=ident_twice[:, :, NODES : 2 * NODES], in_=ident_blocks)
 
-        mb2_col = const.tile([P, 1], F32)
-        nc.vector.tensor_copy(out=mb2_col[:], in_=mb2_bf[:])
-
+        w_raw = const.tile([P, PASSES, PACK, D], BF16)
+        nc.sync.dma_start(out=w_raw[:], in_=mw2.rearrange("(c t p) d -> p c t d", c=PASSES, t=PACK, p=P))
         w_grouped = const.tile([P, PASSES, D, PACK], BF16, align_bytes=64)
         nc.vector.tensor_copy(out=w_grouped[:], in_=w_raw[:].rearrange("p c t d -> p c d t"))
         w_codes = const.tile([P, PASSES * D], U32, align_bytes=64)
@@ -76,6 +106,17 @@ def tile_graphdynamics_pa_t_kernel(tc, xi_p, xj_p, node_mask, mb1, mw2, mb2, out
             in_=w_grouped[:].rearrange("p c d t -> p (c d t)"),
         )
 
+        mb2_bf = const.tile([P, 1], BF16)
+        with nc.allow_non_contiguous_dma(reason="mb2: one value a partition, 128 values in all"):
+            nc.scalar.dma_start(out=mb2_bf[:], in_=mb2.unsqueeze(1))
+        mb2_col = const.tile([P, 1], F32)
+        nc.vector.tensor_copy(out=mb2_col[:], in_=mb2_bf[:])
+
+        mask_all = const.tile([P, GRAPHS, NODES], BF16)
+        nc.scalar.dma_start(
+            out=mask_all[:].rearrange("p b j -> p (b j)"),
+            in_=node_mask.rearrange("b j -> (b j)").partition_broadcast(P),
+        )
         mask_twice = const.tile([P, GRAPHS, 2 * NODES], BF16)
         nc.vector.tensor_copy(out=mask_twice[:, :, 0:NODES], in_=mask_all[:])
         nc.vector.tensor_copy(out=mask_twice[:, :, NODES : 2 * NODES], in_=mask_all[:])
@@ -84,102 +125,75 @@ def tile_graphdynamics_pa_t_kernel(tc, xi_p, xj_p, node_mask, mb1, mw2, mb2, out
             nc.vector.tensor_copy(out=mask_rot[:, q, :, :], in_=mask_twice[:, :, q : q + NODES])
 
         for rt in range(ROW_TILES):
-            tile_rows = slice(rt * P, (rt + 1) * P)
-            xi_tile = rows.tile([P, H], BF16, name="xi_tile")
-            nc.sync.dma_start(out=xi_tile[:], in_=xi_rows[tile_rows, :])
-            xj_tile = rows.tile([P, H], BF16, name="xj_tile")
-            nc.sync.dma_start(out=xj_tile[:], in_=xj_rows[tile_rows, :])
+            recv_rows, send_rows, recv_t, send_t = ready
+            if rt + 1 < ROW_TILES:
+                ready = prepare(rt + 1)
 
-            recv_rows = prep.tile([P, H], F32, name="recv_rows")
-            nc.vector.tensor_tensor(out=recv_rows[:], in0=xi_tile[:], in1=mb1_all[:], op=ADD)
-            send_rows = prep.tile([P, H], F32, name="send_rows")
-            nc.scalar.copy(out=send_rows[:], in_=xj_tile[:])
-
-            recv_t = prep.tile([P, PASSES, P, PACK], F32, name="recv_t")
-            send_t = prep.tile([P, PASSES, TILE_GRAPHS, 2 * NODES, PACK], BF16, name="send_t")
-            for c in range(PASSES):
-                recv_ps = ps_pair.tile([P, PACK, P], F32, name="recv_ps", tag="pair")
-                send_ps = ps_pair.tile([P, PACK, P], F32, name="send_ps", tag="pair")
-                for t in range(PACK):
-                    ks = slice(c * K_PASS + t * P, c * K_PASS + (t + 1) * P)
-                    nc.tensor.transpose(recv_ps[:, t, :], recv_rows[:, ks], ident[:])
-                    nc.tensor.transpose(send_ps[:, t, :], send_rows[:, ks], ident[:])
-                nc.scalar.copy(out=recv_t[:, c, :, :], in_=recv_ps[:].rearrange("p t r -> p r t"))
-                nc.scalar.copy(
-                    out=send_t[:, c, :, 0:NODES, :],
-                    in_=send_ps[:].rearrange("p t (b j) -> p b j t", j=NODES),
+            h_own = hidden.tile([P, PASSES, HALF, P, PACK], BF16, name="h_own", align_bytes=64)
+            for ql in range(HALF):
+                q = HALF + ql
+                nc.vector.tensor_tensor(
+                    out=h_own[:, :, ql, :, :].rearrange("p c (b i) t -> p c b i t", i=NODES),
+                    in0=recv_t[:].rearrange("p c (b i) t -> p c b i t", i=NODES),
+                    in1=send_t[:, :, :, q : q + NODES, :],
+                    op=ADD,
                 )
-            nc.vector.tensor_copy(out=send_t[:, :, :, NODES : 2 * NODES, :], in_=send_t[:, :, :, 0:NODES, :])
+            own_flat = h_own[:].rearrange("p c q r t -> p (c q r t)")
+            nc.vector.tensor_scalar_max(out=own_flat, in0=own_flat, scalar1=0.0)
+            own_q = [quantise(h_own[:, c, :, :, :]) for c in range(PASSES)]
 
-            codes = []
-            scales = []
+            summed_q = []
             for c in range(PASSES):
-                h = hidden.tile([P, NODES, P, PACK], BF16, name="h", align_bytes=64)
-                for q in range(ROT_PE):
+                h_sum = hidden.tile([P, HALF, P, PACK], BF16, name="h_sum", align_bytes=64, bufs=3)
+                for q in range(HALF):
                     pair_ps = ps_pair.tile([P, PACK, P], F32, name="pair_ps", tag="pair")
                     for t in range(PACK):
-                        ks = slice(c * K_PASS + t * P, c * K_PASS + (t + 1) * P)
                         nc.tensor.matmul(
-                            out=pair_ps[:, t, :], lhsT=recv_rows[:, ks], rhs=ident[:],
+                            out=pair_ps[:, t, :], lhsT=recv_rows[:, pass_slice(c, t)], rhs=ident[:],
                             is_transpose=True, start=True, stop=False,
                         )
                         nc.tensor.matmul(
-                            out=pair_ps[:, t, :], lhsT=send_rows[:, ks], rhs=ident_twice[:, :, q : q + NODES],
+                            out=pair_ps[:, t, :], lhsT=send_rows[:, pass_slice(c, t)],
+                            rhs=ident_twice[:, :, q : q + NODES],
                             is_transpose=True, start=False, stop=True,
                         )
-                    nc.scalar.activation(out=h[:, q, :, :], in_=pair_ps[:].rearrange("p t r -> p r t"), func=RELU)
-                for q in range(ROT_PE, NODES):
-                    nc.vector.tensor_tensor(
-                        out=h[:, q, :, :].rearrange("p (b i) t -> p b i t", i=NODES),
-                        in0=recv_t[:, c, :, :].rearrange("p (b i) t -> p b i t", i=NODES),
-                        in1=send_t[:, c, :, q : q + NODES, :],
-                        op=ADD,
+                    nc.scalar.activation(
+                        out=h_sum[:, q, :, :], in_=pair_ps[:].rearrange("p t r -> p r t"), func=RELU
                     )
-                own = h[:, ROT_PE:NODES, :, :].rearrange("p q r t -> p (q r t)")
-                nc.vector.tensor_scalar_max(out=own, in0=own, scalar1=0.0)
+                summed_q.append(quantise(h_sum[:]))
 
-                h_flat = h[:].rearrange("p q r t -> p (q r t)")
-                h_codes = packed.tile([P, NODES * P], U32, name="h_codes", align_bytes=64)
-                h_scales = packed.tile([P, NODES * P], U8, name="h_scales", align_bytes=64)
-                for part in range(NODES * P // QUANT_COLS):
-                    cols = slice(part * QUANT_COLS, (part + 1) * QUANT_COLS)
-                    nc.vector.quantize_mx(
-                        out=h_codes[:, cols].bitcast(FP8X4),
-                        scales=h_scales[:, cols],
-                        in_=h_flat[:, part * QUANT_COLS * PACK : (part + 1) * QUANT_COLS * PACK],
-                    )
-                codes.append(h_codes)
-                scales.append(h_scales)
-
-            msg = tail.tile([P, NODES, P], F32, name="msg")
             out_ps = ps_out.tile([P, D], F32, name="out_ps")
-            rots = N_TILE // P
-            for nb in range(NODES // rots):
-                cols = slice(nb * N_TILE, (nb + 1) * N_TILE)
-                qs = slice(nb * rots, (nb + 1) * rots)
-                acc = ps_acc.tile([P, rots, P], F32, name="acc")
+            banks = NODES // BANK_ROTS
+            for nb in range(banks):
+                operands = own_q if nb < banks // 2 else summed_q
+                first_rot = (HALF + nb * BANK_ROTS) % NODES
+                cols = slice((first_rot % HALF) * P, (first_rot % HALF + BANK_ROTS) * P)
+                acc = ps_acc.tile([P, BANK_ROTS, P], F32, name="acc")
                 for c in range(PASSES):
                     nc.tensor.matmul_mx(
                         out=acc[:].rearrange("d q r -> d (q r)"),
                         lhsT=w_codes[:, c * D : (c + 1) * D].bitcast(FP8X4),
                         lhsT_scale=w_scales[:, c * D : (c + 1) * D],
-                        rhs=codes[c][:, cols].bitcast(FP8X4),
-                        rhs_scale=scales[c][:, cols],
+                        rhs=operands[c][0][:, cols].bitcast(FP8X4),
+                        rhs_scale=operands[c][1][:, cols],
                         start=(c == 0),
                         stop=(c == PASSES - 1),
                     )
-                nc.scalar.activation(out=msg[:, qs, :], in_=acc[:], func=RELU, bias=mb2_col[:], scale=1.0)
+                msg = tail.tile([P, BANK_ROTS, P], F32, name="msg")
+                nc.scalar.activation(out=msg[:], in_=acc[:], func=RELU, bias=mb2_col[:], scale=1.0)
                 nc.vector.tensor_tensor(
-                    out=msg[:, qs, :],
-                    in0=msg[:, qs, :],
-                    in1=mask_rot[:, qs, rt * TILE_GRAPHS : (rt + 1) * TILE_GRAPHS, :].rearrange("p q b i -> p q (b i)"),
+                    out=msg[:],
+                    in0=msg[:],
+                    in1=mask_rot[
+                        :, first_rot : first_rot + BANK_ROTS, rt * TILE_GRAPHS : (rt + 1) * TILE_GRAPHS, :
+                    ].rearrange("p q b i -> p q (b i)"),
                     op=MULT,
                 )
-                for q in range(nb * rots, (nb + 1) * rots):
+                for ql in range(BANK_ROTS):
                     nc.tensor.matmul(
-                        out=out_ps[:], lhsT=msg[:, q, :], rhs=ident[:],
-                        is_transpose=True, start=(q == 0), stop=(q == NODES - 1),
+                        out=out_ps[:], lhsT=msg[:, ql, :], rhs=ident[:], is_transpose=True,
+                        start=(nb == 0 and ql == 0), stop=(nb == banks - 1 and ql == BANK_ROTS - 1),
                     )
             out_sb = tail.tile([P, D], F32, name="out_sb")
             nc.scalar.copy(out=out_sb[:], in_=out_ps[:])
-            nc.sync.dma_start(out=out_rows[tile_rows, :], in_=out_sb[:])
+            nc.sync.dma_start(out=out_rows[rt * P : (rt + 1) * P, :], in_=out_sb[:])

@@ -17,19 +17,23 @@ P = 128
 PACK = 4
 K_PASS = P * PACK
 PASSES = H // K_PASS
-ROW_TILES = GRAPHS * NODES // P
-TILE_GRAPHS = P // NODES
+CHUNKS = PASSES * PACK
+TILE_GRAPHS = 8
+TILES = GRAPHS // TILE_GRAPHS
 N_TILE = 512
 BANK_ROTS = N_TILE // P
-HALF = NODES // 2
+BANK_GRAPHS = N_TILE // P
+BANK_NODES = BANK_GRAPHS * NODES
+QUANT_ROTS = 8
+ROT_PE = 9
 
 FLOPS = 2 * GRAPHS * NODES * NODES * H * D
 
 
 def tile_graphdynamics_pa_t_kernel(tc, xi_p, xj_p, node_mask, mb1, mw2, mb2, out):
     nc = tc.nc
-    xi_rows = xi_p.rearrange("b i k -> (b i) k")
-    xj_rows = xj_p.rearrange("b j k -> (b j) k")
+    xi_chunks = xi_p.rearrange("b i (s k) -> (i s) b k", s=CHUNKS)
+    xj_chunks = xj_p.rearrange("b j (s k) -> (j s) b k", s=CHUNKS)
     out_rows = out.rearrange("b i d -> (b i) d")
 
     with ExitStack() as ctx:
@@ -45,54 +49,58 @@ def tile_graphdynamics_pa_t_kernel(tc, xi_p, xj_p, node_mask, mb1, mw2, mb2, out
 
         ident = const.tile([P, P], F32)
         make_identity(nc, ident[:])
-        mb1_all = const.tile([P, H], BF16)
-        nc.scalar.dma_start(out=mb1_all[:], in_=mb1.partition_broadcast(P))
+        mb1_rows = const.tile([P, P], BF16)
+        for node in range(NODES):
+            nc.scalar.dma_start(
+                out=mb1_rows[node * CHUNKS : (node + 1) * CHUNKS, :],
+                in_=mb1.rearrange("(s k) -> s k", s=CHUNKS),
+            )
 
-        def pass_slice(c, t):
-            return slice(c * K_PASS + t * P, c * K_PASS + (t + 1) * P)
-
-        def prepare(rt):
-            xi_tile = rows.tile([P, H], BF16, name="xi_tile")
-            nc.sync.dma_start(out=xi_tile[:], in_=xi_rows[rt * P : (rt + 1) * P, :])
-            xj_tile = rows.tile([P, H], BF16, name="xj_tile")
-            nc.sync.dma_start(out=xj_tile[:], in_=xj_rows[rt * P : (rt + 1) * P, :])
-            recv_rows = prep.tile([P, H], F32, name="recv_rows")
-            nc.vector.tensor_tensor(out=recv_rows[:], in0=xi_tile[:], in1=mb1_all[:], op=ADD)
-            send_rows = prep.tile([P, H], F32, name="send_rows")
+        def prepare(tile_index):
+            graphs = slice(tile_index * TILE_GRAPHS, (tile_index + 1) * TILE_GRAPHS)
+            xi_tile = rows.tile([P, TILE_GRAPHS, P], BF16, name="xi_tile")
+            nc.sync.dma_start(out=xi_tile[:], in_=xi_chunks[:, graphs, :])
+            xj_tile = rows.tile([P, TILE_GRAPHS, P], BF16, name="xj_tile")
+            nc.sync.dma_start(out=xj_tile[:], in_=xj_chunks[:, graphs, :])
+            recv_rows = prep.tile([P, TILE_GRAPHS, P], F32, name="recv_rows")
+            nc.vector.tensor_tensor(
+                out=recv_rows[:],
+                in0=xi_tile[:],
+                in1=mb1_rows[:].unsqueeze(1).to_broadcast([P, TILE_GRAPHS, P]),
+                op=ADD,
+            )
+            send_rows = prep.tile([P, TILE_GRAPHS, P], F32, name="send_rows")
             nc.scalar.copy(out=send_rows[:], in_=xj_tile[:])
-            recv_t = prep.tile([P, PASSES, P, PACK], F32, name="recv_t")
+            recv_t = prep.tile([P, PASSES, TILE_GRAPHS, NODES, PACK], F32, name="recv_t")
             send_t = prep.tile([P, PASSES, TILE_GRAPHS, 2 * NODES, PACK], BF16, name="send_t")
-            for c in range(PASSES):
-                recv_ps = ps_pair.tile([P, PACK, P], F32, name="recv_ps", tag="pair")
-                send_ps = ps_pair.tile([P, PACK, P], F32, name="send_ps", tag="pair")
-                for t in range(PACK):
-                    nc.tensor.transpose(recv_ps[:, t, :], recv_rows[:, pass_slice(c, t)], ident[:])
-                for t in range(PACK):
-                    nc.tensor.transpose(send_ps[:, t, :], send_rows[:, pass_slice(c, t)], ident[:])
-                nc.scalar.copy(out=recv_t[:, c, :, :], in_=recv_ps[:].rearrange("p t r -> p r t"))
+            for first in range(0, TILE_GRAPHS, BANK_GRAPHS):
+                recv_ps = ps_pair.tile([P, BANK_GRAPHS, NODES, PASSES, PACK], F32, name="recv_ps", tag="pair")
+                send_ps = ps_pair.tile([P, BANK_GRAPHS, NODES, PASSES, PACK], F32, name="send_ps", tag="pair")
+                for g in range(BANK_GRAPHS):
+                    nc.tensor.transpose(
+                        recv_ps[:, g, :, :, :].rearrange("p i c t -> p (i c t)"), recv_rows[:, first + g, :], ident[:]
+                    )
+                for g in range(BANK_GRAPHS):
+                    nc.tensor.transpose(
+                        send_ps[:, g, :, :, :].rearrange("p j c t -> p (j c t)"), send_rows[:, first + g, :], ident[:]
+                    )
                 nc.scalar.copy(
-                    out=send_t[:, c, :, 0:NODES, :],
-                    in_=send_ps[:].rearrange("p t (b j) -> p b j t", j=NODES),
+                    out=recv_t[:, :, first : first + BANK_GRAPHS, :, :],
+                    in_=recv_ps[:].rearrange("p g i c t -> p c g i t"),
+                )
+                nc.scalar.copy(
+                    out=send_t[:, :, first : first + BANK_GRAPHS, 0:NODES, :],
+                    in_=send_ps[:].rearrange("p g j c t -> p c g j t"),
                 )
             nc.vector.tensor_copy(out=send_t[:, :, :, NODES : 2 * NODES, :], in_=send_t[:, :, :, 0:NODES, :])
             return recv_rows, send_rows, recv_t, send_t
 
-        def quantise(h_half):
-            h_codes = packed.tile([P, HALF * P], U32, name="h_codes", align_bytes=64)
-            h_scales = packed.tile([P, HALF * P], U8, name="h_scales", align_bytes=64)
-            nc.vector.quantize_mx(
-                out=h_codes[:].bitcast(FP8X4),
-                scales=h_scales[:],
-                in_=h_half.rearrange("p q r t -> p (q r t)"),
-            )
-            return h_codes, h_scales
-
         ready = prepare(0)
 
-        ident_twice = const.tile([P, TILE_GRAPHS, 2 * NODES], F32)
-        ident_blocks = ident[:].rearrange("p (b j) -> p b j", j=NODES)
-        nc.vector.tensor_copy(out=ident_twice[:, :, 0:NODES], in_=ident_blocks)
-        nc.vector.tensor_copy(out=ident_twice[:, :, NODES : 2 * NODES], in_=ident_blocks)
+        ident_twice = const.tile([P, 2, P], F32)
+        nc.vector.tensor_copy(out=ident_twice[:, 0, :], in_=ident[:])
+        nc.vector.tensor_copy(out=ident_twice[:, 1, :], in_=ident[:])
+        ident_wide = ident_twice[:].rearrange("p two n -> p (two n)")
 
         w_raw = const.tile([P, PASSES, PACK, D], BF16)
         nc.sync.dma_start(out=w_raw[:], in_=mw2.rearrange("(c t p) d -> p c t d", c=PASSES, t=PACK, p=P))
@@ -124,58 +132,67 @@ def tile_graphdynamics_pa_t_kernel(tc, xi_p, xj_p, node_mask, mb1, mw2, mb2, out
         for q in range(NODES):
             nc.vector.tensor_copy(out=mask_rot[:, q, :, :], in_=mask_twice[:, :, q : q + NODES])
 
-        for rt in range(ROW_TILES):
+        for tile_index in range(TILES):
             recv_rows, send_rows, recv_t, send_t = ready
-            if rt + 1 < ROW_TILES:
-                ready = prepare(rt + 1)
+            if tile_index + 1 < TILES:
+                ready = prepare(tile_index + 1)
 
-            h_own = hidden.tile([P, PASSES, HALF, P, PACK], BF16, name="h_own", align_bytes=64)
-            for ql in range(HALF):
-                q = HALF + ql
+            h = hidden.tile([P, PASSES, NODES, TILE_GRAPHS, NODES, PACK], BF16, name="h", align_bytes=64)
+
+            for q in range(ROT_PE, NODES):
                 nc.vector.tensor_tensor(
-                    out=h_own[:, :, ql, :, :].rearrange("p c (b i) t -> p c b i t", i=NODES),
-                    in0=recv_t[:].rearrange("p c (b i) t -> p c b i t", i=NODES),
-                    in1=send_t[:, :, :, q : q + NODES, :],
-                    op=ADD,
+                    out=h[:, :, q, :, :, :], in0=recv_t[:], in1=send_t[:, :, :, q : q + NODES, :], op=ADD
                 )
-            own_flat = h_own[:].rearrange("p c q r t -> p (c q r t)")
-            nc.vector.tensor_scalar_max(out=own_flat, in0=own_flat, scalar1=0.0)
-            own_q = [quantise(h_own[:, c, :, :, :]) for c in range(PASSES)]
+            own = h[:, :, ROT_PE:NODES, :, :, :].rearrange("p c q b i t -> p c (q b i t)")
+            nc.vector.tensor_scalar_max(out=own, in0=own, scalar1=0.0)
 
-            summed_q = []
-            for c in range(PASSES):
-                h_sum = hidden.tile([P, HALF, P, PACK], BF16, name="h_sum", align_bytes=64, bufs=3)
-                for q in range(HALF):
-                    pair_ps = ps_pair.tile([P, PACK, P], F32, name="pair_ps", tag="pair")
-                    for t in range(PACK):
+            for q in range(ROT_PE):
+                for first in range(0, TILE_GRAPHS, BANK_GRAPHS):
+                    pair_ps = ps_pair.tile([P, BANK_GRAPHS, NODES, PASSES, PACK], F32, name="pair_ps", tag="pair")
+                    for g in range(BANK_GRAPHS):
+                        graph_ps = pair_ps[:, g, :, :, :].rearrange("p i c t -> p (i c t)")
                         nc.tensor.matmul(
-                            out=pair_ps[:, t, :], lhsT=recv_rows[:, pass_slice(c, t)], rhs=ident[:],
+                            out=graph_ps, lhsT=recv_rows[:, first + g, :], rhs=ident[:],
                             is_transpose=True, start=True, stop=False,
                         )
                         nc.tensor.matmul(
-                            out=pair_ps[:, t, :], lhsT=send_rows[:, pass_slice(c, t)],
-                            rhs=ident_twice[:, :, q : q + NODES],
+                            out=graph_ps, lhsT=send_rows[:, first + g, :],
+                            rhs=ident_wide[:, q * CHUNKS : q * CHUNKS + P],
                             is_transpose=True, start=False, stop=True,
                         )
                     nc.scalar.activation(
-                        out=h_sum[:, q, :, :], in_=pair_ps[:].rearrange("p t r -> p r t"), func=RELU
+                        out=h[:, :, q, first : first + BANK_GRAPHS, :, :],
+                        in_=pair_ps[:].rearrange("p g i c t -> p c g i t"),
+                        func=RELU,
                     )
-                summed_q.append(quantise(h_sum[:]))
+
+            codes = {}
+            for part in range(NODES // QUANT_ROTS):
+                for c in range(PASSES):
+                    h_codes = packed.tile([P, QUANT_ROTS * P], U32, name="h_codes", align_bytes=64)
+                    h_scales = packed.tile([P, QUANT_ROTS * P], U8, name="h_scales", align_bytes=64)
+                    nc.vector.quantize_mx(
+                        out=h_codes[:].bitcast(FP8X4),
+                        scales=h_scales[:],
+                        in_=h[:, c, part * QUANT_ROTS : (part + 1) * QUANT_ROTS, :, :, :].rearrange(
+                            "p q b i t -> p (q b i t)"
+                        ),
+                    )
+                    codes[(part, c)] = (h_codes, h_scales)
 
             out_ps = ps_out.tile([P, D], F32, name="out_ps")
-            banks = NODES // BANK_ROTS
-            for nb in range(banks):
-                operands = own_q if nb < banks // 2 else summed_q
-                first_rot = (HALF + nb * BANK_ROTS) % NODES
-                cols = slice((first_rot % HALF) * P, (first_rot % HALF + BANK_ROTS) * P)
+            for first_rot in range(0, NODES, BANK_ROTS):
+                part = first_rot // QUANT_ROTS
+                cols = slice((first_rot % QUANT_ROTS) * P, (first_rot % QUANT_ROTS + BANK_ROTS) * P)
                 acc = ps_acc.tile([P, BANK_ROTS, P], F32, name="acc")
                 for c in range(PASSES):
+                    h_codes, h_scales = codes[(part, c)]
                     nc.tensor.matmul_mx(
                         out=acc[:].rearrange("d q r -> d (q r)"),
                         lhsT=w_codes[:, c * D : (c + 1) * D].bitcast(FP8X4),
                         lhsT_scale=w_scales[:, c * D : (c + 1) * D],
-                        rhs=operands[c][0][:, cols].bitcast(FP8X4),
-                        rhs_scale=operands[c][1][:, cols],
+                        rhs=h_codes[:, cols].bitcast(FP8X4),
+                        rhs_scale=h_scales[:, cols],
                         start=(c == 0),
                         stop=(c == PASSES - 1),
                     )
@@ -185,15 +202,19 @@ def tile_graphdynamics_pa_t_kernel(tc, xi_p, xj_p, node_mask, mb1, mw2, mb2, out
                     out=msg[:],
                     in0=msg[:],
                     in1=mask_rot[
-                        :, first_rot : first_rot + BANK_ROTS, rt * TILE_GRAPHS : (rt + 1) * TILE_GRAPHS, :
+                        :,
+                        first_rot : first_rot + BANK_ROTS,
+                        tile_index * TILE_GRAPHS : (tile_index + 1) * TILE_GRAPHS,
+                        :,
                     ].rearrange("p q b i -> p q (b i)"),
                     op=MULT,
                 )
                 for ql in range(BANK_ROTS):
+                    q = first_rot + ql
                     nc.tensor.matmul(
                         out=out_ps[:], lhsT=msg[:, ql, :], rhs=ident[:], is_transpose=True,
-                        start=(nb == 0 and ql == 0), stop=(nb == banks - 1 and ql == BANK_ROTS - 1),
+                        start=(q == 0), stop=(q == NODES - 1),
                     )
             out_sb = tail.tile([P, D], F32, name="out_sb")
             nc.scalar.copy(out=out_sb[:], in_=out_ps[:])
-            nc.sync.dma_start(out=out_rows[rt * P : (rt + 1) * P, :], in_=out_sb[:])
+            nc.sync.dma_start(out=out_rows[tile_index * P : (tile_index + 1) * P, :], in_=out_sb[:])

@@ -17,95 +17,203 @@ P = 128
 PACK = 4
 K_PASS = P * PACK
 PASSES = H // K_PASS
-CHUNKS = PASSES * PACK
-TILE_GRAPHS = 8
+TILE_GRAPHS = P // NODES
 TILES = GRAPHS // TILE_GRAPHS
-N_TILE = 512
-BANK_ROTS = N_TILE // P
-BANK_GRAPHS = N_TILE // P
-BANK_NODES = BANK_GRAPHS * NODES
-QUANT_ROTS = 8
-ROT_PE = 9
+ROTS = 4
+GROUPS = NODES // ROTS
+N_TILE = ROTS * P
+STEPS = 4
+MASK_PITCH = NODES + 1
+MASK_LEN = NODES - ROTS + (ROTS - 1) * MASK_PITCH + NODES + 1
 
 FLOPS = 2 * GRAPHS * NODES * NODES * H * D
 
 
 def tile_graphdynamics_pa_t_kernel(tc, xi_p, xj_p, node_mask, mb1, mw2, mb2, out):
     nc = tc.nc
-    xi_chunks = xi_p.rearrange("b i (s k) -> (i s) b k", s=CHUNKS)
-    xj_chunks = xj_p.rearrange("b j (s k) -> (j s) b k", s=CHUNKS)
+    xi_rows = xi_p.rearrange("b i k -> (b i) k")
+    xj_rows = xj_p.rearrange("b j k -> (b j) k")
     out_rows = out.rearrange("b i d -> (b i) d")
 
     with ExitStack() as ctx:
         const = ctx.enter_context(tc.tile_pool(name="const", bufs=1))
-        rows = ctx.enter_context(tc.tile_pool(name="rows", bufs=3))
+        rows = ctx.enter_context(tc.tile_pool(name="rows", bufs=TILES))
         prep = ctx.enter_context(tc.tile_pool(name="prep", bufs=2))
-        hidden = ctx.enter_context(tc.tile_pool(name="hidden", bufs=2))
-        packed = ctx.enter_context(tc.tile_pool(name="packed", bufs=8))
-        tail = ctx.enter_context(tc.tile_pool(name="tail", bufs=3))
+        hidden = ctx.enter_context(tc.tile_pool(name="hidden", bufs=6))
+        packed = ctx.enter_context(tc.tile_pool(name="packed", bufs=6))
+        tail = ctx.enter_context(tc.tile_pool(name="tail", bufs=8))
         ps_pair = ctx.enter_context(tc.psum_pool(name="ps_pair", bufs=4))
         ps_acc = ctx.enter_context(tc.psum_pool(name="ps_acc", bufs=2))
         ps_out = ctx.enter_context(tc.psum_pool(name="ps_out", bufs=2))
+        ctx.enter_context(tc.manual_schedule())
+
+        mb1_all = const.tile([P, H], BF16)
+        nc.scalar.dma_start(out=mb1_all[:], in_=mb1.partition_broadcast(P))
+        xi_sb = []
+        xj_sb = []
+        for r in range(TILES):
+            xi_tile = rows.tile([P, H], BF16, name="xi_tile")
+            nc.sync.dma_start(out=xi_tile[:], in_=xi_rows[r * P : (r + 1) * P, :])
+            xj_tile = rows.tile([P, H], BF16, name="xj_tile")
+            nc.sync.dma_start(out=xj_tile[:], in_=xj_rows[r * P : (r + 1) * P, :])
+            xi_sb.append(xi_tile)
+            xj_sb.append(xj_tile)
+        mask_all = const.tile([P, GRAPHS, NODES], BF16)
+        nc.scalar.dma_start(
+            out=mask_all[:].rearrange("p b j -> p (b j)"),
+            in_=node_mask.rearrange("b j -> (b j)").partition_broadcast(P),
+        )
+        w_raw = const.tile([P, PASSES, PACK, D], BF16)
+        nc.scalar.dma_start(out=w_raw[:], in_=mw2.rearrange("(c t p) d -> p c t d", c=PASSES, t=PACK, p=P))
+        mb2_bf = const.tile([P, 1], BF16)
+        with nc.allow_non_contiguous_dma(reason="mb2: one value a partition, 128 values in all"):
+            nc.scalar.dma_start(out=mb2_bf[:], in_=mb2.unsqueeze(1))
 
         ident = const.tile([P, P], F32)
         make_identity(nc, ident[:])
-        mb1_rows = const.tile([P, P], BF16)
-        for node in range(NODES):
-            nc.scalar.dma_start(
-                out=mb1_rows[node * CHUNKS : (node + 1) * CHUNKS, :],
-                in_=mb1.rearrange("(s k) -> s k", s=CHUNKS),
-            )
 
-        def prepare(tile_index):
-            graphs = slice(tile_index * TILE_GRAPHS, (tile_index + 1) * TILE_GRAPHS)
-            xi_tile = rows.tile([P, TILE_GRAPHS, P], BF16, name="xi_tile")
-            nc.sync.dma_start(out=xi_tile[:], in_=xi_chunks[:, graphs, :])
-            xj_tile = rows.tile([P, TILE_GRAPHS, P], BF16, name="xj_tile")
-            nc.sync.dma_start(out=xj_tile[:], in_=xj_chunks[:, graphs, :])
-            recv_rows = prep.tile([P, TILE_GRAPHS, P], F32, name="recv_rows")
-            nc.vector.tensor_tensor(
-                out=recv_rows[:],
-                in0=xi_tile[:],
-                in1=mb1_rows[:].unsqueeze(1).to_broadcast([P, TILE_GRAPHS, P]),
-                op=ADD,
-            )
-            send_rows = prep.tile([P, TILE_GRAPHS, P], F32, name="send_rows")
-            nc.scalar.copy(out=send_rows[:], in_=xj_tile[:])
+        rows32 = {}
+        turned = {}
+        h_tiles = {}
+        codes = {}
+        msgs = {}
+        sums = {}
+
+        def pass_slice(c, t):
+            return slice(c * K_PASS + t * P, c * K_PASS + (t + 1) * P)
+
+        def start_tile(r):
+            recv_rows = prep.tile([P, H], F32, name="recv_rows")
+            nc.vector.tensor_tensor(out=recv_rows[:], in0=xi_sb[r][:], in1=mb1_all[:], op=ADD)
+            send_rows = prep.tile([P, H], F32, name="send_rows")
+            nc.scalar.copy(out=send_rows[:], in_=xj_sb[r][:])
+            rows32[r] = (recv_rows, send_rows)
+
+        def turn_tile(r):
+            recv_rows, send_rows = rows32[r]
             recv_t = prep.tile([P, PASSES, TILE_GRAPHS, NODES, PACK], F32, name="recv_t")
             send_t = prep.tile([P, PASSES, TILE_GRAPHS, 2 * NODES, PACK], BF16, name="send_t")
-            for first in range(0, TILE_GRAPHS, BANK_GRAPHS):
-                recv_ps = ps_pair.tile([P, BANK_GRAPHS, NODES, PASSES, PACK], F32, name="recv_ps", tag="pair")
-                send_ps = ps_pair.tile([P, BANK_GRAPHS, NODES, PASSES, PACK], F32, name="send_ps", tag="pair")
-                for g in range(BANK_GRAPHS):
-                    nc.tensor.transpose(
-                        recv_ps[:, g, :, :, :].rearrange("p i c t -> p (i c t)"), recv_rows[:, first + g, :], ident[:]
-                    )
-                for g in range(BANK_GRAPHS):
-                    nc.tensor.transpose(
-                        send_ps[:, g, :, :, :].rearrange("p j c t -> p (j c t)"), send_rows[:, first + g, :], ident[:]
-                    )
+            for c in range(PASSES):
+                recv_ps = ps_pair.tile([P, PACK, P], F32, name="recv_ps", tag="pair")
+                for t in range(PACK):
+                    nc.tensor.transpose(recv_ps[:, t, :], recv_rows[:, pass_slice(c, t)], ident[:])
                 nc.scalar.copy(
-                    out=recv_t[:, :, first : first + BANK_GRAPHS, :, :],
-                    in_=recv_ps[:].rearrange("p g i c t -> p c g i t"),
+                    out=recv_t[:, c, :, :, :], in_=recv_ps[:].rearrange("p t (b i) -> p b i t", i=NODES)
                 )
+                send_ps = ps_pair.tile([P, PACK, P], F32, name="send_ps", tag="pair")
+                for t in range(PACK):
+                    nc.tensor.transpose(send_ps[:, t, :], send_rows[:, pass_slice(c, t)], ident[:])
                 nc.scalar.copy(
-                    out=send_t[:, :, first : first + BANK_GRAPHS, 0:NODES, :],
-                    in_=send_ps[:].rearrange("p g j c t -> p c g j t"),
+                    out=send_t[:, c, :, 0:NODES, :], in_=send_ps[:].rearrange("p t (b j) -> p b j t", j=NODES)
                 )
+            turned[r] = (recv_t, send_t)
+
+        def double_senders(r):
+            send_t = turned[r][1]
             nc.vector.tensor_copy(out=send_t[:, :, :, NODES : 2 * NODES, :], in_=send_t[:, :, :, 0:NODES, :])
-            return recv_rows, send_rows, recv_t, send_t
 
-        ready = prepare(0)
+        def new_h(r, group):
+            h_tiles[(r, group)] = hidden.tile([P, PASSES, ROTS, P, PACK], BF16, name="h", align_bytes=64)
 
-        ident_twice = const.tile([P, 2, P], F32)
-        nc.vector.tensor_copy(out=ident_twice[:, 0, :], in_=ident[:])
-        nc.vector.tensor_copy(out=ident_twice[:, 1, :], in_=ident[:])
-        ident_wide = ident_twice[:].rearrange("p two n -> p (two n)")
+        def psum_sums(r, group, c):
+            recv_rows, send_rows = rows32[r]
+            for ql in range(ROTS):
+                q = group * ROTS + ql
+                pair_ps = ps_pair.tile([P, PACK, P], F32, name="pair_ps", tag="pair")
+                for t in range(PACK):
+                    nc.tensor.matmul(
+                        out=pair_ps[:, t, :], lhsT=recv_rows[:, pass_slice(c, t)], rhs=ident[:],
+                        is_transpose=True, start=True, stop=False,
+                    )
+                    nc.tensor.matmul(
+                        out=pair_ps[:, t, :], lhsT=send_rows[:, pass_slice(c, t)],
+                        rhs=ident_twice[:, :, q : q + NODES],
+                        is_transpose=True, start=False, stop=True,
+                    )
+                nc.scalar.activation(
+                    out=h_tiles[(r, group)][:, c, ql, :, :], in_=pair_ps[:].rearrange("p t r -> p r t"), func=RELU
+                )
 
-        w_raw = const.tile([P, PASSES, PACK, D], BF16)
-        nc.sync.dma_start(out=w_raw[:], in_=mw2.rearrange("(c t p) d -> p c t d", c=PASSES, t=PACK, p=P))
+        def own_sum(r, group, ql):
+            recv_t, send_t = turned[r]
+            q = group * ROTS + ql
+            nc.vector.tensor_tensor(
+                out=h_tiles[(r, group)][:, :, ql, :, :].rearrange("p c (b i) t -> p c b i t", i=NODES),
+                in0=recv_t[:],
+                in1=send_t[:, :, :, q : q + NODES, :],
+                op=ADD,
+            )
+
+        def own_relu(r, group):
+            flat = h_tiles[(r, group)][:].rearrange("p c q r t -> p (c q r t)")
+            nc.vector.tensor_scalar_max(out=flat, in0=flat, scalar1=0.0)
+
+        def quantise(r, group):
+            h_codes = packed.tile([P, PASSES, N_TILE], U32, name="h_codes", align_bytes=64)
+            h_scales = packed.tile([P, PASSES, N_TILE], U8, name="h_scales", align_bytes=64)
+            nc.vector.quantize_mx(
+                out=h_codes[:].rearrange("p c n -> p (c n)").bitcast(FP8X4),
+                scales=h_scales[:].rearrange("p c n -> p (c n)"),
+                in_=h_tiles[(r, group)][:].rearrange("p c q r t -> p (c q r t)"),
+            )
+            codes[(r, group)] = (h_codes, h_scales)
+
+        def multiply(r, group):
+            h_codes, h_scales = codes[(r, group)]
+            acc = ps_acc.tile([P, N_TILE], F32, name="acc")
+            for c in range(PASSES):
+                nc.tensor.matmul_mx(
+                    out=acc[:],
+                    lhsT=w_codes[:, c * D : (c + 1) * D].bitcast(FP8X4),
+                    lhsT_scale=w_scales[:, c * D : (c + 1) * D],
+                    rhs=h_codes[:, c, :].bitcast(FP8X4),
+                    rhs_scale=h_scales[:, c, :],
+                    start=(c == 0),
+                    stop=(c == PASSES - 1),
+                )
+            msg = tail.tile([P, ROTS, TILE_GRAPHS, NODES], F32, name="msg")
+            nc.scalar.activation(
+                out=msg[:].rearrange("d q b i -> d (q b i)"), in_=acc[:], func=RELU, bias=mb2_col[:], scale=1.0
+            )
+            msgs[(r, group)] = msg
+
+        def mask_msgs(r, group):
+            msg = msgs[(r, group)]
+            first = group * ROTS
+            windows = mask_rep[:, r * TILE_GRAPHS : (r + 1) * TILE_GRAPHS, first : first + ROTS * MASK_PITCH]
+            nc.vector.tensor_tensor(
+                out=msg[:],
+                in0=msg[:],
+                in1=windows.rearrange("p b (q w) -> p q b w", w=MASK_PITCH)[:, :, :, 0:NODES],
+                op=MULT,
+            )
+
+        def add_up(r, group, first, last):
+            if first:
+                sums[r] = ps_out.tile([P, D], F32, name="out_ps")
+            msg = msgs[(r, group)]
+            for ql in range(ROTS):
+                nc.tensor.matmul(
+                    out=sums[r][:], lhsT=msg[:, ql, :, :].rearrange("d b i -> d (b i)"), rhs=ident[:],
+                    is_transpose=True, start=(first and ql == 0), stop=(last and ql == ROTS - 1),
+                )
+
+        def finish(r):
+            out_sb = tail.tile([P, D], F32, name="out_sb", bufs=2)
+            nc.scalar.copy(out=out_sb[:], in_=sums[r][:])
+            nc.sync.dma_start(out=out_rows[r * P : (r + 1) * P, :], in_=out_sb[:])
+
+        start_tile(0)
+        ident_twice = const.tile([P, TILE_GRAPHS, 2 * NODES], F32)
+        ident_blocks = ident[:].rearrange("p (b j) -> p b j", j=NODES)
+        nc.vector.tensor_copy(out=ident_twice[:, :, 0:NODES], in_=ident_blocks)
+        nc.vector.tensor_copy(out=ident_twice[:, :, NODES : 2 * NODES], in_=ident_blocks)
+        turn_tile(0)
+
         w_grouped = const.tile([P, PASSES, D, PACK], BF16, align_bytes=64)
         nc.vector.tensor_copy(out=w_grouped[:], in_=w_raw[:].rearrange("p c t d -> p c d t"))
+        mb2_col = const.tile([P, 1], F32)
+        nc.vector.tensor_copy(out=mb2_col[:], in_=mb2_bf[:])
         w_codes = const.tile([P, PASSES * D], U32, align_bytes=64)
         w_scales = const.tile([P, PASSES * D], U8, align_bytes=64)
         nc.vector.quantize_mx(
@@ -113,108 +221,60 @@ def tile_graphdynamics_pa_t_kernel(tc, xi_p, xj_p, node_mask, mb1, mw2, mb2, out
             scales=w_scales[:],
             in_=w_grouped[:].rearrange("p c d t -> p (c d t)"),
         )
+        mask_rep = const.tile([P, GRAPHS, MASK_LEN], BF16)
+        for period in range(MASK_LEN // NODES):
+            nc.vector.tensor_copy(out=mask_rep[:, :, period * NODES : (period + 1) * NODES], in_=mask_all[:])
+        double_senders(0)
 
-        mb2_bf = const.tile([P, 1], BF16)
-        with nc.allow_non_contiguous_dma(reason="mb2: one value a partition, 128 values in all"):
-            nc.scalar.dma_start(out=mb2_bf[:], in_=mb2.unsqueeze(1))
-        mb2_col = const.tile([P, 1], F32)
-        nc.vector.tensor_copy(out=mb2_col[:], in_=mb2_bf[:])
+        def pair_formed_at(step):
+            r, k = divmod(step, STEPS)
+            if 0 <= r < TILES:
+                return r, (k // 2, GROUPS // 2 + k // 2)
+            return None
 
-        mask_all = const.tile([P, GRAPHS, NODES], BF16)
-        nc.scalar.dma_start(
-            out=mask_all[:].rearrange("p b j -> p (b j)"),
-            in_=node_mask.rearrange("b j -> (b j)").partition_broadcast(P),
-        )
-        mask_twice = const.tile([P, GRAPHS, 2 * NODES], BF16)
-        nc.vector.tensor_copy(out=mask_twice[:, :, 0:NODES], in_=mask_all[:])
-        nc.vector.tensor_copy(out=mask_twice[:, :, NODES : 2 * NODES], in_=mask_all[:])
-        mask_rot = const.tile([P, NODES, GRAPHS, NODES], BF16)
-        for q in range(NODES):
-            nc.vector.tensor_copy(out=mask_rot[:, q, :, :], in_=mask_twice[:, :, q : q + NODES])
+        for step in range(STEPS * TILES + 5):
+            r, k = divmod(step, STEPS)
+            odd = k % 2
+            forming = r < TILES
+            psum_group, own_group = k // 2, GROUPS // 2 + k // 2
+            done = pair_formed_at(step - 1) if not odd else pair_formed_at(step - 4)
 
-        for tile_index in range(TILES):
-            recv_rows, send_rows, recv_t, send_t = ready
-            if tile_index + 1 < TILES:
-                ready = prepare(tile_index + 1)
+            if forming:
+                if not odd:
+                    new_h(r, psum_group)
+                    new_h(r, own_group)
+                psum_sums(r, psum_group, odd)
+                own_sum(r, own_group, 2 * odd)
+            if done and not odd:
+                quantise(done[0], done[1][0])
+            if forming:
+                own_sum(r, own_group, 2 * odd + 1)
+            if done and not odd:
+                quantise(done[0], done[1][1])
+            if done and odd:
+                mask_msgs(done[0], done[1][0])
+                mask_msgs(done[0], done[1][1])
+            if forming and odd:
+                own_relu(r, own_group)
 
-            h = hidden.tile([P, PASSES, NODES, TILE_GRAPHS, NODES, PACK], BF16, name="h", align_bytes=64)
+            if odd:
+                ready = pair_formed_at(step - 2)
+                if ready:
+                    multiply(ready[0], ready[1][0])
+                    multiply(ready[0], ready[1][1])
+            else:
+                masked = pair_formed_at(step - 5)
+                if masked:
+                    first_pair = masked[1][0] == 0
+                    add_up(masked[0], masked[1][0], first_pair, False)
+                    add_up(masked[0], masked[1][1], False, not first_pair)
+                    if not first_pair:
+                        finish(masked[0])
 
-            for q in range(ROT_PE, NODES):
-                nc.vector.tensor_tensor(
-                    out=h[:, :, q, :, :, :], in0=recv_t[:], in1=send_t[:, :, :, q : q + NODES, :], op=ADD
-                )
-            own = h[:, :, ROT_PE:NODES, :, :, :].rearrange("p c q b i t -> p c (q b i t)")
-            nc.vector.tensor_scalar_max(out=own, in0=own, scalar1=0.0)
-
-            for q in range(ROT_PE):
-                for first in range(0, TILE_GRAPHS, BANK_GRAPHS):
-                    pair_ps = ps_pair.tile([P, BANK_GRAPHS, NODES, PASSES, PACK], F32, name="pair_ps", tag="pair")
-                    for g in range(BANK_GRAPHS):
-                        graph_ps = pair_ps[:, g, :, :, :].rearrange("p i c t -> p (i c t)")
-                        nc.tensor.matmul(
-                            out=graph_ps, lhsT=recv_rows[:, first + g, :], rhs=ident[:],
-                            is_transpose=True, start=True, stop=False,
-                        )
-                        nc.tensor.matmul(
-                            out=graph_ps, lhsT=send_rows[:, first + g, :],
-                            rhs=ident_wide[:, q * CHUNKS : q * CHUNKS + P],
-                            is_transpose=True, start=False, stop=True,
-                        )
-                    nc.scalar.activation(
-                        out=h[:, :, q, first : first + BANK_GRAPHS, :, :],
-                        in_=pair_ps[:].rearrange("p g i c t -> p c g i t"),
-                        func=RELU,
-                    )
-
-            codes = {}
-            for part in range(NODES // QUANT_ROTS):
-                for c in range(PASSES):
-                    h_codes = packed.tile([P, QUANT_ROTS * P], U32, name="h_codes", align_bytes=64)
-                    h_scales = packed.tile([P, QUANT_ROTS * P], U8, name="h_scales", align_bytes=64)
-                    nc.vector.quantize_mx(
-                        out=h_codes[:].bitcast(FP8X4),
-                        scales=h_scales[:],
-                        in_=h[:, c, part * QUANT_ROTS : (part + 1) * QUANT_ROTS, :, :, :].rearrange(
-                            "p q b i t -> p (q b i t)"
-                        ),
-                    )
-                    codes[(part, c)] = (h_codes, h_scales)
-
-            out_ps = ps_out.tile([P, D], F32, name="out_ps")
-            for first_rot in range(0, NODES, BANK_ROTS):
-                part = first_rot // QUANT_ROTS
-                cols = slice((first_rot % QUANT_ROTS) * P, (first_rot % QUANT_ROTS + BANK_ROTS) * P)
-                acc = ps_acc.tile([P, BANK_ROTS, P], F32, name="acc")
-                for c in range(PASSES):
-                    h_codes, h_scales = codes[(part, c)]
-                    nc.tensor.matmul_mx(
-                        out=acc[:].rearrange("d q r -> d (q r)"),
-                        lhsT=w_codes[:, c * D : (c + 1) * D].bitcast(FP8X4),
-                        lhsT_scale=w_scales[:, c * D : (c + 1) * D],
-                        rhs=h_codes[:, cols].bitcast(FP8X4),
-                        rhs_scale=h_scales[:, cols],
-                        start=(c == 0),
-                        stop=(c == PASSES - 1),
-                    )
-                msg = tail.tile([P, BANK_ROTS, P], F32, name="msg")
-                nc.scalar.activation(out=msg[:], in_=acc[:], func=RELU, bias=mb2_col[:], scale=1.0)
-                nc.vector.tensor_tensor(
-                    out=msg[:],
-                    in0=msg[:],
-                    in1=mask_rot[
-                        :,
-                        first_rot : first_rot + BANK_ROTS,
-                        tile_index * TILE_GRAPHS : (tile_index + 1) * TILE_GRAPHS,
-                        :,
-                    ].rearrange("p q b i -> p q (b i)"),
-                    op=MULT,
-                )
-                for ql in range(BANK_ROTS):
-                    q = first_rot + ql
-                    nc.tensor.matmul(
-                        out=out_ps[:], lhsT=msg[:, ql, :], rhs=ident[:], is_transpose=True,
-                        start=(q == 0), stop=(q == NODES - 1),
-                    )
-            out_sb = tail.tile([P, D], F32, name="out_sb")
-            nc.scalar.copy(out=out_sb[:], in_=out_ps[:])
-            nc.sync.dma_start(out=out_rows[tile_index * P : (tile_index + 1) * P, :], in_=out_sb[:])
+            if r + 1 < TILES:
+                if k == 0:
+                    start_tile(r + 1)
+                if k == 2:
+                    turn_tile(r + 1)
+                if k == 3:
+                    double_senders(r + 1)

@@ -23,6 +23,7 @@ ROTS = 4
 GROUPS = NODES // ROTS
 N_TILE = ROTS * P
 STEPS = 4
+EXTRA = 1
 MASK_PITCH = NODES + 1
 MASK_LEN = NODES - ROTS + (ROTS - 1) * MASK_PITCH + NODES + 1
 
@@ -103,21 +104,19 @@ def tile_graphdynamics_pa_t_kernel(tc, xi_p, xj_p, node_mask, mb1, mw2, mb2, out
                 send_ps = ps_pair.tile([P, PACK, P], F32, name="send_ps", tag="pair")
                 for t in range(PACK):
                     nc.tensor.transpose(send_ps[:, t, :], send_rows[:, pass_slice(c, t)], ident[:])
-                nc.scalar.copy(
-                    out=send_t[:, c, :, 0:NODES, :], in_=send_ps[:].rearrange("p t (b j) -> p b j t", j=NODES)
-                )
+                for copy in range(2):
+                    nc.scalar.copy(
+                        out=send_t[:, c, :, copy * NODES : (copy + 1) * NODES, :],
+                        in_=send_ps[:].rearrange("p t (b j) -> p b j t", j=NODES),
+                    )
             turned[r] = (recv_t, send_t)
-
-        def double_senders(r):
-            send_t = turned[r][1]
-            nc.vector.tensor_copy(out=send_t[:, :, :, NODES : 2 * NODES, :], in_=send_t[:, :, :, 0:NODES, :])
 
         def new_h(r, group):
             h_tiles[(r, group)] = hidden.tile([P, PASSES, ROTS, P, PACK], BF16, name="h", align_bytes=64)
 
-        def psum_sums(r, group, c):
+        def psum_sums(r, group, c, rotations):
             recv_rows, send_rows = rows32[r]
-            for ql in range(ROTS):
+            for ql in range(rotations):
                 q = group * ROTS + ql
                 pair_ps = ps_pair.tile([P, PACK, P], F32, name="pair_ps", tag="pair")
                 for t in range(PACK):
@@ -144,9 +143,9 @@ def tile_graphdynamics_pa_t_kernel(tc, xi_p, xj_p, node_mask, mb1, mw2, mb2, out
                 op=ADD,
             )
 
-        def own_relu(r, group):
-            flat = h_tiles[(r, group)][:].rearrange("p c q r t -> p (c q r t)")
-            nc.vector.tensor_scalar_max(out=flat, in0=flat, scalar1=0.0)
+        def own_relu(r, group, first_own):
+            own = h_tiles[(r, group)][:, :, first_own:ROTS, :, :].rearrange("p c q r t -> p c (q r t)")
+            nc.vector.tensor_scalar_max(out=own, in0=own, scalar1=0.0)
 
         def quantise(r, group):
             h_codes = packed.tile([P, PASSES, N_TILE], U32, name="h_codes", align_bytes=64)
@@ -224,7 +223,6 @@ def tile_graphdynamics_pa_t_kernel(tc, xi_p, xj_p, node_mask, mb1, mw2, mb2, out
         mask_rep = const.tile([P, GRAPHS, MASK_LEN], BF16)
         for period in range(MASK_LEN // NODES):
             nc.vector.tensor_copy(out=mask_rep[:, :, period * NODES : (period + 1) * NODES], in_=mask_all[:])
-        double_senders(0)
 
         def pair_formed_at(step):
             r, k = divmod(step, STEPS)
@@ -239,15 +237,18 @@ def tile_graphdynamics_pa_t_kernel(tc, xi_p, xj_p, node_mask, mb1, mw2, mb2, out
             psum_group, own_group = k // 2, GROUPS // 2 + k // 2
             done = pair_formed_at(step - 1) if not odd else pair_formed_at(step - 4)
 
+            first_own = EXTRA if own_group == GROUPS // 2 else 0
             if forming:
                 if not odd:
                     new_h(r, psum_group)
                     new_h(r, own_group)
-                psum_sums(r, psum_group, odd)
-                own_sum(r, own_group, 2 * odd)
+                psum_sums(r, psum_group, odd, ROTS)
+                psum_sums(r, own_group, odd, first_own)
+                if 2 * odd >= first_own:
+                    own_sum(r, own_group, 2 * odd)
             if done and not odd:
                 quantise(done[0], done[1][0])
-            if forming:
+            if forming and 2 * odd + 1 >= first_own:
                 own_sum(r, own_group, 2 * odd + 1)
             if done and not odd:
                 quantise(done[0], done[1][1])
@@ -255,7 +256,7 @@ def tile_graphdynamics_pa_t_kernel(tc, xi_p, xj_p, node_mask, mb1, mw2, mb2, out
                 mask_msgs(done[0], done[1][0])
                 mask_msgs(done[0], done[1][1])
             if forming and odd:
-                own_relu(r, own_group)
+                own_relu(r, own_group, first_own)
 
             if odd:
                 ready = pair_formed_at(step - 2)
@@ -276,5 +277,3 @@ def tile_graphdynamics_pa_t_kernel(tc, xi_p, xj_p, node_mask, mb1, mw2, mb2, out
                     start_tile(r + 1)
                 if k == 2:
                     turn_tile(r + 1)
-                if k == 3:
-                    double_senders(r + 1)

@@ -11,6 +11,7 @@ FP8X4 = mybir.dt.float8_e4m3fn_x4
 ADD = mybir.AluOpType.add
 MULT = mybir.AluOpType.mult
 RELU = mybir.ActivationFunctionType.Relu
+IDENTITY = mybir.ActivationFunctionType.Identity
 
 GRAPHS, NODES, D, H = 64, 16, 128, 1024
 P = 128
@@ -22,10 +23,7 @@ TILES = GRAPHS // TILE_GRAPHS
 ROTS = 4
 GROUPS = NODES // ROTS
 N_TILE = ROTS * P
-STEPS = 4
-EXTRA = 1
-MASK_PITCH = NODES + 1
-MASK_LEN = NODES - ROTS + (ROTS - 1) * MASK_PITCH + NODES + 1
+MASKED = 2.0**126
 
 FLOPS = 2 * GRAPHS * NODES * NODES * H * D
 
@@ -40,129 +38,171 @@ def tile_graphdynamics_pa_t_kernel(tc, xi_p, xj_p, node_mask, mb1, mw2, mb2, out
         const = ctx.enter_context(tc.tile_pool(name="const", bufs=1))
         rows = ctx.enter_context(tc.tile_pool(name="rows", bufs=TILES))
         prep = ctx.enter_context(tc.tile_pool(name="prep", bufs=2))
-        hidden = ctx.enter_context(tc.tile_pool(name="hidden", bufs=6))
-        packed = ctx.enter_context(tc.tile_pool(name="packed", bufs=6))
-        tail = ctx.enter_context(tc.tile_pool(name="tail", bufs=8))
+        hidden = ctx.enter_context(tc.tile_pool(name="hidden", bufs=4))
+        packed = ctx.enter_context(tc.tile_pool(name="packed", bufs=4))
+        tail = ctx.enter_context(tc.tile_pool(name="tail", bufs=4))
         ps_pair = ctx.enter_context(tc.psum_pool(name="ps_pair", bufs=4))
-        ps_acc = ctx.enter_context(tc.psum_pool(name="ps_acc", bufs=2))
-        ps_out = ctx.enter_context(tc.psum_pool(name="ps_out", bufs=2))
+        ps_recv = ctx.enter_context(tc.psum_pool(name="ps_recv", bufs=2))
+        ps_acc = ctx.enter_context(tc.psum_pool(name="ps_acc", bufs=1))
+        ps_out = ctx.enter_context(tc.psum_pool(name="ps_out", bufs=1))
         ctx.enter_context(tc.manual_schedule())
 
-        mb1_all = const.tile([P, H], BF16)
-        nc.scalar.dma_start(out=mb1_all[:], in_=mb1.partition_broadcast(P))
+        vec_row = const.tile([P, H + D], BF16)
+        nc.vector.memset(vec_row[:], 0.0)
+        nc.scalar.dma_start(out=vec_row[0:1, 0:H], in_=mb1.unsqueeze(0))
+        nc.scalar.dma_start(out=vec_row[0:1, H : H + D], in_=mb2.unsqueeze(0))
+        mask_first = const.tile([P, 1], BF16)
+        mask_rest = const.tile([P, TILES - 1], BF16)
+        mb2_bf = const.tile([P, 1], BF16)
+        w_raw = const.tile([P, PASSES, PACK, D], BF16)
+        with nc.allow_non_contiguous_dma(reason="vectors with one value a partition"):
+            nc.scalar.dma_start(
+                out=mask_first[:], in_=node_mask[0:TILE_GRAPHS, :].rearrange("b j -> (b j)").unsqueeze(1)
+            )
+            nc.scalar.dma_start(out=w_raw[:], in_=mw2.rearrange("(c t p) d -> p c t d", c=PASSES, t=PACK, p=P))
+            nc.scalar.dma_start(
+                out=mask_rest[:],
+                in_=node_mask[TILE_GRAPHS:GRAPHS, :].rearrange("(r b) j -> (b j) r", b=TILE_GRAPHS),
+            )
+            nc.scalar.dma_start(out=mb2_bf[:], in_=mb2.unsqueeze(1))
         xi_sb = []
         xj_sb = []
         for r in range(TILES):
-            xi_tile = rows.tile([P, H], BF16, name="xi_tile")
-            nc.sync.dma_start(out=xi_tile[:], in_=xi_rows[r * P : (r + 1) * P, :])
             xj_tile = rows.tile([P, H], BF16, name="xj_tile")
-            nc.sync.dma_start(out=xj_tile[:], in_=xj_rows[r * P : (r + 1) * P, :])
+            xi_tile = rows.tile([P, H], BF16, name="xi_tile")
+            pieces = PASSES if r == 0 else 1
+            for piece in range(pieces):
+                cols = slice(piece * H // pieces, (piece + 1) * H // pieces)
+                nc.sync.dma_start(out=xj_tile[:, cols], in_=xj_rows[r * P : (r + 1) * P, cols])
+                nc.sync.dma_start(out=xi_tile[:, cols], in_=xi_rows[r * P : (r + 1) * P, cols])
             xi_sb.append(xi_tile)
             xj_sb.append(xj_tile)
-        mask_all = const.tile([P, GRAPHS, NODES], BF16)
-        nc.scalar.dma_start(
-            out=mask_all[:].rearrange("p b j -> p (b j)"),
-            in_=node_mask.rearrange("b j -> (b j)").partition_broadcast(P),
-        )
-        w_raw = const.tile([P, PASSES, PACK, D], BF16)
-        nc.scalar.dma_start(out=w_raw[:], in_=mw2.rearrange("(c t p) d -> p c t d", c=PASSES, t=PACK, p=P))
-        mb2_bf = const.tile([P, 1], BF16)
-        with nc.allow_non_contiguous_dma(reason="mb2: one value a partition, 128 values in all"):
-            nc.scalar.dma_start(out=mb2_bf[:], in_=mb2.unsqueeze(1))
 
         ident = const.tile([P, P], F32)
         make_identity(nc, ident[:])
+        ident_blocks = ident[:].rearrange("p (b j) -> p b j", j=NODES)
+        ones = const.tile([P, P], BF16)
+        nc.vector.memset(ones[:], 1.0)
+        ident_bf = const.tile([P, P], BF16)
+        nc.vector.tensor_copy(out=ident_bf[:], in_=ident[:])
+        perms = const.tile([P, NODES, TILE_GRAPHS, NODES], F32)
+        for q in range(NODES):
+            nc.vector.tensor_copy(out=perms[:, q, :, 0 : NODES - q], in_=ident_blocks[:, :, q:NODES])
+            if q:
+                nc.vector.tensor_copy(out=perms[:, q, :, NODES - q : NODES], in_=ident_blocks[:, :, 0:q])
+        neg_first = const.tile([P, 1], F32)
+        nc.vector.tensor_scalar(
+            out=neg_first[:], in0=mask_first[:], scalar1=-1.0, scalar2=MASKED, op0=ADD, op1=MULT
+        )
+        neg_rest = const.tile([P, TILES - 1], F32)
+        mb1_all = const.tile([P, H], BF16)
 
-        rows32 = {}
+        recv_rows = {}
+        send_rows = {}
         turned = {}
-        h_tiles = {}
+        h_psum = {}
+        h_own = {}
         codes = {}
+        accs = {}
         msgs = {}
         sums = {}
 
-        def pass_slice(c, t):
-            return slice(c * K_PASS + t * P, c * K_PASS + (t + 1) * P)
+        def t_slice(t):
+            return slice(t * P, (t + 1) * P)
 
-        def start_tile(r):
-            recv_rows = prep.tile([P, H], F32, name="recv_rows")
-            nc.vector.tensor_tensor(out=recv_rows[:], in0=xi_sb[r][:], in1=mb1_all[:], op=ADD)
-            send_rows = prep.tile([P, H], F32, name="send_rows")
-            nc.scalar.copy(out=send_rows[:], in_=xj_sb[r][:])
-            rows32[r] = (recv_rows, send_rows)
+        def pass_slice(c):
+            return slice(c * K_PASS, (c + 1) * K_PASS)
 
-        def turn_tile(r):
-            recv_rows, send_rows = rows32[r]
-            recv_t = prep.tile([P, PASSES, TILE_GRAPHS, NODES, PACK], F32, name="recv_t")
-            send_t = prep.tile([P, PASSES, TILE_GRAPHS, 2 * NODES, PACK], BF16, name="send_t")
-            for c in range(PASSES):
-                recv_ps = ps_pair.tile([P, PACK, P], F32, name="recv_ps", tag="pair")
-                for t in range(PACK):
-                    nc.tensor.transpose(recv_ps[:, t, :], recv_rows[:, pass_slice(c, t)], ident[:])
+        def mask_bias(r):
+            return neg_first[:] if r == 0 else neg_rest[:, r - 1 : r]
+
+        def new_receivers(r):
+            recv_rows[r] = [prep.tile([P, K_PASS], F32, name="recv_rows%d" % c) for c in range(PASSES)]
+
+        def add_receivers(r, c):
+            nc.gpsimd.tensor_tensor(
+                out=recv_rows[r][c][:], in0=xi_sb[r][:, pass_slice(c)], in1=mb1_all[:, pass_slice(c)], op=ADD
+            )
+
+        def mask_senders(r, c):
+            name = "send_rows%d" % c
+            send = prep.tile([P, K_PASS], (F32, BF16)[c], name=name)
+            nc.scalar.activation(
+                out=send[:], in_=xj_sb[r][:, pass_slice(c)], func=IDENTITY, bias=mask_bias(r), scale=1.0
+            )
+            send_rows[(r, c)] = send
+
+        def turn(r):
+            recv_ps = ps_recv.tile([P, PACK, P], F32, name="recv_ps", tag="recv")
+            for t in range(PACK):
+                nc.tensor.transpose(recv_ps[:, t, :], recv_rows[r][1][:, t_slice(t)], ident[:])
+            send_ps = ps_pair.tile([P, PACK, P], BF16, name="send_ps", tag="pair")
+            for t in range(PACK):
+                nc.tensor.transpose(send_ps[:, t, :], send_rows[(r, 1)][:, t_slice(t)], ident_bf[:])
+            send_t = prep.tile([P, TILE_GRAPHS, 2 * NODES, PACK], BF16, name="send_t")
+            for copy in range(2):
                 nc.scalar.copy(
-                    out=recv_t[:, c, :, :, :], in_=recv_ps[:].rearrange("p t (b i) -> p b i t", i=NODES)
+                    out=send_t[:, :, copy * NODES : (copy + 1) * NODES, :],
+                    in_=send_ps[:].rearrange("p t (b j) -> p b j t", j=NODES),
                 )
-                send_ps = ps_pair.tile([P, PACK, P], F32, name="send_ps", tag="pair")
-                for t in range(PACK):
-                    nc.tensor.transpose(send_ps[:, t, :], send_rows[:, pass_slice(c, t)], ident[:])
-                for copy in range(2):
-                    nc.scalar.copy(
-                        out=send_t[:, c, :, copy * NODES : (copy + 1) * NODES, :],
-                        in_=send_ps[:].rearrange("p t (b j) -> p b j t", j=NODES),
-                    )
-            turned[r] = (recv_t, send_t)
+            turned[r] = (recv_ps, send_t)
 
-        def new_h(r, group):
-            h_tiles[(r, group)] = hidden.tile([P, PASSES, ROTS, P, PACK], BF16, name="h", align_bytes=64)
-
-        def psum_sums(r, group, c, rotations):
-            recv_rows, send_rows = rows32[r]
-            for ql in range(rotations):
-                q = group * ROTS + ql
-                pair_ps = ps_pair.tile([P, PACK, P], F32, name="pair_ps", tag="pair")
-                for t in range(PACK):
-                    nc.tensor.matmul(
-                        out=pair_ps[:, t, :], lhsT=recv_rows[:, pass_slice(c, t)], rhs=ident[:],
-                        is_transpose=True, start=True, stop=False,
-                    )
-                    nc.tensor.matmul(
-                        out=pair_ps[:, t, :], lhsT=send_rows[:, pass_slice(c, t)],
-                        rhs=ident_twice[:, :, q : q + NODES],
-                        is_transpose=True, start=False, stop=True,
-                    )
-                nc.scalar.activation(
-                    out=h_tiles[(r, group)][:, c, ql, :, :], in_=pair_ps[:].rearrange("p t r -> p r t"), func=RELU
+        def psum_sum(n, ql):
+            r, group = divmod(n, GROUPS)
+            if ql == 0:
+                h_psum[n] = hidden.tile([P, ROTS, P, PACK], BF16, name="h_psum", align_bytes=64)
+            q = group * ROTS + ql
+            pair_ps = ps_pair.tile([P, PACK, P], F32, name="pair_ps", tag="pair")
+            for t in range(PACK):
+                nc.tensor.matmul(
+                    out=pair_ps[:, t, :], lhsT=recv_rows[r][0][:, t_slice(t)], rhs=ident[:],
+                    is_transpose=True, start=True, stop=False,
                 )
+                nc.tensor.matmul(
+                    out=pair_ps[:, t, :], lhsT=send_rows[(r, 0)][:, t_slice(t)],
+                    rhs=perms[:, q, :, :].rearrange("p b i -> p (b i)"),
+                    is_transpose=True, start=False, stop=True,
+                )
+            nc.scalar.activation(
+                out=h_psum[n][:, ql, :, :], in_=pair_ps[:].rearrange("p t r -> p r t"), func=RELU
+            )
 
-        def own_sum(r, group, ql):
-            recv_t, send_t = turned[r]
+        def own_sum(n, ql):
+            r, group = divmod(n, GROUPS)
+            if ql == 0:
+                h_own[n] = hidden.tile([P, ROTS, P, PACK], BF16, name="h_own", align_bytes=64)
+            recv_ps, send_t = turned[r]
             q = group * ROTS + ql
             nc.vector.tensor_tensor(
-                out=h_tiles[(r, group)][:, :, ql, :, :].rearrange("p c (b i) t -> p c b i t", i=NODES),
-                in0=recv_t[:],
-                in1=send_t[:, :, :, q : q + NODES, :],
+                out=h_own[n][:, ql, :, :].rearrange("p (b i) t -> p b i t", i=NODES),
+                in0=recv_ps[:].rearrange("p t (b i) -> p b i t", i=NODES),
+                in1=send_t[:, :, q : q + NODES, :],
                 op=ADD,
             )
 
-        def own_relu(r, group, first_own):
-            own = h_tiles[(r, group)][:, :, first_own:ROTS, :, :].rearrange("p c q r t -> p c (q r t)")
+        def own_relu(n):
+            own = h_own[n][:].rearrange("p q r t -> p (q r t)")
             nc.vector.tensor_scalar_max(out=own, in0=own, scalar1=0.0)
 
-        def quantise(r, group):
-            h_codes = packed.tile([P, PASSES, N_TILE], U32, name="h_codes", align_bytes=64)
-            h_scales = packed.tile([P, PASSES, N_TILE], U8, name="h_scales", align_bytes=64)
+        def quantise(n, c):
+            if n not in codes:
+                h_codes = packed.tile([P, PASSES, N_TILE], U32, name="h_codes", align_bytes=64)
+                h_scales = packed.tile([P, PASSES, N_TILE], U8, name="h_scales", align_bytes=64)
+                codes[n] = (h_codes, h_scales)
+            h_codes, h_scales = codes[n]
+            h = (h_psum, h_own)[c][n]
             nc.vector.quantize_mx(
-                out=h_codes[:].rearrange("p c n -> p (c n)").bitcast(FP8X4),
-                scales=h_scales[:].rearrange("p c n -> p (c n)"),
-                in_=h_tiles[(r, group)][:].rearrange("p c q r t -> p (c q r t)"),
+                out=h_codes[:, c, :].bitcast(FP8X4),
+                scales=h_scales[:, c, :],
+                in_=h[:].rearrange("p q r t -> p (q r t)"),
             )
-            codes[(r, group)] = (h_codes, h_scales)
 
-        def multiply(r, group):
-            h_codes, h_scales = codes[(r, group)]
-            acc = ps_acc.tile([P, N_TILE], F32, name="acc")
+        def multiply(n):
+            h_codes, h_scales = codes[n]
+            accs[n] = ps_acc.tile([P, N_TILE], F32, name="acc")
             for c in range(PASSES):
                 nc.tensor.matmul_mx(
-                    out=acc[:],
+                    out=accs[n][:],
                     lhsT=w_codes[:, c * D : (c + 1) * D].bitcast(FP8X4),
                     lhsT_scale=w_scales[:, c * D : (c + 1) * D],
                     rhs=h_codes[:, c, :].bitcast(FP8X4),
@@ -170,110 +210,136 @@ def tile_graphdynamics_pa_t_kernel(tc, xi_p, xj_p, node_mask, mb1, mw2, mb2, out
                     start=(c == 0),
                     stop=(c == PASSES - 1),
                 )
-            msg = tail.tile([P, ROTS, TILE_GRAPHS, NODES], F32, name="msg")
+
+        def finish_msgs(n):
+            msgs[n] = tail.tile([P, ROTS, P], F32, name="msg")
             nc.scalar.activation(
-                out=msg[:].rearrange("d q b i -> d (q b i)"), in_=acc[:], func=RELU, bias=mb2_col[:], scale=1.0
-            )
-            msgs[(r, group)] = msg
-
-        def mask_msgs(r, group):
-            msg = msgs[(r, group)]
-            first = group * ROTS
-            windows = mask_rep[:, r * TILE_GRAPHS : (r + 1) * TILE_GRAPHS, first : first + ROTS * MASK_PITCH]
-            nc.vector.tensor_tensor(
-                out=msg[:],
-                in0=msg[:],
-                in1=windows.rearrange("p b (q w) -> p q b w", w=MASK_PITCH)[:, :, :, 0:NODES],
-                op=MULT,
+                out=msgs[n][:].rearrange("d q r -> d (q r)"), in_=accs[n][:], func=RELU, bias=mb2_col[:], scale=1.0
             )
 
-        def add_up(r, group, first, last):
-            if first:
+        def add_up(n):
+            r, group = divmod(n, GROUPS)
+            if group == 0:
                 sums[r] = ps_out.tile([P, D], F32, name="out_ps")
-            msg = msgs[(r, group)]
             for ql in range(ROTS):
                 nc.tensor.matmul(
-                    out=sums[r][:], lhsT=msg[:, ql, :, :].rearrange("d b i -> d (b i)"), rhs=ident[:],
-                    is_transpose=True, start=(first and ql == 0), stop=(last and ql == ROTS - 1),
+                    out=sums[r][:], lhsT=msgs[n][:, ql, :], rhs=ident[:], is_transpose=True,
+                    start=(group == 0 and ql == 0), stop=(group == GROUPS - 1 and ql == ROTS - 1),
                 )
 
         def finish(r):
             out_sb = tail.tile([P, D], F32, name="out_sb", bufs=2)
-            nc.scalar.copy(out=out_sb[:], in_=sums[r][:])
+            nc.vector.scalar_tensor_tensor(
+                out=out_sb[:], in0=relu_mb2[:], scalar=minus_masked[:, r : r + 1], in1=sums[r][:], op0=MULT, op1=ADD
+            )
             nc.sync.dma_start(out=out_rows[r * P : (r + 1) * P, :], in_=out_sb[:])
 
-        start_tile(0)
-        ident_twice = const.tile([P, TILE_GRAPHS, 2 * NODES], F32)
-        ident_blocks = ident[:].rearrange("p (b j) -> p b j", j=NODES)
-        nc.vector.tensor_copy(out=ident_twice[:, :, 0:NODES], in_=ident_blocks)
-        nc.vector.tensor_copy(out=ident_twice[:, :, NODES : 2 * NODES], in_=ident_blocks)
-        turn_tile(0)
+        mb1_ps = [
+            ps_acc.tile([P, K_PASS], F32, name="acc"),
+            ps_out.tile([P, K_PASS], F32, name="out_ps"),
+        ]
+        for c in range(PASSES):
+            nc.tensor.matmul(out=mb1_ps[c][:], lhsT=ones[:], rhs=vec_row[:, pass_slice(c)], start=True, stop=True)
+        new_receivers(0)
+        for c in range(PASSES):
+            mask_senders(0, c)
+            nc.vector.tensor_tensor(
+                out=recv_rows[0][c][:], in0=xi_sb[0][:, pass_slice(c)], in1=mb1_ps[c][:], op=ADD
+            )
+        turn(0)
 
         w_grouped = const.tile([P, PASSES, D, PACK], BF16, align_bytes=64)
-        nc.vector.tensor_copy(out=w_grouped[:], in_=w_raw[:].rearrange("p c t d -> p c d t"))
         mb2_col = const.tile([P, 1], F32)
-        nc.vector.tensor_copy(out=mb2_col[:], in_=mb2_bf[:])
         w_codes = const.tile([P, PASSES * D], U32, align_bytes=64)
         w_scales = const.tile([P, PASSES * D], U8, align_bytes=64)
-        nc.vector.quantize_mx(
-            out=w_codes[:].bitcast(FP8X4),
-            scales=w_scales[:],
-            in_=w_grouped[:].rearrange("p c d t -> p (c d t)"),
-        )
-        mask_rep = const.tile([P, GRAPHS, MASK_LEN], BF16)
-        for period in range(MASK_LEN // NODES):
-            nc.vector.tensor_copy(out=mask_rep[:, :, period * NODES : (period + 1) * NODES], in_=mask_all[:])
+        relu_mb2 = const.tile([P, D], F32)
+        minus_masked = const.tile([P, TILES], F32)
+        mask_all = const.tile([P, TILES], BF16)
+        block_rows = const.tile([P, TILE_GRAPHS], F32)
+        block_ones = const.tile([P, TILE_GRAPHS, NODES], BF16)
 
-        def pair_formed_at(step):
-            r, k = divmod(step, STEPS)
-            if 0 <= r < TILES:
-                return r, (k // 2, GROUPS // 2 + k // 2)
-            return None
+        def late_constants():
+            nc.vector.tensor_copy(out=w_grouped[:], in_=w_raw[:].rearrange("p c t d -> p c d t"))
+            nc.vector.tensor_scalar(
+                out=neg_rest[:], in0=mask_rest[:], scalar1=-1.0, scalar2=MASKED, op0=ADD, op1=MULT
+            )
+            nc.vector.tensor_copy(out=mb2_col[:], in_=mb2_bf[:])
+            nc.vector.quantize_mx(
+                out=w_codes[:].bitcast(FP8X4),
+                scales=w_scales[:],
+                in_=w_grouped[:].rearrange("p c d t -> p (c d t)"),
+            )
+            for c in range(PASSES):
+                nc.scalar.copy(out=mb1_all[:, pass_slice(c)], in_=mb1_ps[c][:])
 
-        for step in range(STEPS * TILES + 5):
-            r, k = divmod(step, STEPS)
-            odd = k % 2
-            forming = r < TILES
-            psum_group, own_group = k // 2, GROUPS // 2 + k // 2
-            done = pair_formed_at(step - 1) if not odd else pair_formed_at(step - 4)
+        def graph_blocks():
+            nc.vector.tensor_copy(out=mask_all[:, 0:1], in_=mask_first[:])
+            nc.vector.tensor_copy(out=mask_all[:, 1:TILES], in_=mask_rest[:])
+            nc.vector.tensor_reduce(out=block_rows[:], in_=ident_blocks, axis=mybir.AxisListType.X, op=ADD)
+            nc.vector.tensor_copy(
+                out=block_ones[:], in_=block_rows[:].unsqueeze(2).to_broadcast([P, TILE_GRAPHS, NODES])
+            )
 
-            first_own = EXTRA if own_group == GROUPS // 2 else 0
+        def correction_sums():
+            vec_ps = ps_pair.tile([P, D + TILES], F32, name="vec_ps", tag="pair")
+            nc.tensor.matmul(
+                out=vec_ps[:, 0:D], lhsT=ones[:], rhs=vec_row[:, H : H + D], start=True, stop=True
+            )
+            nc.tensor.matmul(
+                out=vec_ps[:, D : D + TILES], lhsT=block_ones[:].rearrange("p b j -> p (b j)"), rhs=mask_all[:],
+                start=True, stop=True,
+            )
+            return vec_ps
+
+        def correction_constants(vec_ps):
+            nc.vector.tensor_scalar_max(out=relu_mb2[:], in0=vec_ps[:, 0:D], scalar1=0.0)
+            nc.vector.tensor_scalar(
+                out=minus_masked[:], in0=vec_ps[:, D : D + TILES], scalar1=-float(NODES), scalar2=0.0, op0=ADD, op1=ADD
+            )
+
+        groups = TILES * GROUPS
+        for n in range(groups + 5):
+            r, group = divmod(n, GROUPS)
+            forming = n < groups
+            if n == 3:
+                correction_constants(vec_ps)
+            if n - 5 >= 0 and (n - 5) % GROUPS == GROUPS - 1:
+                finish((n - 5) // GROUPS)
             if forming:
-                if not odd:
-                    new_h(r, psum_group)
-                    new_h(r, own_group)
-                psum_sums(r, psum_group, odd, ROTS)
-                psum_sums(r, own_group, odd, first_own)
-                if 2 * odd >= first_own:
-                    own_sum(r, own_group, 2 * odd)
-            if done and not odd:
-                quantise(done[0], done[1][0])
-            if forming and 2 * odd + 1 >= first_own:
-                own_sum(r, own_group, 2 * odd + 1)
-            if done and not odd:
-                quantise(done[0], done[1][1])
-            if done and odd:
-                mask_msgs(done[0], done[1][0])
-                mask_msgs(done[0], done[1][1])
-            if forming and odd:
-                own_relu(r, own_group, first_own)
-
-            if odd:
-                ready = pair_formed_at(step - 2)
-                if ready:
-                    multiply(ready[0], ready[1][0])
-                    multiply(ready[0], ready[1][1])
-            else:
-                masked = pair_formed_at(step - 5)
-                if masked:
-                    first_pair = masked[1][0] == 0
-                    add_up(masked[0], masked[1][0], first_pair, False)
-                    add_up(masked[0], masked[1][1], False, not first_pair)
-                    if not first_pair:
-                        finish(masked[0])
-
-            if r + 1 < TILES:
-                if k == 0:
-                    start_tile(r + 1)
-                if k == 2:
-                    turn_tile(r + 1)
+                psum_sum(n, 0)
+                psum_sum(n, 1)
+            if 0 <= n - 3 < groups:
+                finish_msgs(n - 3)
+            if forming:
+                psum_sum(n, 2)
+                psum_sum(n, 3)
+                own_sum(n, 0)
+                own_sum(n, 1)
+            if 0 <= n - 1 < groups:
+                own_relu(n - 1)
+            if forming:
+                own_sum(n, 2)
+                own_sum(n, 3)
+            if 0 <= n - 1 < groups:
+                quantise(n - 1, 1)
+                quantise(n - 1, 0)
+            if n == 0:
+                late_constants()
+            if n == 1:
+                graph_blocks()
+            if n == 2:
+                vec_ps = correction_sums()
+            if 0 <= n - 4 < groups:
+                add_up(n - 4)
+            if forming and r + 1 < TILES:
+                if group == 0:
+                    new_receivers(r + 1)
+                    add_receivers(r + 1, 1)
+                    mask_senders(r + 1, 1)
+                    add_receivers(r + 1, 0)
+                if group == 1:
+                    mask_senders(r + 1, 0)
+                if group == 2:
+                    turn(r + 1)
+            if 0 <= n - 2 < groups:
+                multiply(n - 2)

@@ -25,6 +25,11 @@ GROUPS = NODES // ROTS
 N_TILE = ROTS * P
 MASKED = 2.0**126
 
+VECTOR_RELUS = 3
+OWN_ROTS = 2
+PITCH = NODES + 1
+PERIODS = -(-(NODES - OWN_ROTS + OWN_ROTS * PITCH) // NODES)
+
 FLOPS = 2 * GRAPHS * NODES * NODES * H * D
 
 
@@ -48,9 +53,10 @@ def tile_graphdynamics_pa_t_kernel(tc, xi_p, xj_p, node_mask, mb1, mw2, mb2, out
         ctx.enter_context(tc.manual_schedule())
 
         vec_row = const.tile([P, H + D], BF16)
-        nc.vector.memset(vec_row[:], 0.0)
-        nc.scalar.dma_start(out=vec_row[0:1, 0:H], in_=mb1.unsqueeze(0))
-        nc.scalar.dma_start(out=vec_row[0:1, H : H + D], in_=mb2.unsqueeze(0))
+        nc.gpsimd.memset(vec_row[:, 0:K_PASS].bitcast(F32), 0.0)
+        nc.vector.memset(vec_row[:, K_PASS : H + D].bitcast(F32), 0.0)
+        warm = const.tile([P, 1], F32)
+        nc.vector.memset(warm[:], 0.0)
         mask_first = const.tile([P, 1], BF16)
         mask_rest = const.tile([P, TILES - 1], BF16)
         mb2_bf = const.tile([P, 1], BF16)
@@ -59,6 +65,9 @@ def tile_graphdynamics_pa_t_kernel(tc, xi_p, xj_p, node_mask, mb1, mw2, mb2, out
             nc.scalar.dma_start(
                 out=mask_first[:], in_=node_mask[0:TILE_GRAPHS, :].rearrange("b j -> (b j)").unsqueeze(1)
             )
+            nc.scalar.dma_start(out=vec_row[0:1, 0:H], in_=mb1.unsqueeze(0))
+            nc.scalar.activation(out=warm[:], in_=warm[:], func=IDENTITY, bias=0.0, scale=1.0)
+            nc.scalar.dma_start(out=vec_row[0:1, H : H + D], in_=mb2.unsqueeze(0))
             nc.scalar.dma_start(out=w_raw[:], in_=mw2.rearrange("(c t p) d -> p c t d", c=PASSES, t=PACK, p=P))
             nc.scalar.dma_start(
                 out=mask_rest[:],
@@ -71,7 +80,7 @@ def tile_graphdynamics_pa_t_kernel(tc, xi_p, xj_p, node_mask, mb1, mw2, mb2, out
             xj_tile = rows.tile([P, H], BF16, name="xj_tile")
             xi_tile = rows.tile([P, H], BF16, name="xi_tile")
             pieces = PASSES if r == 0 else 1
-            for piece in range(pieces):
+            for piece in reversed(range(pieces)):
                 cols = slice(piece * H // pieces, (piece + 1) * H // pieces)
                 nc.sync.dma_start(out=xj_tile[:, cols], in_=xj_rows[r * P : (r + 1) * P, cols])
                 nc.sync.dma_start(out=xi_tile[:, cols], in_=xi_rows[r * P : (r + 1) * P, cols])
@@ -86,10 +95,14 @@ def tile_graphdynamics_pa_t_kernel(tc, xi_p, xj_p, node_mask, mb1, mw2, mb2, out
         ident_bf = const.tile([P, P], BF16)
         nc.vector.tensor_copy(out=ident_bf[:], in_=ident[:])
         perms = const.tile([P, NODES, TILE_GRAPHS, NODES], F32)
-        for q in range(NODES):
-            nc.vector.tensor_copy(out=perms[:, q, :, 0 : NODES - q], in_=ident_blocks[:, :, q:NODES])
-            if q:
-                nc.vector.tensor_copy(out=perms[:, q, :, NODES - q : NODES], in_=ident_blocks[:, :, 0:q])
+
+        def make_perms(first, last):
+            for q in range(first, last):
+                nc.vector.tensor_copy(out=perms[:, q, :, 0 : NODES - q], in_=ident_blocks[:, :, q:NODES])
+                if q:
+                    nc.vector.tensor_copy(out=perms[:, q, :, NODES - q : NODES], in_=ident_blocks[:, :, 0:q])
+
+        make_perms(0, ROTS)
         neg_first = const.tile([P, 1], F32)
         nc.vector.tensor_scalar(
             out=neg_first[:], in0=mask_first[:], scalar1=-1.0, scalar2=MASKED, op0=ADD, op1=MULT
@@ -99,9 +112,9 @@ def tile_graphdynamics_pa_t_kernel(tc, xi_p, xj_p, node_mask, mb1, mw2, mb2, out
 
         recv_rows = {}
         send_rows = {}
-        turned = {}
-        h_psum = {}
-        h_own = {}
+        recv_ps = {}
+        send_t = {}
+        h = {}
         codes = {}
         accs = {}
         msgs = {}
@@ -120,108 +133,118 @@ def tile_graphdynamics_pa_t_kernel(tc, xi_p, xj_p, node_mask, mb1, mw2, mb2, out
             recv_rows[r] = [prep.tile([P, K_PASS], F32, name="recv_rows%d" % c) for c in range(PASSES)]
 
         def add_receivers(r, c):
-            nc.gpsimd.tensor_tensor(
-                out=recv_rows[r][c][:], in0=xi_sb[r][:, pass_slice(c)], in1=mb1_all[:, pass_slice(c)], op=ADD
-            )
+            for t in range(PACK):
+                cols = slice(c * K_PASS + t * P, c * K_PASS + (t + 1) * P)
+                nc.gpsimd.tensor_tensor(
+                    out=recv_rows[r][c][:, t_slice(t)], in0=xi_sb[r][:, cols], in1=mb1_all[:, cols], op=ADD
+                )
 
-        def mask_senders(r, c):
-            name = "send_rows%d" % c
-            send = prep.tile([P, K_PASS], (F32, BF16)[c], name=name)
+        def mask_senders(r, c, dtype):
+            send = prep.tile([P, K_PASS], dtype, name="send_f32_%d" % c if dtype == F32 else "send_bf16")
             nc.scalar.activation(
                 out=send[:], in_=xj_sb[r][:, pass_slice(c)], func=IDENTITY, bias=mask_bias(r), scale=1.0
             )
-            send_rows[(r, c)] = send
+            send_rows[(r, c, dtype)] = send
 
-        def turn(r):
-            recv_ps = ps_recv.tile([P, PACK, P], F32, name="recv_ps", tag="recv")
+        def turn_receivers(r):
+            recv_ps[r] = ps_recv.tile([P, PACK, P], F32, name="recv_ps", tag="recv")
             for t in range(PACK):
-                nc.tensor.transpose(recv_ps[:, t, :], recv_rows[r][1][:, t_slice(t)], ident[:])
+                nc.tensor.transpose(recv_ps[r][:, t, :], recv_rows[r][1][:, t_slice(t)], ident[:])
+
+        def turn_senders(r):
             send_ps = ps_pair.tile([P, PACK, P], BF16, name="send_ps", tag="pair")
             for t in range(PACK):
-                nc.tensor.transpose(send_ps[:, t, :], send_rows[(r, 1)][:, t_slice(t)], ident_bf[:])
-            send_t = prep.tile([P, TILE_GRAPHS, 2 * NODES, PACK], BF16, name="send_t")
-            for copy in range(2):
+                nc.tensor.transpose(send_ps[:, t, :], send_rows[(r, 1, BF16)][:, t_slice(t)], ident_bf[:])
+            send_t[r] = prep.tile([P, TILE_GRAPHS, PERIODS * NODES, PACK], BF16, name="send_t")
+            for copy in range(PERIODS):
                 nc.scalar.copy(
-                    out=send_t[:, :, copy * NODES : (copy + 1) * NODES, :],
+                    out=send_t[r][:, :, copy * NODES : (copy + 1) * NODES, :],
                     in_=send_ps[:].rearrange("p t (b j) -> p b j t", j=NODES),
                 )
-            turned[r] = (recv_ps, send_t)
 
-        def psum_sum(n, ql):
+        def new_h(n):
+            h[n] = [hidden.tile([P, ROTS, P, PACK], BF16, name="h%d" % c, align_bytes=64) for c in range(PASSES)]
+
+        def psum_sum(n, c, ql):
             r, group = divmod(n, GROUPS)
-            if ql == 0:
-                h_psum[n] = hidden.tile([P, ROTS, P, PACK], BF16, name="h_psum", align_bytes=64)
             q = group * ROTS + ql
             pair_ps = ps_pair.tile([P, PACK, P], F32, name="pair_ps", tag="pair")
             for t in range(PACK):
                 nc.tensor.matmul(
-                    out=pair_ps[:, t, :], lhsT=recv_rows[r][0][:, t_slice(t)], rhs=ident[:],
+                    out=pair_ps[:, t, :], lhsT=recv_rows[r][c][:, t_slice(t)], rhs=ident[:],
                     is_transpose=True, start=True, stop=False,
                 )
                 nc.tensor.matmul(
-                    out=pair_ps[:, t, :], lhsT=send_rows[(r, 0)][:, t_slice(t)],
+                    out=pair_ps[:, t, :], lhsT=send_rows[(r, c, F32)][:, t_slice(t)],
                     rhs=perms[:, q, :, :].rearrange("p b i -> p (b i)"),
                     is_transpose=True, start=False, stop=True,
                 )
             nc.scalar.activation(
-                out=h_psum[n][:, ql, :, :], in_=pair_ps[:].rearrange("p t r -> p r t"), func=RELU
+                out=h[n][c][:, ql, :, :], in_=pair_ps[:].rearrange("p t r -> p r t"), func=RELU
             )
 
         def own_sum(n, ql):
             r, group = divmod(n, GROUPS)
-            if ql == 0:
-                h_own[n] = hidden.tile([P, ROTS, P, PACK], BF16, name="h_own", align_bytes=64)
-            recv_ps, send_t = turned[r]
             q = group * ROTS + ql
+            windows = send_t[r][:, :, q : q + OWN_ROTS * PITCH, :].rearrange("p b (q w) t -> p q b w t", w=PITCH)
             nc.vector.tensor_tensor(
-                out=h_own[n][:, ql, :, :].rearrange("p (b i) t -> p b i t", i=NODES),
-                in0=recv_ps[:].rearrange("p t (b i) -> p b i t", i=NODES),
-                in1=send_t[:, :, q : q + NODES, :],
+                out=h[n][1][:, ql : ql + OWN_ROTS, :, :].rearrange("p q (b i) t -> p q b i t", i=NODES),
+                in0=recv_ps[r][:].rearrange("p t (b i) -> p b i t", i=NODES)
+                .unsqueeze(1)
+                .to_broadcast([P, OWN_ROTS, TILE_GRAPHS, NODES, PACK]),
+                in1=windows[:, :, :, 0:NODES, :],
                 op=ADD,
             )
 
-        def own_relu(n):
-            own = h_own[n][:].rearrange("p q r t -> p (q r t)")
+        def vector_relu(n, first, last):
+            own = h[n][1][:, first:last, :, :].rearrange("p q r t -> p (q r t)")
             nc.vector.tensor_scalar_max(out=own, in0=own, scalar1=0.0)
 
-        def quantise(n, c):
+        def scalar_relu(n, first, last):
+            own = h[n][1][:, first:last, :, :].rearrange("p q r t -> p (q r t)")
+            nc.scalar.activation(out=own, in_=own, func=RELU)
+
+        def quantise(n, c, first=0, last=ROTS):
             if n not in codes:
                 h_codes = packed.tile([P, PASSES, N_TILE], U32, name="h_codes", align_bytes=64)
                 h_scales = packed.tile([P, PASSES, N_TILE], U8, name="h_scales", align_bytes=64)
                 codes[n] = (h_codes, h_scales)
             h_codes, h_scales = codes[n]
-            h = (h_psum, h_own)[c][n]
             nc.vector.quantize_mx(
-                out=h_codes[:, c, :].bitcast(FP8X4),
-                scales=h_scales[:, c, :],
-                in_=h[:].rearrange("p q r t -> p (q r t)"),
+                out=h_codes[:, c, first * P : last * P].bitcast(FP8X4),
+                scales=h_scales[:, c, first * P : last * P],
+                in_=h[n][c][:, first:last, :, :].rearrange("p q r t -> p (q r t)"),
             )
 
-        def multiply(n):
+        def multiply(n, first=0, last=ROTS):
             h_codes, h_scales = codes[n]
-            accs[n] = ps_acc.tile([P, N_TILE], F32, name="acc")
+            if first == 0:
+                accs[n] = ps_acc.tile([P, N_TILE], F32, name="acc")
+            cols = slice(first * P, last * P)
             for c in range(PASSES):
                 nc.tensor.matmul_mx(
-                    out=accs[n][:],
+                    out=accs[n][:, cols],
                     lhsT=w_codes[:, c * D : (c + 1) * D].bitcast(FP8X4),
                     lhsT_scale=w_scales[:, c * D : (c + 1) * D],
-                    rhs=h_codes[:, c, :].bitcast(FP8X4),
-                    rhs_scale=h_scales[:, c, :],
+                    rhs=h_codes[:, c, cols].bitcast(FP8X4),
+                    rhs_scale=h_scales[:, c, cols],
                     start=(c == 0),
                     stop=(c == PASSES - 1),
                 )
 
-        def finish_msgs(n):
-            msgs[n] = tail.tile([P, ROTS, P], F32, name="msg")
+        def finish_msgs(n, first=0, last=ROTS):
+            if first == 0:
+                msgs[n] = tail.tile([P, ROTS, P], F32, name="msg")
             nc.scalar.activation(
-                out=msgs[n][:].rearrange("d q r -> d (q r)"), in_=accs[n][:], func=RELU, bias=mb2_col[:], scale=1.0
+                out=msgs[n][:, first:last, :].rearrange("d q r -> d (q r)"), in_=accs[n][:, first * P : last * P],
+                func=RELU, bias=mb2_col[:], scale=1.0,
             )
 
-        def add_up(n):
+        def add_up(n, first=0, last=ROTS):
             r, group = divmod(n, GROUPS)
-            if group == 0:
+            if group == 0 and first == 0:
                 sums[r] = ps_out.tile([P, D], F32, name="out_ps")
-            for ql in range(ROTS):
+            for ql in range(first, last):
                 nc.tensor.matmul(
                     out=sums[r][:], lhsT=msgs[n][:, ql, :], rhs=ident[:], is_transpose=True,
                     start=(group == 0 and ql == 0), stop=(group == GROUPS - 1 and ql == ROTS - 1),
@@ -238,15 +261,28 @@ def tile_graphdynamics_pa_t_kernel(tc, xi_p, xj_p, node_mask, mb1, mw2, mb2, out
             ps_acc.tile([P, K_PASS], F32, name="acc"),
             ps_out.tile([P, K_PASS], F32, name="out_ps"),
         ]
-        for c in range(PASSES):
+        def spread_mb1(c):
             nc.tensor.matmul(out=mb1_ps[c][:], lhsT=ones[:], rhs=vec_row[:, pass_slice(c)], start=True, stop=True)
-        new_receivers(0)
-        for c in range(PASSES):
-            mask_senders(0, c)
+
+        def first_receivers(c):
             nc.vector.tensor_tensor(
                 out=recv_rows[0][c][:], in0=xi_sb[0][:, pass_slice(c)], in1=mb1_ps[c][:], op=ADD
             )
-        turn(0)
+
+        new_receivers(0)
+        mask_senders(0, 1, BF16)
+        send_rows[(0, 0, F32)] = prep.tile([P, K_PASS], F32, name="send_f32_0")
+        nc.gpsimd.tensor_scalar(
+            out=send_rows[(0, 0, F32)][:], in0=xj_sb[0][:, pass_slice(0)], scalar1=mask_bias(0), scalar2=0.0,
+            op0=ADD, op1=ADD,
+        )
+        spread_mb1(1)
+        first_receivers(1)
+        turn_senders(0)
+        spread_mb1(0)
+        first_receivers(0)
+        turn_receivers(0)
+        make_perms(ROTS, NODES)
 
         w_grouped = const.tile([P, PASSES, D, PACK], BF16, align_bytes=64)
         mb2_col = const.tile([P, 1], F32)
@@ -254,7 +290,7 @@ def tile_graphdynamics_pa_t_kernel(tc, xi_p, xj_p, node_mask, mb1, mw2, mb2, out
         w_scales = const.tile([P, PASSES * D], U8, align_bytes=64)
         relu_mb2 = const.tile([P, D], F32)
         minus_masked = const.tile([P, TILES], F32)
-        mask_all = const.tile([P, TILES], BF16)
+        minus_one = const.tile([P, TILES], BF16)
         block_rows = const.tile([P, TILE_GRAPHS], F32)
         block_ones = const.tile([P, TILE_GRAPHS, NODES], BF16)
 
@@ -273,8 +309,8 @@ def tile_graphdynamics_pa_t_kernel(tc, xi_p, xj_p, node_mask, mb1, mw2, mb2, out
                 nc.scalar.copy(out=mb1_all[:, pass_slice(c)], in_=mb1_ps[c][:])
 
         def graph_blocks():
-            nc.vector.tensor_copy(out=mask_all[:, 0:1], in_=mask_first[:])
-            nc.vector.tensor_copy(out=mask_all[:, 1:TILES], in_=mask_rest[:])
+            nc.vector.tensor_scalar_add(out=minus_one[:, 0:1], in0=mask_first[:], scalar1=-1.0)
+            nc.vector.tensor_scalar_add(out=minus_one[:, 1:TILES], in0=mask_rest[:], scalar1=-1.0)
             nc.vector.tensor_reduce(out=block_rows[:], in_=ident_blocks, axis=mybir.AxisListType.X, op=ADD)
             nc.vector.tensor_copy(
                 out=block_ones[:], in_=block_rows[:].unsqueeze(2).to_broadcast([P, TILE_GRAPHS, NODES])
@@ -286,60 +322,88 @@ def tile_graphdynamics_pa_t_kernel(tc, xi_p, xj_p, node_mask, mb1, mw2, mb2, out
                 out=vec_ps[:, 0:D], lhsT=ones[:], rhs=vec_row[:, H : H + D], start=True, stop=True
             )
             nc.tensor.matmul(
-                out=vec_ps[:, D : D + TILES], lhsT=block_ones[:].rearrange("p b j -> p (b j)"), rhs=mask_all[:],
+                out=vec_ps[:, D : D + TILES], lhsT=block_ones[:].rearrange("p b j -> p (b j)"), rhs=minus_one[:],
                 start=True, stop=True,
             )
             return vec_ps
 
         def correction_constants(vec_ps):
-            nc.vector.tensor_scalar_max(out=relu_mb2[:], in0=vec_ps[:, 0:D], scalar1=0.0)
-            nc.vector.tensor_scalar(
-                out=minus_masked[:], in0=vec_ps[:, D : D + TILES], scalar1=-float(NODES), scalar2=0.0, op0=ADD, op1=ADD
-            )
+            nc.scalar.activation(out=relu_mb2[:], in_=vec_ps[:, 0:D], func=RELU)
+            nc.scalar.copy(out=minus_masked[:], in_=vec_ps[:, D : D + TILES])
 
         groups = TILES * GROUPS
-        for n in range(groups + 5):
+
+        def own_rotations(n):
+            return ROTS if n < groups - 1 else ROTS // 2
+
+        for n in range(groups):
             r, group = divmod(n, GROUPS)
-            forming = n < groups
             if n == 3:
                 correction_constants(vec_ps)
             if n - 5 >= 0 and (n - 5) % GROUPS == GROUPS - 1:
                 finish((n - 5) // GROUPS)
-            if forming:
-                psum_sum(n, 0)
-                psum_sum(n, 1)
-            if 0 <= n - 3 < groups:
+            new_h(n)
+            if n >= 3:
                 finish_msgs(n - 3)
-            if forming:
-                psum_sum(n, 2)
-                psum_sum(n, 3)
-                own_sum(n, 0)
-                own_sum(n, 1)
-            if 0 <= n - 1 < groups:
-                own_relu(n - 1)
-            if forming:
-                own_sum(n, 2)
-                own_sum(n, 3)
-            if 0 <= n - 1 < groups:
-                quantise(n - 1, 1)
+            psum_sum(n, 0, 0)
+            psum_sum(n, 0, 1)
+            if n >= 1:
+                scalar_relu(n - 1, VECTOR_RELUS, ROTS)
+            psum_sum(n, 0, 2)
+            psum_sum(n, 0, 3)
+            own_sum(n, 0)
+            if n >= 1:
+                vector_relu(n - 1, 0, VECTOR_RELUS)
+            for ql in range(OWN_ROTS, ROTS, OWN_ROTS):
+                if ql < own_rotations(n):
+                    own_sum(n, ql)
+                else:
+                    for q in range(OWN_ROTS):
+                        psum_sum(n, 1, ql + q)
+            if n >= 1:
                 quantise(n - 1, 0)
+                quantise(n - 1, 1)
             if n == 0:
                 late_constants()
             if n == 1:
                 graph_blocks()
             if n == 2:
                 vec_ps = correction_sums()
-            if 0 <= n - 4 < groups:
+            if n >= 4:
                 add_up(n - 4)
-            if forming and r + 1 < TILES:
+            if r + 1 < TILES:
                 if group == 0:
                     new_receivers(r + 1)
                     add_receivers(r + 1, 1)
-                    mask_senders(r + 1, 1)
+                    mask_senders(r + 1, 1, BF16)
                     add_receivers(r + 1, 0)
                 if group == 1:
-                    mask_senders(r + 1, 0)
+                    mask_senders(r + 1, 0, F32)
+                    if r + 1 == TILES - 1:
+                        mask_senders(r + 1, 1, F32)
                 if group == 2:
-                    turn(r + 1)
-            if 0 <= n - 2 < groups:
+                    turn_senders(r + 1)
+                    turn_receivers(r + 1)
+            if n >= 2:
                 multiply(n - 2)
+
+        last = groups - 1
+        halves = ((0, ROTS // 2), (ROTS // 2, ROTS))
+        finish(TILES - 2)
+        finish_msgs(last - 2)
+        vector_relu(last, 0, own_rotations(last))
+        for first, end in halves:
+            quantise(last, 0, first, end)
+            quantise(last, 1, first, end)
+        add_up(last - 3)
+        multiply(last - 1)
+        finish_msgs(last - 1)
+        add_up(last - 2)
+        for first, end in halves:
+            multiply(last, first, end)
+        add_up(last - 1)
+        for first, end in halves:
+            finish_msgs(last, first, end)
+        for first, end in halves:
+            add_up(last, first, end)
+        finish(TILES - 1)

@@ -26,6 +26,12 @@ N_TILE = ROTS * P
 MASKED = 2.0**126
 
 VECTOR_RELUS = 3
+SET_STARTS = (0, 3, 5)
+SET_COLS = ((0, 48), (48, 96), (96, 128))
+SET_ROWS = 3 * NODES
+ROW_MB1, ROW_MASK = 2 * SET_ROWS, 2 * SET_ROWS + 1
+PICKED = 2
+PICKED_FROM, PICKED_SUMS = 8, 20
 OWN_ROTS = 2
 PITCH = NODES + 1
 PERIODS = -(-(NODES - OWN_ROTS + OWN_ROTS * PITCH) // NODES)
@@ -52,9 +58,9 @@ def tile_graphdynamics_pa_t_kernel(tc, xi_p, xj_p, node_mask, mb1, mw2, mb2, out
         ps_out = ctx.enter_context(tc.psum_pool(name="ps_out", bufs=1))
         ctx.enter_context(tc.manual_schedule())
 
-        vec_row = const.tile([P, H + D], BF16)
+        vec_row = const.tile([P, H], BF16)
         nc.gpsimd.memset(vec_row[:, 0:K_PASS].bitcast(F32), 0.0)
-        nc.vector.memset(vec_row[:, K_PASS : H + D].bitcast(F32), 0.0)
+        nc.vector.memset(vec_row[:, K_PASS:H].bitcast(F32), 0.0)
         warm = const.tile([P, 1], F32)
         nc.vector.memset(warm[:], 0.0)
         mask_first = const.tile([P, 1], BF16)
@@ -67,13 +73,6 @@ def tile_graphdynamics_pa_t_kernel(tc, xi_p, xj_p, node_mask, mb1, mw2, mb2, out
             )
             nc.scalar.dma_start(out=vec_row[0:1, 0:H], in_=mb1.unsqueeze(0))
             nc.scalar.activation(out=warm[:], in_=warm[:], func=IDENTITY, bias=0.0, scale=1.0)
-            nc.scalar.dma_start(out=vec_row[0:1, H : H + D], in_=mb2.unsqueeze(0))
-            nc.scalar.dma_start(out=w_raw[:], in_=mw2.rearrange("(c t p) d -> p c t d", c=PASSES, t=PACK, p=P))
-            nc.scalar.dma_start(
-                out=mask_rest[:],
-                in_=node_mask[TILE_GRAPHS:GRAPHS, :].rearrange("(r b) j -> (b j) r", b=TILE_GRAPHS),
-            )
-            nc.scalar.dma_start(out=mb2_bf[:], in_=mb2.unsqueeze(1))
         xi_sb = []
         xj_sb = []
         for r in range(TILES):
@@ -86,12 +85,31 @@ def tile_graphdynamics_pa_t_kernel(tc, xi_p, xj_p, node_mask, mb1, mw2, mb2, out
                 nc.sync.dma_start(out=xi_tile[:, cols], in_=xi_rows[r * P : (r + 1) * P, cols])
             xi_sb.append(xi_tile)
             xj_sb.append(xj_tile)
+            if r == 0:
+                with nc.allow_non_contiguous_dma(reason="vectors with one value a partition"):
+                    nc.sync.dma_start(
+                        out=mask_rest[:],
+                        in_=node_mask[TILE_GRAPHS:GRAPHS, :].rearrange("(r b) j -> (b j) r", b=TILE_GRAPHS),
+                    )
+                    nc.sync.dma_start(out=mb2_bf[:], in_=mb2.unsqueeze(1))
+                    nc.sync.dma_start(
+                        out=w_raw[:], in_=mw2.rearrange("(c t p) d -> p c t d", c=PASSES, t=PACK, p=P)
+                    )
 
         ident = const.tile([P, P], F32)
         make_identity(nc, ident[:])
         ident_blocks = ident[:].rearrange("p (b j) -> p b j", j=NODES)
         ones = const.tile([P, P], BF16)
         nc.vector.memset(ones[:], 1.0)
+        idle = const.tile([P, 2 * P], F32)
+        nc.vector.memset(idle[:], 0.0)
+
+        def keep_busy(columns):
+            idle_ps = ps_pair.tile([P, 2 * P], F32, name="idle_ps", tag="pair")
+            nc.tensor.matmul(
+                out=idle_ps[:, 0:columns], lhsT=idle[:, 0:P], rhs=idle[:, 0:columns], start=True, stop=True
+            )
+
         ident_bf = const.tile([P, P], BF16)
         nc.vector.tensor_copy(out=ident_bf[:], in_=ident[:])
         perms = const.tile([P, NODES, TILE_GRAPHS, NODES], F32)
@@ -109,6 +127,10 @@ def tile_graphdynamics_pa_t_kernel(tc, xi_p, xj_p, node_mask, mb1, mw2, mb2, out
         )
         neg_rest = const.tile([P, TILES - 1], F32)
         mb1_all = const.tile([P, H], BF16)
+
+        pick_rows = const.tile([P, 2, len(SET_STARTS), K_PASS], BF16)
+        picks = const.tile([P, GROUPS, TILES, P], BF16)
+        mask_row = const.tile([P, GRAPHS, NODES], BF16)
 
         recv_rows = {}
         send_rows = {}
@@ -133,11 +155,10 @@ def tile_graphdynamics_pa_t_kernel(tc, xi_p, xj_p, node_mask, mb1, mw2, mb2, out
             recv_rows[r] = [prep.tile([P, K_PASS], F32, name="recv_rows%d" % c) for c in range(PASSES)]
 
         def add_receivers(r, c):
-            for t in range(PACK):
-                cols = slice(c * K_PASS + t * P, c * K_PASS + (t + 1) * P)
-                nc.gpsimd.tensor_tensor(
-                    out=recv_rows[r][c][:, t_slice(t)], in0=xi_sb[r][:, cols], in1=mb1_all[:, cols], op=ADD
-                )
+            nc.vector.memset(recv_rows[r][c][:, 0:1], 0.0)
+            nc.gpsimd.tensor_tensor(
+                out=recv_rows[r][c][:], in0=xi_sb[r][:, pass_slice(c)], in1=mb1_all[:, pass_slice(c)], op=ADD
+            )
 
         def mask_senders(r, c, dtype):
             send = prep.tile([P, K_PASS], dtype, name="send_f32_%d" % c if dtype == F32 else "send_bf16")
@@ -162,6 +183,83 @@ def tile_graphdynamics_pa_t_kernel(tc, xi_p, xj_p, node_mask, mb1, mw2, mb2, out
                     in_=send_ps[:].rearrange("p t (b j) -> p b j t", j=NODES),
                 )
 
+        def load_pick_rows(r):
+            for s, start in enumerate(SET_STARTS):
+                first = r * P + start * NODES
+                for part, source in ((0, xi_rows), (SET_ROWS, xj_rows)):
+                    nc.sync.dma_start(
+                        out=pick_rows[part : part + SET_ROWS, r % 2, s, :],
+                        in_=source[first : first + SET_ROWS, pass_slice(0)],
+                    )
+
+        def last_pick_rows():
+            column = const.tile([P, 1], F32, name="masked_column")
+            nc.vector.tensor_scalar(
+                out=column[low, :], in0=ident[low, ROW_MASK : ROW_MASK + 1], scalar1=-MASKED, scalar2=0.0,
+                op0=MULT, op1=ADD,
+            )
+            nc.vector.tensor_scalar(
+                out=pick_rows[low, :, :, :].rearrange("p u s (t k) -> p (u s t) k", k=P),
+                in0=ident_bf[low, :].unsqueeze(1).to_broadcast([P - ROW_MB1, 2 * len(SET_STARTS) * PACK, P]),
+                scalar1=0.0, scalar2=column[low, :], op0=MULT, op1=ADD,
+            )
+            nc.sync.dma_start(
+                out=pick_rows[ROW_MB1 : ROW_MB1 + 1, :, :, :].rearrange("p u s k -> p (u s) k"),
+                in_=mb1[pass_slice(0)].unsqueeze(0).unsqueeze(0).to_broadcast([1, 2 * len(SET_STARTS), K_PASS]),
+            )
+
+        def make_picks(group):
+            q = group * ROTS + PICKED
+            base = const.tile([P, P], BF16, name="pick_base%d" % group)
+            for start, (first, last) in zip(SET_STARTS, SET_COLS):
+                graphs = slice(first // NODES - start, last // NODES - start)
+                senders = slice(3 + graphs.start, 3 + graphs.stop)
+                nc.vector.tensor_tensor(
+                    out=base[:, first:last].rearrange("p (b i) -> p b i", i=NODES),
+                    in0=ident_blocks[:, graphs, :], in1=perms[:, q, senders, :], op=ADD,
+                )
+            nc.vector.tensor_copy(out=picks[:, group, :, :], in_=base[:].unsqueeze(1).to_broadcast([P, TILES, P]))
+
+        def load_mask_row():
+            nc.sync.dma_start(
+                out=mask_row[low, :, :].rearrange("p b j -> p (b j)"),
+                in_=node_mask.rearrange("b j -> (b j)").partition_broadcast(P - ROW_MB1),
+            )
+            nc.gpsimd.tensor_scalar(
+                out=minus_mask[low, :], in0=ident[low, ROW_MASK : ROW_MASK + 1], scalar1=-1.0, scalar2=0.0,
+                op0=MULT, op1=ADD,
+            )
+            nc.gpsimd.tensor_tensor(
+                out=low_ones[low, :], in0=ident[low, ROW_MB1 : ROW_MB1 + 1],
+                in1=ident[low, ROW_MASK : ROW_MASK + 1], op=ADD,
+            )
+
+        def mask_picks(group):
+            q = group * ROTS + PICKED
+            low_picks = picks[low, group, :, :].rearrange("p r (b i) -> p (r b) i", i=NODES)
+            for to, source in ((slice(0, NODES - q), slice(q, NODES)), (slice(NODES - q, NODES), slice(0, q))):
+                nc.gpsimd.tensor_scalar(
+                    out=low_picks[:, :, to], in0=mask_row[low, :, source],
+                    scalar1=minus_mask[low, :], scalar2=low_ones[low, :], op0=MULT, op1=ADD,
+                )
+
+        low = slice(ROW_MB1, P)
+        minus_mask = const.tile([P, 1], F32)
+        low_ones = const.tile([P, 1], F32)
+
+        def is_picked(n, ql):
+            r, group = divmod(n, GROUPS)
+            return ql == PICKED and PICKED_FROM <= n < PICKED_FROM + PICKED_SUMS
+
+        def picked_sum(n, pair_ps):
+            r, group = divmod(n, GROUPS)
+            for t in range(PACK):
+                for s, (first, last) in enumerate(SET_COLS):
+                    nc.tensor.matmul(
+                        out=pair_ps[:, t, first:last], lhsT=pick_rows[:, r % 2, s, t_slice(t)],
+                        rhs=picks[:, group, r, first:last], start=True, stop=True,
+                    )
+
         def new_h(n):
             h[n] = [hidden.tile([P, ROTS, P, PACK], BF16, name="h%d" % c, align_bytes=64) for c in range(PASSES)]
 
@@ -169,7 +267,10 @@ def tile_graphdynamics_pa_t_kernel(tc, xi_p, xj_p, node_mask, mb1, mw2, mb2, out
             r, group = divmod(n, GROUPS)
             q = group * ROTS + ql
             pair_ps = ps_pair.tile([P, PACK, P], F32, name="pair_ps", tag="pair")
-            for t in range(PACK):
+            picked = c == 0 and is_picked(n, ql)
+            if picked:
+                picked_sum(n, pair_ps)
+            for t in range(0 if picked else PACK):
                 nc.tensor.matmul(
                     out=pair_ps[:, t, :], lhsT=recv_rows[r][c][:, t_slice(t)], rhs=ident[:],
                     is_transpose=True, start=True, stop=False,
@@ -244,17 +345,20 @@ def tile_graphdynamics_pa_t_kernel(tc, xi_p, xj_p, node_mask, mb1, mw2, mb2, out
             r, group = divmod(n, GROUPS)
             if group == 0 and first == 0:
                 sums[r] = ps_out.tile([P, D], F32, name="out_ps")
+                nc.tensor.matmul(
+                    out=sums[r][:],
+                    lhsT=correction[:, r * TILE_GRAPHS : (r + 1) * TILE_GRAPHS, :].rearrange("d b i -> d (b i)"),
+                    rhs=ident[:], is_transpose=True, start=True, stop=False,
+                )
             for ql in range(first, last):
                 nc.tensor.matmul(
                     out=sums[r][:], lhsT=msgs[n][:, ql, :], rhs=ident[:], is_transpose=True,
-                    start=(group == 0 and ql == 0), stop=(group == GROUPS - 1 and ql == ROTS - 1),
+                    start=False, stop=(group == GROUPS - 1 and ql == ROTS - 1),
                 )
 
         def finish(r):
             out_sb = tail.tile([P, D], F32, name="out_sb", bufs=2)
-            nc.vector.scalar_tensor_tensor(
-                out=out_sb[:], in0=relu_mb2[:], scalar=minus_masked[:, r : r + 1], in1=sums[r][:], op0=MULT, op1=ADD
-            )
+            nc.scalar.copy(out=out_sb[:], in_=sums[r][:])
             nc.sync.dma_start(out=out_rows[r * P : (r + 1) * P, :], in_=out_sb[:])
 
         mb1_ps = [
@@ -276,29 +380,33 @@ def tile_graphdynamics_pa_t_kernel(tc, xi_p, xj_p, node_mask, mb1, mw2, mb2, out
             out=send_rows[(0, 0, F32)][:], in0=xj_sb[0][:, pass_slice(0)], scalar1=mask_bias(0), scalar2=0.0,
             op0=ADD, op1=ADD,
         )
+        for warm_up in range(2):
+            keep_busy(2 * P)
         spread_mb1(1)
         first_receivers(1)
         turn_senders(0)
         spread_mb1(0)
         first_receivers(0)
+        keep_busy(P)
         turn_receivers(0)
         make_perms(ROTS, NODES)
+        nc.vector.tensor_scalar(
+            out=neg_rest[:], in0=mask_rest[:], scalar1=-1.0, scalar2=MASKED, op0=ADD, op1=MULT
+        )
 
         w_grouped = const.tile([P, PASSES, D, PACK], BF16, align_bytes=64)
         mb2_col = const.tile([P, 1], F32)
         w_codes = const.tile([P, PASSES * D], U32, align_bytes=64)
         w_scales = const.tile([P, PASSES * D], U8, align_bytes=64)
-        relu_mb2 = const.tile([P, D], F32)
-        minus_masked = const.tile([P, TILES], F32)
-        minus_one = const.tile([P, TILES], BF16)
+        relu_mb2 = const.tile([P, 1], F32)
+        masked_blocks = const.tile([P, TILES, TILE_GRAPHS], BF16)
+        excess = const.tile([P, GRAPHS], F32)
+        correction = const.tile([P, GRAPHS, NODES], F32)
+        minus_one = const.tile([P, TILES], F32)
         block_rows = const.tile([P, TILE_GRAPHS], F32)
-        block_ones = const.tile([P, TILE_GRAPHS, NODES], BF16)
 
         def late_constants():
             nc.vector.tensor_copy(out=w_grouped[:], in_=w_raw[:].rearrange("p c t d -> p c d t"))
-            nc.vector.tensor_scalar(
-                out=neg_rest[:], in0=mask_rest[:], scalar1=-1.0, scalar2=MASKED, op0=ADD, op1=MULT
-            )
             nc.vector.tensor_copy(out=mb2_col[:], in_=mb2_bf[:])
             nc.vector.quantize_mx(
                 out=w_codes[:].bitcast(FP8X4),
@@ -312,24 +420,24 @@ def tile_graphdynamics_pa_t_kernel(tc, xi_p, xj_p, node_mask, mb1, mw2, mb2, out
             nc.vector.tensor_scalar_add(out=minus_one[:, 0:1], in0=mask_first[:], scalar1=-1.0)
             nc.vector.tensor_scalar_add(out=minus_one[:, 1:TILES], in0=mask_rest[:], scalar1=-1.0)
             nc.vector.tensor_reduce(out=block_rows[:], in_=ident_blocks, axis=mybir.AxisListType.X, op=ADD)
-            nc.vector.tensor_copy(
-                out=block_ones[:], in_=block_rows[:].unsqueeze(2).to_broadcast([P, TILE_GRAPHS, NODES])
-            )
+            for r in range(TILES):
+                nc.vector.tensor_scalar_mul(
+                    out=masked_blocks[:, r, :], in0=block_rows[:], scalar1=minus_one[:, r : r + 1]
+                )
 
         def correction_sums():
-            vec_ps = ps_pair.tile([P, D + TILES], F32, name="vec_ps", tag="pair")
+            count_ps = ps_pair.tile([P, GRAPHS], F32, name="count_ps", tag="pair")
             nc.tensor.matmul(
-                out=vec_ps[:, 0:D], lhsT=ones[:], rhs=vec_row[:, H : H + D], start=True, stop=True
+                out=count_ps[:], lhsT=ones[:], rhs=masked_blocks[:].rearrange("p r b -> p (r b)"), start=True, stop=True
             )
-            nc.tensor.matmul(
-                out=vec_ps[:, D : D + TILES], lhsT=block_ones[:].rearrange("p b j -> p (b j)"), rhs=minus_one[:],
-                start=True, stop=True,
-            )
-            return vec_ps
+            return count_ps
 
-        def correction_constants(vec_ps):
-            nc.scalar.activation(out=relu_mb2[:], in_=vec_ps[:, 0:D], func=RELU)
-            nc.scalar.copy(out=minus_masked[:], in_=vec_ps[:, D : D + TILES])
+        def correction_constants(count_ps):
+            nc.scalar.activation(out=relu_mb2[:], in_=mb2_col[:], func=RELU)
+            nc.scalar.activation(
+                out=excess[:], in_=count_ps[:], func=mybir.ActivationFunctionType.Copy, scale=relu_mb2[:]
+            )
+            nc.scalar.copy(out=correction[:], in_=excess[:].unsqueeze(2).to_broadcast([P, GRAPHS, NODES]))
 
         groups = TILES * GROUPS
 
@@ -339,43 +447,51 @@ def tile_graphdynamics_pa_t_kernel(tc, xi_p, xj_p, node_mask, mb1, mw2, mb2, out
         for n in range(groups):
             r, group = divmod(n, GROUPS)
             if n == 3:
-                correction_constants(vec_ps)
-            if n - 5 >= 0 and (n - 5) % GROUPS == GROUPS - 1:
-                finish((n - 5) // GROUPS)
+                correction_constants(count_ps)
             new_h(n)
             if n >= 3:
                 finish_msgs(n - 3)
+            if n - 5 >= 0 and (n - 5) % GROUPS == GROUPS - 1:
+                finish((n - 5) // GROUPS)
             psum_sum(n, 0, 0)
             psum_sum(n, 0, 1)
             if n >= 1:
                 scalar_relu(n - 1, VECTOR_RELUS, ROTS)
             psum_sum(n, 0, 2)
             psum_sum(n, 0, 3)
-            own_sum(n, 0)
-            if n >= 1:
-                vector_relu(n - 1, 0, VECTOR_RELUS)
-            for ql in range(OWN_ROTS, ROTS, OWN_ROTS):
+            for ql in range(0, ROTS, OWN_ROTS):
                 if ql < own_rotations(n):
                     own_sum(n, ql)
                 else:
                     for q in range(OWN_ROTS):
                         psum_sum(n, 1, ql + q)
             if n >= 1:
+                vector_relu(n - 1, 0, VECTOR_RELUS)
                 quantise(n - 1, 0)
                 quantise(n - 1, 1)
             if n == 0:
                 late_constants()
-            if n == 1:
+                new_receivers(1)
+                add_receivers(1, 1)
                 graph_blocks()
+            if n == 1:
+                last_pick_rows()
+                for r_picked in (2, 3):
+                    load_pick_rows(r_picked)
+                load_mask_row()
             if n == 2:
-                vec_ps = correction_sums()
+                count_ps = correction_sums()
             if n >= 4:
                 add_up(n - 4)
+            early = (n + 1) // GROUPS + 1
+            if (n + 1) % GROUPS == 0 and early < TILES:
+                new_receivers(early)
+                add_receivers(early, 1)
             if r + 1 < TILES:
                 if group == 0:
-                    new_receivers(r + 1)
-                    add_receivers(r + 1, 1)
                     mask_senders(r + 1, 1, BF16)
+                    if r > 2:
+                        load_pick_rows(r + 1)
                     add_receivers(r + 1, 0)
                 if group == 1:
                     mask_senders(r + 1, 0, F32)
@@ -384,13 +500,18 @@ def tile_graphdynamics_pa_t_kernel(tc, xi_p, xj_p, node_mask, mb1, mw2, mb2, out
                 if group == 2:
                     turn_senders(r + 1)
                     turn_receivers(r + 1)
+            if 2 <= n < 2 + GROUPS:
+                make_picks(n - 2)
+                mask_picks(n - 2)
             if n >= 2:
                 multiply(n - 2)
+            else:
+                keep_busy(2 * P)
 
         last = groups - 1
         halves = ((0, ROTS // 2), (ROTS // 2, ROTS))
-        finish(TILES - 2)
         finish_msgs(last - 2)
+        finish(TILES - 2)
         vector_relu(last, 0, own_rotations(last))
         for first, end in halves:
             quantise(last, 0, first, end)

@@ -26,12 +26,6 @@ N_TILE = ROTS * P
 MASKED = 2.0**126
 
 VECTOR_RELUS = 3
-SET_STARTS = (0, 3, 5)
-SET_COLS = ((0, 48), (48, 96), (96, 128))
-SET_ROWS = 3 * NODES
-ROW_MB1, ROW_MASK = 2 * SET_ROWS, 2 * SET_ROWS + 1
-PICKED = 2
-PICKED_FROM, PICKED_SUMS = 8, 20
 OWN_ROTS = 2
 PITCH = NODES + 1
 PERIODS = -(-(NODES - OWN_ROTS + OWN_ROTS * PITCH) // NODES)
@@ -128,10 +122,6 @@ def tile_graphdynamics_pa_t_kernel(tc, xi_p, xj_p, node_mask, mb1, mw2, mb2, out
         neg_rest = const.tile([P, TILES - 1], F32)
         mb1_all = const.tile([P, H], BF16)
 
-        pick_rows = const.tile([P, 2, len(SET_STARTS), K_PASS], BF16)
-        picks = const.tile([P, GROUPS, TILES, P], BF16)
-        mask_row = const.tile([P, GRAPHS, NODES], BF16)
-
         recv_rows = {}
         send_rows = {}
         recv_ps = {}
@@ -183,83 +173,6 @@ def tile_graphdynamics_pa_t_kernel(tc, xi_p, xj_p, node_mask, mb1, mw2, mb2, out
                     in_=send_ps[:].rearrange("p t (b j) -> p b j t", j=NODES),
                 )
 
-        def load_pick_rows(r):
-            for s, start in enumerate(SET_STARTS):
-                first = r * P + start * NODES
-                for part, source in ((0, xi_rows), (SET_ROWS, xj_rows)):
-                    nc.sync.dma_start(
-                        out=pick_rows[part : part + SET_ROWS, r % 2, s, :],
-                        in_=source[first : first + SET_ROWS, pass_slice(0)],
-                    )
-
-        def last_pick_rows():
-            column = const.tile([P, 1], F32, name="masked_column")
-            nc.vector.tensor_scalar(
-                out=column[low, :], in0=ident[low, ROW_MASK : ROW_MASK + 1], scalar1=-MASKED, scalar2=0.0,
-                op0=MULT, op1=ADD,
-            )
-            nc.vector.tensor_scalar(
-                out=pick_rows[low, :, :, :].rearrange("p u s (t k) -> p (u s t) k", k=P),
-                in0=ident_bf[low, :].unsqueeze(1).to_broadcast([P - ROW_MB1, 2 * len(SET_STARTS) * PACK, P]),
-                scalar1=0.0, scalar2=column[low, :], op0=MULT, op1=ADD,
-            )
-            nc.sync.dma_start(
-                out=pick_rows[ROW_MB1 : ROW_MB1 + 1, :, :, :].rearrange("p u s k -> p (u s) k"),
-                in_=mb1[pass_slice(0)].unsqueeze(0).unsqueeze(0).to_broadcast([1, 2 * len(SET_STARTS), K_PASS]),
-            )
-
-        def make_picks(group):
-            q = group * ROTS + PICKED
-            base = const.tile([P, P], BF16, name="pick_base%d" % group)
-            for start, (first, last) in zip(SET_STARTS, SET_COLS):
-                graphs = slice(first // NODES - start, last // NODES - start)
-                senders = slice(3 + graphs.start, 3 + graphs.stop)
-                nc.vector.tensor_tensor(
-                    out=base[:, first:last].rearrange("p (b i) -> p b i", i=NODES),
-                    in0=ident_blocks[:, graphs, :], in1=perms[:, q, senders, :], op=ADD,
-                )
-            nc.vector.tensor_copy(out=picks[:, group, :, :], in_=base[:].unsqueeze(1).to_broadcast([P, TILES, P]))
-
-        def load_mask_row():
-            nc.sync.dma_start(
-                out=mask_row[low, :, :].rearrange("p b j -> p (b j)"),
-                in_=node_mask.rearrange("b j -> (b j)").partition_broadcast(P - ROW_MB1),
-            )
-            nc.gpsimd.tensor_scalar(
-                out=minus_mask[low, :], in0=ident[low, ROW_MASK : ROW_MASK + 1], scalar1=-1.0, scalar2=0.0,
-                op0=MULT, op1=ADD,
-            )
-            nc.gpsimd.tensor_tensor(
-                out=low_ones[low, :], in0=ident[low, ROW_MB1 : ROW_MB1 + 1],
-                in1=ident[low, ROW_MASK : ROW_MASK + 1], op=ADD,
-            )
-
-        def mask_picks(group):
-            q = group * ROTS + PICKED
-            low_picks = picks[low, group, :, :].rearrange("p r (b i) -> p (r b) i", i=NODES)
-            for to, source in ((slice(0, NODES - q), slice(q, NODES)), (slice(NODES - q, NODES), slice(0, q))):
-                nc.gpsimd.tensor_scalar(
-                    out=low_picks[:, :, to], in0=mask_row[low, :, source],
-                    scalar1=minus_mask[low, :], scalar2=low_ones[low, :], op0=MULT, op1=ADD,
-                )
-
-        low = slice(ROW_MB1, P)
-        minus_mask = const.tile([P, 1], F32)
-        low_ones = const.tile([P, 1], F32)
-
-        def is_picked(n, ql):
-            r, group = divmod(n, GROUPS)
-            return ql == PICKED and PICKED_FROM <= n < PICKED_FROM + PICKED_SUMS
-
-        def picked_sum(n, pair_ps):
-            r, group = divmod(n, GROUPS)
-            for t in range(PACK):
-                for s, (first, last) in enumerate(SET_COLS):
-                    nc.tensor.matmul(
-                        out=pair_ps[:, t, first:last], lhsT=pick_rows[:, r % 2, s, t_slice(t)],
-                        rhs=picks[:, group, r, first:last], start=True, stop=True,
-                    )
-
         def new_h(n):
             h[n] = [hidden.tile([P, ROTS, P, PACK], BF16, name="h%d" % c, align_bytes=64) for c in range(PASSES)]
 
@@ -267,10 +180,7 @@ def tile_graphdynamics_pa_t_kernel(tc, xi_p, xj_p, node_mask, mb1, mw2, mb2, out
             r, group = divmod(n, GROUPS)
             q = group * ROTS + ql
             pair_ps = ps_pair.tile([P, PACK, P], F32, name="pair_ps", tag="pair")
-            picked = c == 0 and is_picked(n, ql)
-            if picked:
-                picked_sum(n, pair_ps)
-            for t in range(0 if picked else PACK):
+            for t in range(PACK):
                 nc.tensor.matmul(
                     out=pair_ps[:, t, :], lhsT=recv_rows[r][c][:, t_slice(t)], rhs=ident[:],
                     is_transpose=True, start=True, stop=False,
@@ -474,11 +384,6 @@ def tile_graphdynamics_pa_t_kernel(tc, xi_p, xj_p, node_mask, mb1, mw2, mb2, out
                 new_receivers(1)
                 add_receivers(1, 1)
                 graph_blocks()
-            if n == 1:
-                last_pick_rows()
-                for r_picked in (2, 3):
-                    load_pick_rows(r_picked)
-                load_mask_row()
             if n == 2:
                 count_ps = correction_sums()
             if n >= 4:
@@ -490,8 +395,6 @@ def tile_graphdynamics_pa_t_kernel(tc, xi_p, xj_p, node_mask, mb1, mw2, mb2, out
             if r + 1 < TILES:
                 if group == 0:
                     mask_senders(r + 1, 1, BF16)
-                    if r > 2:
-                        load_pick_rows(r + 1)
                     add_receivers(r + 1, 0)
                 if group == 1:
                     mask_senders(r + 1, 0, F32)
@@ -500,9 +403,6 @@ def tile_graphdynamics_pa_t_kernel(tc, xi_p, xj_p, node_mask, mb1, mw2, mb2, out
                 if group == 2:
                     turn_senders(r + 1)
                     turn_receivers(r + 1)
-            if 2 <= n < 2 + GROUPS:
-                make_picks(n - 2)
-                mask_picks(n - 2)
             if n >= 2:
                 multiply(n - 2)
             else:

@@ -25,7 +25,7 @@ GROUPS = NODES // ROTS
 N_TILE = ROTS * P
 MASKED = 2.0**126
 
-VECTOR_RELUS = 3
+VECTOR_RELUS = 4
 OWN_ROTS = 2
 PITCH = NODES + 1
 PERIODS = -(-(NODES - OWN_ROTS + OWN_ROTS * PITCH) // NODES)
@@ -48,8 +48,7 @@ def tile_graphdynamics_pa_t_kernel(tc, xi_p, xj_p, node_mask, mb1, mw2, mb2, out
         tail = ctx.enter_context(tc.tile_pool(name="tail", bufs=4))
         ps_pair = ctx.enter_context(tc.psum_pool(name="ps_pair", bufs=4))
         ps_recv = ctx.enter_context(tc.psum_pool(name="ps_recv", bufs=2))
-        ps_acc = ctx.enter_context(tc.psum_pool(name="ps_acc", bufs=1))
-        ps_out = ctx.enter_context(tc.psum_pool(name="ps_out", bufs=1))
+        ps_acc = ctx.enter_context(tc.psum_pool(name="ps_acc", bufs=2))
         ctx.enter_context(tc.manual_schedule())
 
         vec_row = const.tile([P, H], BF16)
@@ -95,30 +94,23 @@ def tile_graphdynamics_pa_t_kernel(tc, xi_p, xj_p, node_mask, mb1, mw2, mb2, out
         ident_blocks = ident[:].rearrange("p (b j) -> p b j", j=NODES)
         ones = const.tile([P, P], BF16)
         nc.vector.memset(ones[:], 1.0)
-        idle = const.tile([P, 2 * P], F32)
-        nc.vector.memset(idle[:], 0.0)
-
-        def keep_busy(columns):
-            idle_ps = ps_pair.tile([P, 2 * P], F32, name="idle_ps", tag="pair")
-            nc.tensor.matmul(
-                out=idle_ps[:, 0:columns], lhsT=idle[:, 0:P], rhs=idle[:, 0:columns], start=True, stop=True
-            )
-
         ident_bf = const.tile([P, P], BF16)
         nc.vector.tensor_copy(out=ident_bf[:], in_=ident[:])
         perms = const.tile([P, NODES, TILE_GRAPHS, NODES], F32)
 
-        def make_perms(first, last):
-            for q in range(first, last):
-                nc.vector.tensor_copy(out=perms[:, q, :, 0 : NODES - q], in_=ident_blocks[:, :, q:NODES])
-                if q:
-                    nc.vector.tensor_copy(out=perms[:, q, :, NODES - q : NODES], in_=ident_blocks[:, :, 0:q])
+        def turned_identity(q):
+            for to, source in ((slice(0, NODES - q), slice(q, NODES)), (slice(NODES - q, NODES), slice(0, q))):
+                if q or to.start == 0:
+                    nc.vector.tensor_copy(out=perms[:, q, :, to], in_=ident_blocks[:, :, source])
 
-        make_perms(0, ROTS)
+        for q in range(ROTS):
+            turned_identity(q)
         neg_first = const.tile([P, 1], F32)
         nc.vector.tensor_scalar(
             out=neg_first[:], in0=mask_first[:], scalar1=-1.0, scalar2=MASKED, op0=ADD, op1=MULT
         )
+        for q in range(ROTS, 2 * ROTS):
+            turned_identity(q)
         neg_rest = const.tile([P, TILES - 1], F32)
         mb1_all = const.tile([P, H], BF16)
 
@@ -130,6 +122,7 @@ def tile_graphdynamics_pa_t_kernel(tc, xi_p, xj_p, node_mask, mb1, mw2, mb2, out
         codes = {}
         accs = {}
         msgs = {}
+        half_sums = {}
         sums = {}
 
         def t_slice(t):
@@ -141,13 +134,16 @@ def tile_graphdynamics_pa_t_kernel(tc, xi_p, xj_p, node_mask, mb1, mw2, mb2, out
         def mask_bias(r):
             return neg_first[:] if r == 0 else neg_rest[:, r - 1 : r]
 
-        def new_receivers(r):
-            recv_rows[r] = [prep.tile([P, K_PASS], F32, name="recv_rows%d" % c) for c in range(PASSES)]
+        def new_receivers(r, c):
+            recv_rows[(r, c)] = prep.tile([P, K_PASS], F32, name="recv_rows%d" % c)
 
-        def add_receivers(r, c):
-            nc.vector.memset(recv_rows[r][c][:, 0:1], 0.0)
+        def add_receivers(r, c, half):
+            cols = slice(half * K_PASS // 2, (half + 1) * K_PASS // 2)
+            if r == 1:
+                nc.vector.memset(recv_rows[(r, c)][:, cols.start : cols.start + 1], 0.0)
+            source = slice(c * K_PASS + cols.start, c * K_PASS + cols.stop)
             nc.gpsimd.tensor_tensor(
-                out=recv_rows[r][c][:], in0=xi_sb[r][:, pass_slice(c)], in1=mb1_all[:, pass_slice(c)], op=ADD
+                out=recv_rows[(r, c)][:, cols], in0=xi_sb[r][:, source], in1=mb1_all[:, source], op=ADD
             )
 
         def mask_senders(r, c, dtype):
@@ -160,7 +156,7 @@ def tile_graphdynamics_pa_t_kernel(tc, xi_p, xj_p, node_mask, mb1, mw2, mb2, out
         def turn_receivers(r):
             recv_ps[r] = ps_recv.tile([P, PACK, P], F32, name="recv_ps", tag="recv")
             for t in range(PACK):
-                nc.tensor.transpose(recv_ps[r][:, t, :], recv_rows[r][1][:, t_slice(t)], ident[:])
+                nc.tensor.transpose(recv_ps[r][:, t, :], recv_rows[(r, 1)][:, t_slice(t)], ident[:])
 
         def turn_senders(r):
             send_ps = ps_pair.tile([P, PACK, P], BF16, name="send_ps", tag="pair")
@@ -182,7 +178,7 @@ def tile_graphdynamics_pa_t_kernel(tc, xi_p, xj_p, node_mask, mb1, mw2, mb2, out
             pair_ps = ps_pair.tile([P, PACK, P], F32, name="pair_ps", tag="pair")
             for t in range(PACK):
                 nc.tensor.matmul(
-                    out=pair_ps[:, t, :], lhsT=recv_rows[r][c][:, t_slice(t)], rhs=ident[:],
+                    out=pair_ps[:, t, :], lhsT=recv_rows[(r, c)][:, t_slice(t)], rhs=ident[:],
                     is_transpose=True, start=True, stop=False,
                 )
                 nc.tensor.matmul(
@@ -245,25 +241,34 @@ def tile_graphdynamics_pa_t_kernel(tc, xi_p, xj_p, node_mask, mb1, mw2, mb2, out
 
         def finish_msgs(n, first=0, last=ROTS):
             if first == 0:
-                msgs[n] = tail.tile([P, ROTS, P], F32, name="msg")
+                msgs[n] = tail.tile([P, ROTS, P], F32, name="msg", bufs=6)
             nc.scalar.activation(
                 out=msgs[n][:, first:last, :].rearrange("d q r -> d (q r)"), in_=accs[n][:, first * P : last * P],
                 func=RELU, bias=mb2_col[:], scale=1.0,
             )
 
-        def add_up(n, first=0, last=ROTS):
-            r, group = divmod(n, GROUPS)
-            if group == 0 and first == 0:
-                sums[r] = ps_out.tile([P, D], F32, name="out_ps")
+        def sum_msgs(n):
+            half_sums[n] = tail.tile([P, ROTS // 2, P], F32, name="half_sum", bufs=8)
+            nc.vector.memset(half_sums[n][:, 0, 0:1], 0.0)
+            nc.gpsimd.tensor_tensor(
+                out=half_sums[n][:], in0=msgs[n][:, 0 : ROTS // 2, :], in1=msgs[n][:, ROTS // 2 : ROTS, :], op=ADD
+            )
+
+        def add_up(r, first=0, last=GROUPS):
+            sources = []
+            if first == 0:
+                sums[r] = ps_pair.tile([P, D], F32, name="out_ps", tag="pair")
+                graphs = slice(r * TILE_GRAPHS, (r + 1) * TILE_GRAPHS)
+                sources.append(correction[:, graphs, :].rearrange("d b i -> d (b i)"))
+            for n in range(r * GROUPS + first, r * GROUPS + last):
+                if n in half_sums:
+                    sources.extend([half_sums[n][:, ql, :] for ql in range(ROTS // 2)])
+                else:
+                    sources.extend([msgs[n][:, ql, :] for ql in range(ROTS)])
+            for index, source in enumerate(sources):
                 nc.tensor.matmul(
-                    out=sums[r][:],
-                    lhsT=correction[:, r * TILE_GRAPHS : (r + 1) * TILE_GRAPHS, :].rearrange("d b i -> d (b i)"),
-                    rhs=ident[:], is_transpose=True, start=True, stop=False,
-                )
-            for ql in range(first, last):
-                nc.tensor.matmul(
-                    out=sums[r][:], lhsT=msgs[n][:, ql, :], rhs=ident[:], is_transpose=True,
-                    start=False, stop=(group == GROUPS - 1 and ql == ROTS - 1),
+                    out=sums[r][:], lhsT=source, rhs=ident[:], is_transpose=True,
+                    start=(first == 0 and index == 0), stop=(last == GROUPS and index == len(sources) - 1),
                 )
 
         def finish(r):
@@ -273,33 +278,30 @@ def tile_graphdynamics_pa_t_kernel(tc, xi_p, xj_p, node_mask, mb1, mw2, mb2, out
 
         mb1_ps = [
             ps_acc.tile([P, K_PASS], F32, name="acc"),
-            ps_out.tile([P, K_PASS], F32, name="out_ps"),
+            ps_acc.tile([P, K_PASS], F32, name="acc"),
         ]
         def spread_mb1(c):
             nc.tensor.matmul(out=mb1_ps[c][:], lhsT=ones[:], rhs=vec_row[:, pass_slice(c)], start=True, stop=True)
 
         def first_receivers(c):
             nc.vector.tensor_tensor(
-                out=recv_rows[0][c][:], in0=xi_sb[0][:, pass_slice(c)], in1=mb1_ps[c][:], op=ADD
+                out=recv_rows[(0, c)][:], in0=xi_sb[0][:, pass_slice(c)], in1=mb1_ps[c][:], op=ADD
             )
 
-        new_receivers(0)
+        for c in range(PASSES):
+            new_receivers(0, c)
         mask_senders(0, 1, BF16)
         send_rows[(0, 0, F32)] = prep.tile([P, K_PASS], F32, name="send_f32_0")
         nc.gpsimd.tensor_scalar(
             out=send_rows[(0, 0, F32)][:], in0=xj_sb[0][:, pass_slice(0)], scalar1=mask_bias(0), scalar2=0.0,
             op0=ADD, op1=ADD,
         )
-        for warm_up in range(2):
-            keep_busy(2 * P)
         spread_mb1(1)
         first_receivers(1)
         turn_senders(0)
         spread_mb1(0)
         first_receivers(0)
-        keep_busy(P)
         turn_receivers(0)
-        make_perms(ROTS, NODES)
         nc.vector.tensor_scalar(
             out=neg_rest[:], in0=mask_rest[:], scalar1=-1.0, scalar2=MASKED, op0=ADD, op1=MULT
         )
@@ -316,15 +318,17 @@ def tile_graphdynamics_pa_t_kernel(tc, xi_p, xj_p, node_mask, mb1, mw2, mb2, out
         block_rows = const.tile([P, TILE_GRAPHS], F32)
 
         def late_constants():
-            nc.vector.tensor_copy(out=w_grouped[:], in_=w_raw[:].rearrange("p c t d -> p c d t"))
             nc.vector.tensor_copy(out=mb2_col[:], in_=mb2_bf[:])
+            for c in range(PASSES):
+                nc.scalar.copy(out=mb1_all[:, pass_slice(c)], in_=mb1_ps[c][:])
+            nc.scalar.copy(out=w_grouped[:], in_=w_raw[:].rearrange("p c t d -> p c d t"))
+
+        def quantise_weights():
             nc.vector.quantize_mx(
                 out=w_codes[:].bitcast(FP8X4),
                 scales=w_scales[:],
                 in_=w_grouped[:].rearrange("p c d t -> p (c d t)"),
             )
-            for c in range(PASSES):
-                nc.scalar.copy(out=mb1_all[:, pass_slice(c)], in_=mb1_ps[c][:])
 
         def graph_blocks():
             nc.vector.tensor_scalar_add(out=minus_one[:, 0:1], in0=mask_first[:], scalar1=-1.0)
@@ -359,14 +363,13 @@ def tile_graphdynamics_pa_t_kernel(tc, xi_p, xj_p, node_mask, mb1, mw2, mb2, out
             if n == 3:
                 correction_constants(count_ps)
             new_h(n)
-            if n >= 3:
+            if n >= 4 and n % 2 == 0:
+                finish_msgs(n - 4)
                 finish_msgs(n - 3)
-            if n - 5 >= 0 and (n - 5) % GROUPS == GROUPS - 1:
-                finish((n - 5) // GROUPS)
+            if n >= GROUPS + 6 and (n - 6) % GROUPS == 0:
+                finish((n - 6) // GROUPS - 1)
             psum_sum(n, 0, 0)
             psum_sum(n, 0, 1)
-            if n >= 1:
-                scalar_relu(n - 1, VECTOR_RELUS, ROTS)
             psum_sum(n, 0, 2)
             psum_sum(n, 0, 3)
             for ql in range(0, ROTS, OWN_ROTS):
@@ -379,23 +382,35 @@ def tile_graphdynamics_pa_t_kernel(tc, xi_p, xj_p, node_mask, mb1, mw2, mb2, out
                 vector_relu(n - 1, 0, VECTOR_RELUS)
                 quantise(n - 1, 0)
                 quantise(n - 1, 1)
+            if 4 <= n < groups - 2:
+                sum_msgs(n - 4)
             if n == 0:
+                for q in range(2 * ROTS, NODES):
+                    turned_identity(q)
                 late_constants()
-                new_receivers(1)
-                add_receivers(1, 1)
                 graph_blocks()
+            if n == 1:
+                quantise_weights()
             if n == 2:
                 count_ps = correction_sums()
-            if n >= 4:
-                add_up(n - 4)
-            early = (n + 1) // GROUPS + 1
-            if (n + 1) % GROUPS == 0 and early < TILES:
-                new_receivers(early)
-                add_receivers(early, 1)
+            if n >= GROUPS + 5 and (n - 5) % GROUPS == 0:
+                add_up((n - 5) // GROUPS - 1)
+            if n == 0:
+                new_receivers(1, 1)
+                for half in range(2):
+                    add_receivers(1, 1, half)
+            early = (n + 2) // GROUPS + 1
+            if group >= 2 and early < TILES:
+                if group == 2:
+                    new_receivers(early, 1)
+                add_receivers(early, 1, group - 2)
+            if group < 2 and r + 1 < TILES:
+                if group == 0:
+                    new_receivers(r + 1, 0)
+                add_receivers(r + 1, 0, group)
             if r + 1 < TILES:
                 if group == 0:
                     mask_senders(r + 1, 1, BF16)
-                    add_receivers(r + 1, 0)
                 if group == 1:
                     mask_senders(r + 1, 0, F32)
                     if r + 1 == TILES - 1:
@@ -403,28 +418,25 @@ def tile_graphdynamics_pa_t_kernel(tc, xi_p, xj_p, node_mask, mb1, mw2, mb2, out
                 if group == 2:
                     turn_senders(r + 1)
                     turn_receivers(r + 1)
-            if n >= 2:
+            if n >= 3 and n % 2:
+                multiply(n - 3)
                 multiply(n - 2)
-            else:
-                keep_busy(2 * P)
 
         last = groups - 1
         halves = ((0, ROTS // 2), (ROTS // 2, ROTS))
+        finish_msgs(last - 3)
         finish_msgs(last - 2)
-        finish(TILES - 2)
         vector_relu(last, 0, own_rotations(last))
         for first, end in halves:
             quantise(last, 0, first, end)
             quantise(last, 1, first, end)
-        add_up(last - 3)
+        add_up(TILES - 2)
+        finish(TILES - 2)
+        add_up(TILES - 1, 0, GROUPS - 2)
         multiply(last - 1)
         finish_msgs(last - 1)
-        add_up(last - 2)
         for first, end in halves:
             multiply(last, first, end)
-        add_up(last - 1)
-        for first, end in halves:
             finish_msgs(last, first, end)
-        for first, end in halves:
-            add_up(last, first, end)
+        add_up(TILES - 1, GROUPS - 2)
         finish(TILES - 1)

from contextlib import ExitStack

import concourse.mybir as mybir
from concourse.masks import make_identity

F32 = mybir.dt.float32
BF16 = mybir.dt.bfloat16
U32 = mybir.dt.uint32
U8 = mybir.dt.uint8
FP8X4 = mybir.dt.float8_e4m3fn_x4
ADD = mybir.AluOpType.add
MULT = mybir.AluOpType.mult
RELU = mybir.ActivationFunctionType.Relu
IDENTITY = mybir.ActivationFunctionType.Identity

GRAPHS, NODES, D, H = 64, 16, 128, 1024
P = 128
PACK = 4
K_PASS = P * PACK
PASSES = H // K_PASS
TILE_GRAPHS = P // NODES
TILES = GRAPHS // TILE_GRAPHS
ROTS = 4
GROUPS = NODES // ROTS
N_TILE = ROTS * P
MASKED = 2.0**126

VECTOR_RELUS = 4
OWN_ROTS = 2
PITCH = NODES + 1
PERIODS = -(-(NODES - OWN_ROTS + OWN_ROTS * PITCH) // NODES)

FLOPS = 2 * GRAPHS * NODES * NODES * H * D


def tile_graphdynamics_pa_t_kernel(tc, xi_p, xj_p, node_mask, mb1, mw2, mb2, out):
    nc = tc.nc
    xi_rows = xi_p.rearrange("b i k -> (b i) k")
    xj_rows = xj_p.rearrange("b j k -> (b j) k")
    out_rows = out.rearrange("b i d -> (b i) d")

    with ExitStack() as ctx:
        const = ctx.enter_context(tc.tile_pool(name="const", bufs=1))
        rows = ctx.enter_context(tc.tile_pool(name="rows", bufs=TILES))
        prep = ctx.enter_context(tc.tile_pool(name="prep", bufs=2))
        hidden = ctx.enter_context(tc.tile_pool(name="hidden", bufs=4))
        packed = ctx.enter_context(tc.tile_pool(name="packed", bufs=4))
        tail = ctx.enter_context(tc.tile_pool(name="tail", bufs=4))
        ps_pair = ctx.enter_context(tc.psum_pool(name="ps_pair", bufs=4))
        ps_recv = ctx.enter_context(tc.psum_pool(name="ps_recv", bufs=2))
        ps_acc = ctx.enter_context(tc.psum_pool(name="ps_acc", bufs=2))
        ctx.enter_context(tc.manual_schedule())

        vec_row = const.tile([P, H], BF16)
        nc.gpsimd.memset(vec_row[:, 0:K_PASS].bitcast(F32), 0.0)
        nc.vector.memset(vec_row[:, K_PASS:H].bitcast(F32), 0.0)
        warm = const.tile([P, 1], F32)
        nc.vector.memset(warm[:], 0.0)
        mask_first = const.tile([P, 1], BF16)
        mask_rest = const.tile([P, TILES - 1], BF16)
        mb2_bf = const.tile([P, 1], BF16)
        w_raw = const.tile([P, PASSES, PACK, D], BF16)
        with nc.allow_non_contiguous_dma(reason="vectors with one value a partition"):
            nc.scalar.dma_start(
                out=mask_first[:], in_=node_mask[0:TILE_GRAPHS, :].rearrange("b j -> (b j)").unsqueeze(1)
            )
            nc.scalar.dma_start(out=vec_row[0:1, 0:H], in_=mb1.unsqueeze(0))
            nc.scalar.activation(out=warm[:], in_=warm[:], func=IDENTITY, bias=0.0, scale=1.0)
        xi_sb = []
        xj_sb = []
        for r in range(TILES):
            xj_tile = rows.tile([P, H], BF16, name="xj_tile")
            xi_tile = rows.tile([P, H], BF16, name="xi_tile")
            pieces = PASSES if r == 0 else 1
            for piece in reversed(range(pieces)):
                cols = slice(piece * H // pieces, (piece + 1) * H // pieces)
                nc.sync.dma_start(out=xj_tile[:, cols], in_=xj_rows[r * P : (r + 1) * P, cols])
                nc.sync.dma_start(out=xi_tile[:, cols], in_=xi_rows[r * P : (r + 1) * P, cols])
            xi_sb.append(xi_tile)
            xj_sb.append(xj_tile)
            if r == 0:
                with nc.allow_non_contiguous_dma(reason="vectors with one value a partition"):
                    nc.sync.dma_start(
                        out=mask_rest[:],
                        in_=node_mask[TILE_GRAPHS:GRAPHS, :].rearrange("(r b) j -> (b j) r", b=TILE_GRAPHS),
                    )
                    nc.sync.dma_start(out=mb2_bf[:], in_=mb2.unsqueeze(1))
                    nc.sync.dma_start(
                        out=w_raw[:], in_=mw2.rearrange("(c t p) d -> p c t d", c=PASSES, t=PACK, p=P)
                    )

        ident = const.tile([P, P], F32)
        make_identity(nc, ident[:])
        ident_blocks = ident[:].rearrange("p (b j) -> p b j", j=NODES)
        ones = const.tile([P, P], BF16)
        nc.vector.memset(ones[:], 1.0)
        ident_bf = const.tile([P, P], BF16)
        nc.vector.tensor_copy(out=ident_bf[:], in_=ident[:])
        perms = const.tile([P, NODES, TILE_GRAPHS, NODES], F32)

        def turned_identity(q):
            for to, source in ((slice(0, NODES - q), slice(q, NODES)), (slice(NODES - q, NODES), slice(0, q))):
                if q or to.start == 0:
                    nc.vector.tensor_copy(out=perms[:, q, :, to], in_=ident_blocks[:, :, source])

        for q in range(ROTS):
            turned_identity(q)
        neg_first = const.tile([P, 1], F32)
        nc.vector.tensor_scalar(
            out=neg_first[:], in0=mask_first[:], scalar1=-1.0, scalar2=MASKED, op0=ADD, op1=MULT
        )
        for q in range(ROTS, 2 * ROTS):
            turned_identity(q)
        neg_rest = const.tile([P, TILES - 1], F32)
        mb1_all = const.tile([P, H], BF16)

        recv_rows = {}
        send_rows = {}
        recv_ps = {}
        send_t = {}
        h = {}
        codes = {}
        accs = {}
        msgs = {}
        half_sums = {}
        sums = {}

        def t_slice(t):
            return slice(t * P, (t + 1) * P)

        def pass_slice(c):
            return slice(c * K_PASS, (c + 1) * K_PASS)

        def mask_bias(r):
            return neg_first[:] if r == 0 else neg_rest[:, r - 1 : r]

        def new_receivers(r, c):
            recv_rows[(r, c)] = prep.tile([P, K_PASS], F32, name="recv_rows%d" % c)

        def add_receivers(r, c, half):
            cols = slice(half * K_PASS // 2, (half + 1) * K_PASS // 2)
            if r == 1:
                nc.vector.memset(recv_rows[(r, c)][:, cols.start : cols.start + 1], 0.0)
            source = slice(c * K_PASS + cols.start, c * K_PASS + cols.stop)
            nc.gpsimd.tensor_tensor(
                out=recv_rows[(r, c)][:, cols], in0=xi_sb[r][:, source], in1=mb1_all[:, source], op=ADD
            )

        def mask_senders(r, c, dtype):
            send = prep.tile([P, K_PASS], dtype, name="send_f32_%d" % c if dtype == F32 else "send_bf16")
            nc.scalar.activation(
                out=send[:], in_=xj_sb[r][:, pass_slice(c)], func=IDENTITY, bias=mask_bias(r), scale=1.0
            )
            send_rows[(r, c, dtype)] = send

        def turn_receivers(r):
            recv_ps[r] = ps_recv.tile([P, PACK, P], F32, name="recv_ps", tag="recv")
            for t in range(PACK):
                nc.tensor.transpose(recv_ps[r][:, t, :], recv_rows[(r, 1)][:, t_slice(t)], ident[:])

        def turn_senders(r):
            send_ps = ps_pair.tile([P, PACK, P], BF16, name="send_ps", tag="pair")
            for t in range(PACK):
                nc.tensor.transpose(send_ps[:, t, :], send_rows[(r, 1, BF16)][:, t_slice(t)], ident_bf[:])
            send_t[r] = prep.tile([P, TILE_GRAPHS, PERIODS * NODES, PACK], BF16, name="send_t")
            for copy in range(PERIODS):
                nc.scalar.copy(
                    out=send_t[r][:, :, copy * NODES : (copy + 1) * NODES, :],
                    in_=send_ps[:].rearrange("p t (b j) -> p b j t", j=NODES),
                )

        def new_h(n):
            h[n] = [hidden.tile([P, ROTS, P, PACK], BF16, name="h%d" % c, align_bytes=64) for c in range(PASSES)]

        def psum_sum(n, c, ql):
            r, group = divmod(n, GROUPS)
            q = group * ROTS + ql
            pair_ps = ps_pair.tile([P, PACK, P], F32, name="pair_ps", tag="pair")
            for t in range(PACK):
                nc.tensor.matmul(
                    out=pair_ps[:, t, :], lhsT=recv_rows[(r, c)][:, t_slice(t)], rhs=ident[:],
                    is_transpose=True, start=True, stop=False,
                )
                nc.tensor.matmul(
                    out=pair_ps[:, t, :], lhsT=send_rows[(r, c, F32)][:, t_slice(t)],
                    rhs=perms[:, q, :, :].rearrange("p b i -> p (b i)"),
                    is_transpose=True, start=False, stop=True,
                )
            nc.scalar.activation(
                out=h[n][c][:, ql, :, :], in_=pair_ps[:].rearrange("p t r -> p r t"), func=RELU
            )

        def own_sum(n, ql):
            r, group = divmod(n, GROUPS)
            q = group * ROTS + ql
            windows = send_t[r][:, :, q : q + OWN_ROTS * PITCH, :].rearrange("p b (q w) t -> p q b w t", w=PITCH)
            nc.vector.tensor_tensor(
                out=h[n][1][:, ql : ql + OWN_ROTS, :, :].rearrange("p q (b i) t -> p q b i t", i=NODES),
                in0=recv_ps[r][:].rearrange("p t (b i) -> p b i t", i=NODES)
                .unsqueeze(1)
                .to_broadcast([P, OWN_ROTS, TILE_GRAPHS, NODES, PACK]),
                in1=windows[:, :, :, 0:NODES, :],
                op=ADD,
            )

        def vector_relu(n, first, last):
            own = h[n][1][:, first:last, :, :].rearrange("p q r t -> p (q r t)")
            nc.vector.tensor_scalar_max(out=own, in0=own, scalar1=0.0)

        def scalar_relu(n, first, last):
            own = h[n][1][:, first:last, :, :].rearrange("p q r t -> p (q r t)")
            nc.scalar.activation(out=own, in_=own, func=RELU)

        def quantise(n, c, first=0, last=ROTS):
            if n not in codes:
                h_codes = packed.tile([P, PASSES, N_TILE], U32, name="h_codes", align_bytes=64)
                h_scales = packed.tile([P, PASSES, N_TILE], U8, name="h_scales", align_bytes=64)
                codes[n] = (h_codes, h_scales)
            h_codes, h_scales = codes[n]
            nc.vector.quantize_mx(
                out=h_codes[:, c, first * P : last * P].bitcast(FP8X4),
                scales=h_scales[:, c, first * P : last * P],
                in_=h[n][c][:, first:last, :, :].rearrange("p q r t -> p (q r t)"),
            )

        def multiply(n, first=0, last=ROTS):
            h_codes, h_scales = codes[n]
            if first == 0:
                accs[n] = ps_acc.tile([P, N_TILE], F32, name="acc")
            cols = slice(first * P, last * P)
            for c in range(PASSES):
                nc.tensor.matmul_mx(
                    out=accs[n][:, cols],
                    lhsT=w_codes[:, c * D : (c + 1) * D].bitcast(FP8X4),
                    lhsT_scale=w_scales[:, c * D : (c + 1) * D],
                    rhs=h_codes[:, c, cols].bitcast(FP8X4),
                    rhs_scale=h_scales[:, c, cols],
                    start=(c == 0),
                    stop=(c == PASSES - 1),
                )

        def finish_msgs(n, first=0, last=ROTS):
            if first == 0:
                msgs[n] = tail.tile([P, ROTS, P], F32, name="msg", bufs=6)
            nc.scalar.activation(
                out=msgs[n][:, first:last, :].rearrange("d q r -> d (q r)"), in_=accs[n][:, first * P : last * P],
                func=RELU, bias=mb2_col[:], scale=1.0,
            )

        def sum_msgs(n):
            half_sums[n] = tail.tile([P, ROTS // 2, P], F32, name="half_sum", bufs=8)
            nc.vector.memset(half_sums[n][:, 0, 0:1], 0.0)
            nc.gpsimd.tensor_tensor(
                out=half_sums[n][:], in0=msgs[n][:, 0 : ROTS // 2, :], in1=msgs[n][:, ROTS // 2 : ROTS, :], op=ADD
            )

        def add_up(r, first=0, last=GROUPS):
            sources = []
            if first == 0:
                sums[r] = ps_pair.tile([P, D], F32, name="out_ps", tag="pair")
                graphs = slice(r * TILE_GRAPHS, (r + 1) * TILE_GRAPHS)
                sources.append(correction[:, graphs, :].rearrange("d b i -> d (b i)"))
            for n in range(r * GROUPS + first, r * GROUPS + last):
                if n in half_sums:
                    sources.extend([half_sums[n][:, ql, :] for ql in range(ROTS // 2)])
                else:
                    sources.extend([msgs[n][:, ql, :] for ql in range(ROTS)])
            for index, source in enumerate(sources):
                nc.tensor.matmul(
                    out=sums[r][:], lhsT=source, rhs=ident[:], is_transpose=True,
                    start=(first == 0 and index == 0), stop=(last == GROUPS and index == len(sources) - 1),
                )

        def finish(r):
            out_sb = tail.tile([P, D], F32, name="out_sb", bufs=2)
            nc.scalar.copy(out=out_sb[:], in_=sums[r][:])
            nc.sync.dma_start(out=out_rows[r * P : (r + 1) * P, :], in_=out_sb[:])

        mb1_ps = [
            ps_acc.tile([P, K_PASS], F32, name="acc"),
            ps_acc.tile([P, K_PASS], F32, name="acc"),
        ]
        def spread_mb1(c):
            nc.tensor.matmul(out=mb1_ps[c][:], lhsT=ones[:], rhs=vec_row[:, pass_slice(c)], start=True, stop=True)

        def first_receivers(c):
            nc.vector.tensor_tensor(
                out=recv_rows[(0, c)][:], in0=xi_sb[0][:, pass_slice(c)], in1=mb1_ps[c][:], op=ADD
            )

        for c in range(PASSES):
            new_receivers(0, c)
        mask_senders(0, 1, BF16)
        send_rows[(0, 0, F32)] = prep.tile([P, K_PASS], F32, name="send_f32_0")
        nc.gpsimd.tensor_scalar(
            out=send_rows[(0, 0, F32)][:], in0=xj_sb[0][:, pass_slice(0)], scalar1=mask_bias(0), scalar2=0.0,
            op0=ADD, op1=ADD,
        )
        spread_mb1(1)
        first_receivers(1)
        turn_senders(0)
        spread_mb1(0)
        first_receivers(0)
        turn_receivers(0)
        nc.vector.tensor_scalar(
            out=neg_rest[:], in0=mask_rest[:], scalar1=-1.0, scalar2=MASKED, op0=ADD, op1=MULT
        )

        w_grouped = const.tile([P, PASSES, D, PACK], BF16, align_bytes=64)
        mb2_col = const.tile([P, 1], F32)
        w_codes = const.tile([P, PASSES * D], U32, align_bytes=64)
        w_scales = const.tile([P, PASSES * D], U8, align_bytes=64)
        relu_mb2 = const.tile([P, 1], F32)
        masked_blocks = const.tile([P, TILES, TILE_GRAPHS], BF16)
        excess = const.tile([P, GRAPHS], F32)
        correction = const.tile([P, GRAPHS, NODES], F32)
        minus_one = const.tile([P, TILES], F32)
        block_rows = const.tile([P, TILE_GRAPHS], F32)

        def late_constants():
            nc.vector.tensor_copy(out=mb2_col[:], in_=mb2_bf[:])
            for c in range(PASSES):
                nc.scalar.copy(out=mb1_all[:, pass_slice(c)], in_=mb1_ps[c][:])
            nc.scalar.copy(out=w_grouped[:], in_=w_raw[:].rearrange("p c t d -> p c d t"))

        def quantise_weights():
            nc.vector.quantize_mx(
                out=w_codes[:].bitcast(FP8X4),
                scales=w_scales[:],
                in_=w_grouped[:].rearrange("p c d t -> p (c d t)"),
            )

        def graph_blocks():
            nc.vector.tensor_scalar_add(out=minus_one[:, 0:1], in0=mask_first[:], scalar1=-1.0)
            nc.vector.tensor_scalar_add(out=minus_one[:, 1:TILES], in0=mask_rest[:], scalar1=-1.0)
            nc.vector.tensor_reduce(out=block_rows[:], in_=ident_blocks, axis=mybir.AxisListType.X, op=ADD)
            for r in range(TILES):
                nc.vector.tensor_scalar_mul(
                    out=masked_blocks[:, r, :], in0=block_rows[:], scalar1=minus_one[:, r : r + 1]
                )

        def correction_sums():
            count_ps = ps_pair.tile([P, GRAPHS], F32, name="count_ps", tag="pair")
            nc.tensor.matmul(
                out=count_ps[:], lhsT=ones[:], rhs=masked_blocks[:].rearrange("p r b -> p (r b)"), start=True, stop=True
            )
            return count_ps

        def correction_constants(count_ps):
            nc.scalar.activation(out=relu_mb2[:], in_=mb2_col[:], func=RELU)
            nc.scalar.activation(
                out=excess[:], in_=count_ps[:], func=mybir.ActivationFunctionType.Copy, scale=relu_mb2[:]
            )
            nc.scalar.copy(out=correction[:], in_=excess[:].unsqueeze(2).to_broadcast([P, GRAPHS, NODES]))

        groups = TILES * GROUPS

        def own_rotations(n):
            return ROTS if n < groups - 1 else ROTS // 2

        for n in range(groups):
            r, group = divmod(n, GROUPS)
            if n == 3:
                correction_constants(count_ps)
            new_h(n)
            if n >= 4 and n % 2 == 0:
                finish_msgs(n - 4)
                finish_msgs(n - 3)
            if n >= GROUPS + 6 and (n - 6) % GROUPS == 0:
                finish((n - 6) // GROUPS - 1)
            psum_sum(n, 0, 0)
            psum_sum(n, 0, 1)
            psum_sum(n, 0, 2)
            psum_sum(n, 0, 3)
            for ql in range(0, ROTS, OWN_ROTS):
                if ql < own_rotations(n):
                    own_sum(n, ql)
                else:
                    for q in range(OWN_ROTS):
                        psum_sum(n, 1, ql + q)
            if n >= 1:
                vector_relu(n - 1, 0, VECTOR_RELUS)
                quantise(n - 1, 0)
                quantise(n - 1, 1)
            if 4 <= n < groups - 2:
                sum_msgs(n - 4)
            if n == 0:
                for q in range(2 * ROTS, NODES):
                    turned_identity(q)
                late_constants()
                graph_blocks()
            if n == 1:
                quantise_weights()
            if n == 2:
                count_ps = correction_sums()
            if n >= GROUPS + 5 and (n - 5) % GROUPS == 0:
                add_up((n - 5) // GROUPS - 1)
            if n == 0:
                new_receivers(1, 1)
                for half in range(2):
                    add_receivers(1, 1, half)
            early = (n + 2) // GROUPS + 1
            if group >= 2 and early < TILES:
                if group == 2:
                    new_receivers(early, 1)
                add_receivers(early, 1, group - 2)
            if group < 2 and r + 1 < TILES:
                if group == 0:
                    new_receivers(r + 1, 0)
                add_receivers(r + 1, 0, group)
            if r + 1 < TILES:
                if group == 0:
                    mask_senders(r + 1, 1, BF16)
                if group == 1:
                    mask_senders(r + 1, 0, F32)
                    if r + 1 == TILES - 1:
                        mask_senders(r + 1, 1, F32)
                if group == 2:
                    turn_senders(r + 1)
                    turn_receivers(r + 1)
            if n >= 3 and n % 2:
                multiply(n - 3)
                multiply(n - 2)

        last = groups - 1
        halves = ((0, ROTS // 2), (ROTS // 2, ROTS))
        finish_msgs(last - 3)
        finish_msgs(last - 2)
        vector_relu(last, 0, own_rotations(last))
        for first, end in halves:
            quantise(last, 0, first, end)
            quantise(last, 1, first, end)
        add_up(TILES - 2)
        finish(TILES - 2)
        add_up(TILES - 1, 0, GROUPS - 2)
        multiply(last - 1)
        finish_msgs(last - 1)
        for first, end in halves:
            multiply(last, first, end)
            finish_msgs(last, first, end)
        add_up(TILES - 1, GROUPS - 2)
        finish(TILES - 1)
